import numpy as np
import ml_dtypes


def mxq(x, axis, fmt="e4m3"):
    dtype, down = {"e4m3": (ml_dtypes.float8_e4m3fn, 7), "e5m2": (ml_dtypes.float8_e5m2, 14)}[fmt]
    v = np.moveaxis(np.asarray(x, np.float32).astype(ml_dtypes.bfloat16).astype(np.float64), axis, -1)
    blocks = v.reshape(v.shape[:-1] + (-1, 32))
    amax = np.abs(blocks).max(-1, keepdims=True)
    byte = np.maximum(np.where(amax > 0, np.frexp(amax)[1] - 1 + 127, 0) - down, 1)
    scale = np.exp2(byte - 127.0)
    codes = (blocks / scale).astype(np.float32).astype(dtype).astype(np.float64)
    return np.moveaxis((codes * scale).reshape(v.shape), -1, axis)


WIDE = False


def mx_kscale(k):
    if not WIDE:
        return np.ones(k)
    levels = np.array([10, -10, 5, -5, 0])
    if k % 512:
        return np.exp2(np.random.permutation(np.resize(levels, k // 32))).repeat(32)
    a = np.empty((k // 512, 16))
    for p in range(k // 512):
        a[p, :8] = np.random.permutation(np.resize(levels, 8))
        for g in range(8):
            far = levels[np.abs(levels - a[p, g]) >= 10]
            a[p, g + 8] = far[np.random.randint(len(far))]
    return np.exp2(a.ravel()).repeat(32)


BF16 = ml_dtypes.bfloat16


def bf(x):
    return np.asarray(x, np.float32).astype(BF16)


def f64(x):
    return np.asarray(x).astype(np.float64)


N, C, E, T, H, CK = 3, 512, 512, 1024, 8, 64
EPS = 1e-5


def setup_inputs():
    s = mx_kscale(C)
    return {
        "h_attn": bf(np.random.standard_normal((N, T, C)) * 0.4 * s),
        "x": bf(np.random.standard_normal((N, E, T))),
        "masks": bf(np.random.uniform(0.2, 1.0, (N, 1, T))),
        "Wo": bf(np.random.standard_normal((E, C)) * 2.0 / np.sqrt(C) / s[None, :]),
        "bo": bf(np.random.standard_normal(E) * 0.5),
    }


def core(h_attn, x, masks, Wo, bo):
    o = (mxq(f64(h_attn), 2, "e4m3") @ mxq(f64(Wo), 1, "e4m3").T) + f64(bo)
    y = o.transpose(0, 2, 1) * f64(masks) + f64(x)
    mean = y.mean(-1, keepdims=True)
    var = np.square(y - mean).mean(-1, keepdims=True)
    return (y - mean) / np.sqrt(var + EPS)


def e4m3fn_bytes(y):
    return np.clip(np.asarray(y, np.float64), -448.0, 448.0).astype(np.float32).astype(ml_dtypes.float8_e4m3fn).view(np.uint8)


def reference(h_attn, x, masks, Wo, bo):
    out = core(h_attn, x, masks, Wo, bo)
    s = np.max(np.abs(out)) / 448.0
    return out, e4m3fn_bytes(out / s)

@@ -1,0 +1,288 @@
+from contextlib import ExitStack
+
+import concourse.mybir as mybir
+from concourse.masks import make_identity
+
+F32 = mybir.dt.float32
+BF16 = mybir.dt.bfloat16
+U32 = mybir.dt.uint32
+U8 = mybir.dt.uint8
+FP8X4 = mybir.dt.float8_e4m3fn_x4
+FP8 = mybir.dt.float8_e4m3fn
+ALU = mybir.AluOpType
+ACT = mybir.ActivationFunctionType
+AX = mybir.AxisListType
+
+NSEQ, T, C, E = 3, 1024, 512, 512
+P = 128
+NJ = E // P
+NU = NSEQ * NJ
+HALF = 512
+EPS = 1e-5
+FLOPS = 2 * NSEQ * T * C * E
+
+
+def tile_transformerencoderblock_pa_kernel(tc, h_attn, x, masks, Wo, bo, out_0, out_1):
+    nc = tc.nc
+    with ExitStack() as ctx:
+        keep = ctx.enter_context(tc.tile_pool(name="keep", bufs=1))
+        work = ctx.enter_context(tc.tile_pool(name="work", bufs=3))
+        upool = ctx.enter_context(tc.tile_pool(name="upool", bufs=5))
+        ps_t = ctx.enter_context(tc.psum_pool(name="ps_t", bufs=4))
+        ps_a = ctx.enter_context(tc.psum_pool(name="ps_a", bufs=4))
+
+        mrow = [keep.tile([P, T], BF16, name="mrow%d" % n) for n in range(NSEQ)]
+        eps_t = keep.tile([P, 1], F32, name="eps_t")
+        zero_t = keep.tile([P, 1], F32, name="zero_t")
+        nc.vector.memset(eps_t[:], EPS)
+        nc.vector.memset(mrow[0][:], 0.0)
+        nc.vector.memset(zero_t[:], 0.0)
+        nc.vector.memset(mrow[1][:], 0.0)
+        nc.vector.memset(mrow[2][:], 0.0)
+        warm = keep.tile([P, 1], F32, name="warm")
+        nc.scalar.activation(out=warm[:], in_=eps_t[:], func=ACT.Abs_reciprocal_sqrt)
+        ident = keep.tile([P, P], F32, name="ident")
+        make_identity(nc, ident[:])
+        ones = keep.tile([P, P], BF16, name="ones")
+        nc.gpsimd.memset(ones[:], 1.0)
+
+        wraw = [keep.tile([P, 2, C], BF16, name="wraw%d" % b) for b in range(2)]
+        wview = Wo.rearrange("(p j) c -> p j c", j=NJ)
+        hraw = {}
+        xs = {}
+        bo_bf = keep.tile([P, NJ], BF16, name="bo_bf")
+
+        def load_w(b):
+            nc.sync.dma_start(out=wraw[b][:], in_=wview[:, 2 * b : 2 * b + 2, :])
+
+        def load_h(n, c):
+            hraw[(n, c)] = keep.tile([P, 2, C], BF16, name="h%d_%d" % (n, c))
+            nc.sync.dma_start(
+                out=hraw[(n, c)][:],
+                in_=h_attn[n, c * 256 : (c + 1) * 256, :].rearrange("(i p) c -> p i c", p=P),
+            )
+
+        def load_x(n, j):
+            xs[(n, j)] = keep.tile([P, T], BF16, name="x%d_%d" % (n, j))
+            nc.sync.dma_start(out=xs[(n, j)][:], in_=x[n].rearrange("(p j) t -> p j t", j=NJ)[:, j, :])
+
+        def load_mask(n):
+            nc.sync.dma_start(out=mrow[n][0:1, :], in_=masks[n])
+
+        load_w(0)
+        load_h(0, 0)
+        load_mask(0)
+        nc.sync.dma_start(out=bo_bf[:], in_=bo.rearrange("(p j) -> p j", j=NJ))
+        load_h(0, 1)
+        load_w(1)
+        load_h(0, 2)
+        load_h(0, 3)
+        for j in range(NJ):
+            load_x(0, j)
+        for n in range(1, NSEQ):
+            load_mask(n)
+            for c in range(4):
+                load_h(n, c)
+            for j in range(NJ):
+                load_x(n, j)
+
+        mask_bc = keep.tile([P, NSEQ * T], F32, name="mask_bc")
+        bo32 = keep.tile([P, NJ], F32, name="bo32")
+        wg = keep.tile([P, 4 * E], BF16, name="wg", align_bytes=64)
+        wc = keep.tile([P, E], U32, name="wc", align_bytes=64)
+        wsc = keep.tile([P, E], U8, name="wsc", align_bytes=64)
+        hg = {}
+        hc = {}
+        hs = {}
+        tps = {}
+
+        def spread_mask(n, half, pool, tag, copy):
+            pm = pool.tile([P, HALF], F32, tag=tag, name="pm%d_%d" % (n, half))
+            nc.tensor.matmul(
+                out=pm[:], lhsT=ones[:], rhs=mrow[n][:, half * HALF : (half + 1) * HALF], start=True, stop=True
+            )
+            copy(out=mask_bc[:, n * T + half * HALF : n * T + (half + 1) * HALF], in_=pm[:])
+
+        def transposes(key, raw):
+            words = raw[:].bitcast(F32)
+            tp = ps_t.tile([P, 2, 2, P], F32, tag="tp", name="tp_%s" % key)
+            for i in range(2):
+                for u in range(2):
+                    nc.tensor.transpose(tp[:, i, u, :], words[:, i, u:256:2], ident[:])
+            tps[key] = tp
+
+        def copy_out(key, copy, dst, part):
+            copy(
+                out=dst[:].bitcast(F32)[:, part * 512 : (part + 1) * 512].rearrange("p (i t u) -> p i t u", i=2, u=2),
+                in_=tps[key][:].rearrange("p i u t -> p i t u"),
+            )
+
+        def new_hg(n, half):
+            hg[(n, half)] = work.tile([P, 4 * HALF], BF16, tag="hg", name="hg%d_%d" % (n, half), align_bytes=64)
+
+        def quantise_w(b):
+            nc.vector.quantize_mx(
+                out=wc[:, b * 256 : (b + 1) * 256].bitcast(FP8X4),
+                scales=wsc[:, b * 256 : (b + 1) * 256],
+                in_=wg[:, b * 1024 : (b + 1) * 1024],
+            )
+
+        def quantise(n, half):
+            hc[(n, half)] = keep.tile([P, HALF], U32, name="hc%d_%d" % (n, half), align_bytes=64)
+            hs[(n, half)] = keep.tile([P, HALF], U8, name="hs%d_%d" % (n, half), align_bytes=64)
+            nc.vector.quantize_mx(
+                out=hc[(n, half)][:].bitcast(FP8X4), scales=hs[(n, half)][:], in_=hg[(n, half)][:]
+            )
+
+        sums = keep.tile([P, NU], F32, name="sums")
+        negmean = keep.tile([P, NU], F32, name="negmean")
+        ssq = keep.tile([P, NU], F32, name="ssq")
+        rstd = keep.tile([P, NU], F32, name="rstd")
+        nbias = keep.tile([P, NU], F32, name="nbias")
+        amx = keep.tile([P, NU + 1], F32, name="amx")
+        us = {}
+        ys = {}
+        o0 = {}
+
+        def project(i, half):
+            n, j = divmod(i, NJ)
+            if half == 0:
+                us[i] = upool.tile([P, T], F32, tag="u", name="u%d" % i)
+            acc = ps_a.tile([P, HALF], F32, tag="acc", name="acc%d_%d" % (i, half))
+            nc.tensor.matmul_mx(
+                out=acc[:],
+                lhsT=wc[:, j * P : (j + 1) * P].bitcast(FP8X4),
+                lhsT_scale=wsc[:, j * P : (j + 1) * P],
+                rhs=hc[(n, half)][:].bitcast(FP8X4),
+                rhs_scale=hs[(n, half)][:],
+                start=True,
+                stop=True,
+            )
+            nc.vector.scalar_tensor_tensor(
+                out=us[i][:, half * HALF : (half + 1) * HALF],
+                in0=acc[:],
+                scalar=bo32[:, j : j + 1],
+                in1=mask_bc[:, n * T + half * HALF : n * T + (half + 1) * HALF],
+                op0=ALU.add,
+                op1=ALU.mult,
+            )
+
+        def residual(i):
+            n, j = divmod(i, NJ)
+            ys[i] = work.tile([P, T], F32, tag="y", name="y%d" % i)
+            nc.vector.scalar_tensor_tensor(
+                out=ys[i][:],
+                in0=us[i][:],
+                scalar=1.0,
+                in1=xs[(n, j)][:],
+                op0=ALU.mult,
+                op1=ALU.add,
+                accum_out=sums[:, i : i + 1],
+            )
+
+        def normalise(i, pieces):
+            n, j = divmod(i, NJ)
+            col = slice(i, i + 1)
+            nc.scalar.activation(out=negmean[:, col], in_=sums[:, col], func=ACT.Copy, scale=-1.0 / T)
+            sq = work.tile([P, T], BF16, tag="sq", name="sq%d" % i)
+            nc.scalar.activation(
+                out=sq[:], in_=ys[i][:], func=ACT.Square, bias=negmean[:, col], scale=1.0, accum_out=ssq[:, col]
+            )
+            nc.scalar.activation(
+                out=rstd[:, col], in_=ssq[:, col], func=ACT.Abs_reciprocal_sqrt, bias=eps_t[:, 0:1], scale=1.0 / T
+            )
+            nc.scalar.activation(out=nbias[:, col], in_=negmean[:, col], func=ACT.Copy, scale=rstd[:, col])
+            o0[i] = keep.tile([P, T], F32, name="o0_%d" % i)
+            w = T // pieces
+            for k in range(pieces):
+                nc.scalar.activation(
+                    out=o0[i][:, k * w : (k + 1) * w],
+                    in_=ys[i][:, k * w : (k + 1) * w],
+                    func=ACT.Identity,
+                    bias=nbias[:, col],
+                    scale=rstd[:, col],
+                )
+            nc.sync.dma_start(out=out_0[n].rearrange("(p j) t -> p j t", j=NJ)[:, j, :], in_=o0[i][:])
+
+        def row_amax(i, c0, c1, col):
+            nc.vector.tensor_reduce(
+                out=amx[:, col : col + 1], in_=o0[i][:, c0:c1], axis=AX.X, op=ALU.max, apply_absolute_value=True
+            )
+
+        vcopy = nc.vector.tensor_copy
+        scopy = nc.scalar.copy
+
+        transposes("w0", wraw[0])
+        copy_out("w0", vcopy, wg, 0)
+        transposes("h0_0", hraw[(0, 0)])
+        new_hg(0, 0)
+        copy_out("h0_0", scopy, hg[(0, 0)], 0)
+        quantise_w(0)
+        spread_mask(0, 0, ps_a, "acc", vcopy)
+        nc.vector.tensor_copy(out=bo32[:], in_=bo_bf[:])
+        transposes("h0_1", hraw[(0, 1)])
+        copy_out("h0_1", vcopy, hg[(0, 0)], 1)
+        spread_mask(0, 1, ps_a, "acc", scopy)
+        transposes("w1", wraw[1])
+        copy_out("w1", scopy, wg, 1)
+        quantise(0, 0)
+        new_hg(0, 1)
+        transposes("h0_2", hraw[(0, 2)])
+        copy_out("h0_2", scopy, hg[(0, 1)], 0)
+        transposes("h0_3", hraw[(0, 3)])
+        copy_out("h0_3", scopy, hg[(0, 1)], 1)
+        project(0, 0)
+        project(1, 0)
+        quantise_w(1)
+        project(2, 0)
+        project(3, 0)
+        quantise(0, 1)
+
+        for i in range(NU):
+            n, j = divmod(i, NJ)
+            if n > 0:
+                project(i, 0)
+            project(i, 1)
+            residual(i)
+            if n + 1 < NSEQ:
+                if j < 2:
+                    new_hg(n + 1, j)
+                    for cc in range(2):
+                        key = "h%d_%d" % (n + 1, 2 * j + cc)
+                        transposes(key, hraw[(n + 1, 2 * j + cc)])
+                        copy_out(key, scopy, hg[(n + 1, j)], cc)
+                    spread_mask(n + 1, j, ps_t, "tp", scopy)
+                else:
+                    quantise(n + 1, j - 2)
+            normalise(i, 2 if i == NU - 1 else 1)
+            if i >= 2:
+                row_amax(i - 2, 0, T, i - 2)
+        row_amax(NU - 2, 0, T, NU - 2)
+        row_amax(NU - 1, 0, HALF, NU - 1)
+        row_amax(NU - 1, HALF, T, NU)
+
+        am1 = keep.tile([P, 1], F32, name="am1")
+        nc.vector.tensor_reduce(out=am1[:], in_=amx[:], axis=AX.X, op=ALU.max)
+        pt = ps_t.tile([P, P], F32, tag="tp", name="pt")
+        nc.tensor.transpose(pt[:], am1[:, 0:1].to_broadcast([P, P]), ident[:])
+        am2 = keep.tile([P, 1], F32, name="am2")
+        nc.vector.tensor_reduce(out=am2[:], in_=pt[:], axis=AX.X, op=ALU.max)
+        rc = keep.tile([P, 1], F32, name="rc")
+        nc.vector.reciprocal(out=rc[:], in_=am2[:])
+        r448 = keep.tile([P, 1], F32, name="r448")
+        nc.vector.tensor_scalar(out=r448[:], in0=rc[:], scalar1=448.0, scalar2=None, op0=ALU.mult)
+
+        for i in range(NU):
+            n, j = divmod(i, NJ)
+            f8 = keep.tile([P, T], FP8, name="f8_%d" % i)
+            if i % 3 == 2:
+                nc.scalar.activation(
+                    out=f8[:], in_=o0[i][:], func=ACT.Identity, scale=r448[:, 0:1], bias=zero_t[:, 0:1], saturate=False
+                )
+            else:
+                nc.vector.tensor_scalar(
+                    out=f8[:], in0=o0[i][:], scalar1=r448[:, 0:1], scalar2=None, op0=ALU.mult, saturate=False
+                )
+            nc.sync.dma_start(
+                out=out_1[n].rearrange("(p j) t -> p j t", j=NJ)[:, j, :], in_=f8[:].bitcast(U8)
+            )

@@ -12,6 +12,7 @@ FP8 = mybir.dt.float8_e4m3fn
 ALU = mybir.AluOpType
 ACT = mybir.ActivationFunctionType
 AX = mybir.AxisListType
+ENG = mybir.EngineType
 
 NSEQ, T, C, E = 3, 1024, 512, 512
 P = 128
@@ -28,66 +29,25 @@ def tile_transformerencoderblock_pa_kernel(tc, h_attn, x, masks, Wo, bo, out_0, 
         keep = ctx.enter_context(tc.tile_pool(name="keep", bufs=1))
         work = ctx.enter_context(tc.tile_pool(name="work", bufs=3))
         upool = ctx.enter_context(tc.tile_pool(name="upool", bufs=5))
+        ypool = ctx.enter_context(tc.tile_pool(name="ypool", bufs=3))
         ps_t = ctx.enter_context(tc.psum_pool(name="ps_t", bufs=4))
         ps_a = ctx.enter_context(tc.psum_pool(name="ps_a", bufs=4))
+        ctx.enter_context(tc.manual_schedule())
 
         mrow = [keep.tile([P, T], BF16, name="mrow%d" % n) for n in range(NSEQ)]
         eps_t = keep.tile([P, 1], F32, name="eps_t")
         zero_t = keep.tile([P, 1], F32, name="zero_t")
-        nc.vector.memset(eps_t[:], EPS)
-        nc.vector.memset(mrow[0][:], 0.0)
-        nc.vector.memset(zero_t[:], 0.0)
-        nc.vector.memset(mrow[1][:], 0.0)
-        nc.vector.memset(mrow[2][:], 0.0)
         warm = keep.tile([P, 1], F32, name="warm")
-        nc.scalar.activation(out=warm[:], in_=eps_t[:], func=ACT.Abs_reciprocal_sqrt)
         ident = keep.tile([P, P], F32, name="ident")
-        make_identity(nc, ident[:])
         ones = keep.tile([P, P], BF16, name="ones")
-        nc.gpsimd.memset(ones[:], 1.0)
-
         wraw = [keep.tile([P, 2, C], BF16, name="wraw%d" % b) for b in range(2)]
         wview = Wo.rearrange("(p j) c -> p j c", j=NJ)
-        hraw = {}
+        raw = {}
         xs = {}
         bo_bf = keep.tile([P, NJ], BF16, name="bo_bf")
-
-        def load_w(b):
-            nc.sync.dma_start(out=wraw[b][:], in_=wview[:, 2 * b : 2 * b + 2, :])
-
-        def load_h(n, c):
-            hraw[(n, c)] = keep.tile([P, 2, C], BF16, name="h%d_%d" % (n, c))
-            nc.sync.dma_start(
-                out=hraw[(n, c)][:],
-                in_=h_attn[n, c * 256 : (c + 1) * 256, :].rearrange("(i p) c -> p i c", p=P),
-            )
-
-        def load_x(n, j):
-            xs[(n, j)] = keep.tile([P, T], BF16, name="x%d_%d" % (n, j))
-            nc.sync.dma_start(out=xs[(n, j)][:], in_=x[n].rearrange("(p j) t -> p j t", j=NJ)[:, j, :])
-
-        def load_mask(n):
-            nc.sync.dma_start(out=mrow[n][0:1, :], in_=masks[n])
-
-        load_w(0)
-        load_h(0, 0)
-        load_mask(0)
-        nc.sync.dma_start(out=bo_bf[:], in_=bo.rearrange("(p j) -> p j", j=NJ))
-        load_h(0, 1)
-        load_w(1)
-        load_h(0, 2)
-        load_h(0, 3)
-        for j in range(NJ):
-            load_x(0, j)
-        for n in range(1, NSEQ):
-            load_mask(n)
-            for c in range(4):
-                load_h(n, c)
-            for j in range(NJ):
-                load_x(n, j)
-
         mask_bc = keep.tile([P, NSEQ * T], F32, name="mask_bc")
         bo32 = keep.tile([P, NJ], F32, name="bo32")
+        mask_dma = {}
         wg = keep.tile([P, 4 * E], BF16, name="wg", align_bytes=64)
         wc = keep.tile([P, E], U32, name="wc", align_bytes=64)
         wsc = keep.tile([P, E], U8, name="wsc", align_bytes=64)
@@ -95,30 +55,78 @@ def tile_transformerencoderblock_pa_kernel(tc, h_attn, x, masks, Wo, bo, out_0, 
         hc = {}
         hs = {}
         tps = {}
+        pms = {}
+        accs = {}
+        sums = keep.tile([P, NU, 4], F32, name="sums")
+        junk3 = keep.tile([P, NU, 4], F32, name="junk3")
+        negmean = keep.tile([P, NU], F32, name="negmean")
+        ssq = keep.tile([P, NU], F32, name="ssq")
+        rstd = keep.tile([P, NU], F32, name="rstd")
+        nbias = keep.tile([P, NU], F32, name="nbias")
+        amx = keep.tile([P, NU + 1], F32, name="amx")
+        us = {}
+        ys = {}
+        o0 = {}
+        copies = {"V": nc.vector.tensor_copy, "S": nc.scalar.copy}
 
-        def spread_mask(n, half, pool, tag, copy):
-            pm = pool.tile([P, HALF], F32, tag=tag, name="pm%d_%d" % (n, half))
-            nc.tensor.matmul(
-                out=pm[:], lhsT=ones[:], rhs=mrow[n][:, half * HALF : (half + 1) * HALF], start=True, stop=True
+        def load_w(b):
+            raw["w%d" % b] = wraw[b]
+            nc.sync.dma_start(out=wraw[b][:], in_=wview[:, 2 * b : 2 * b + 2, :])
+
+        def load_h(n, c):
+            raw["h%d_%d" % (n, c)] = keep.tile([P, 2, C], BF16, name="h%d_%d" % (n, c))
+            nc.sync.dma_start(
+                out=raw["h%d_%d" % (n, c)][:],
+                in_=h_attn[n, c * 256 : (c + 1) * 256, :].rearrange("(i p) c -> p i c", p=P),
             )
-            copy(out=mask_bc[:, n * T + half * HALF : n * T + (half + 1) * HALF], in_=pm[:])
 
-        def transposes(key, raw):
-            words = raw[:].bitcast(F32)
+        def load_x(i):
+            n, j = divmod(i, NJ)
+            xs[i] = keep.tile([P, T], BF16, name="x%d" % i)
+            nc.sync.dma_start(out=xs[i][:], in_=x[n].rearrange("(p j) t -> p j t", j=NJ)[:, j, :])
+
+        def load_mask(n):
+            nc.sync.dma_start(out=mrow[n][0:1, :], in_=masks[n])
+
+        def load_mask_spread(n):
+            mask_dma[n] = keep.tile([P, T], BF16, name="mask_dma%d" % n)
+            nc.sync.dma_start(out=mask_dma[n][:], in_=masks[n, 0].partition_broadcast(P))
+
+        def mask_of(n, half):
+            if n in mask_dma:
+                return mask_dma[n][:, half * HALF : (half + 1) * HALF]
+            return mask_bc[:, n * T + half * HALF : n * T + (half + 1) * HALF]
+
+        def mask_mm(n, half, where):
+            pool = ps_a if where == "acc" else ps_t
+            pms[(n, half)] = pool.tile([P, HALF], F32, tag=where, name="pm%d_%d" % (n, half))
+            nc.tensor.matmul(
+                out=pms[(n, half)][:], lhsT=ones[:], rhs=mrow[n][:, half * HALF : (half + 1) * HALF],
+                start=True, stop=True,
+            )
+
+        def mask_copy(n, half, eng):
+            copies[eng](out=mask_bc[:, n * T + half * HALF : n * T + (half + 1) * HALF], in_=pms[(n, half)][:])
+
+        def transposes(key):
+            words = raw[key][:].bitcast(F32)
             tp = ps_t.tile([P, 2, 2, P], F32, tag="tp", name="tp_%s" % key)
             for i in range(2):
                 for u in range(2):
                     nc.tensor.transpose(tp[:, i, u, :], words[:, i, u:256:2], ident[:])
             tps[key] = tp
 
-        def copy_out(key, copy, dst, part):
-            copy(
+        def copy_out(key, eng, dst, part):
+            copies[eng](
                 out=dst[:].bitcast(F32)[:, part * 512 : (part + 1) * 512].rearrange("p (i t u) -> p i t u", i=2, u=2),
                 in_=tps[key][:].rearrange("p i u t -> p i t u"),
             )
 
-        def new_hg(n, half):
-            hg[(n, half)] = work.tile([P, 4 * HALF], BF16, tag="hg", name="hg%d_%d" % (n, half), align_bytes=64)
+        def copy_out_h(n, c, eng):
+            half, cc = divmod(c, 2)
+            if cc == 0:
+                hg[(n, half)] = work.tile([P, 4 * HALF], BF16, tag="hg", name="hg%d_%d" % (n, half), align_bytes=64)
+            copy_out("h%d_%d" % (n, c), eng, hg[(n, half)], cc)
 
         def quantise_w(b):
             nc.vector.quantize_mx(
@@ -134,23 +142,21 @@ def tile_transformerencoderblock_pa_kernel(tc, h_attn, x, masks, Wo, bo, out_0, 
                 out=hc[(n, half)][:].bitcast(FP8X4), scales=hs[(n, half)][:], in_=hg[(n, half)][:]
             )
 
-        sums = keep.tile([P, NU], F32, name="sums")
-        negmean = keep.tile([P, NU], F32, name="negmean")
-        ssq = keep.tile([P, NU], F32, name="ssq")
-        rstd = keep.tile([P, NU], F32, name="rstd")
-        nbias = keep.tile([P, NU], F32, name="nbias")
-        amx = keep.tile([P, NU + 1], F32, name="amx")
-        us = {}
-        ys = {}
-        o0 = {}
+        def sum_x(i, eng):
+            jx = work.tile([P, T], BF16, tag="jx" + eng, name="jx%d" % i)
+            if eng == "V":
+                nc.vector.tensor_scalar(
+                    out=jx[:], in0=xs[i][:], scalar1=1.0, scalar2=None, op0=ALU.mult, op1=ALU.add,
+                    accum_out=sums[:, i, 2:3],
+                )
+            else:
+                nc.scalar.activation(out=jx[:], in_=xs[i][:], func=ACT.Copy, accum_out=sums[:, i, 2:3])
 
         def project(i, half):
             n, j = divmod(i, NJ)
-            if half == 0:
-                us[i] = upool.tile([P, T], F32, tag="u", name="u%d" % i)
-            acc = ps_a.tile([P, HALF], F32, tag="acc", name="acc%d_%d" % (i, half))
+            accs[(i, half)] = ps_a.tile([P, HALF], F32, tag="acc", name="acc%d_%d" % (i, half))
             nc.tensor.matmul_mx(
-                out=acc[:],
+                out=accs[(i, half)][:],
                 lhsT=wc[:, j * P : (j + 1) * P].bitcast(FP8X4),
                 lhsT_scale=wsc[:, j * P : (j + 1) * P],
                 rhs=hc[(n, half)][:].bitcast(FP8X4),
@@ -158,32 +164,45 @@ def tile_transformerencoderblock_pa_kernel(tc, h_attn, x, masks, Wo, bo, out_0, 
                 start=True,
                 stop=True,
             )
+
+        def bias_mask(i, half, with_sum):
+            n, j = divmod(i, NJ)
+            if i not in us:
+                us[i] = upool.tile([P, T], F32, tag="u", name="u%d" % i)
             nc.vector.scalar_tensor_tensor(
                 out=us[i][:, half * HALF : (half + 1) * HALF],
-                in0=acc[:],
+                in0=accs[(i, half)][:],
                 scalar=bo32[:, j : j + 1],
-                in1=mask_bc[:, n * T + half * HALF : n * T + (half + 1) * HALF],
+                in1=mask_of(n, half),
                 op0=ALU.add,
                 op1=ALU.mult,
+                accum_out=(sums[:, i, half : half + 1] if with_sum else None),
             )
 
-        def residual(i):
-            n, j = divmod(i, NJ)
-            ys[i] = work.tile([P, T], F32, tag="y", name="y%d" % i)
+        def new_y(i):
+            if i not in ys:
+                ys[i] = ypool.tile([P, T], F32, tag="y", name="y%d" % i)
+
+        def residual_g(i, half):
+            new_y(i)
+            cols = slice(half * HALF, (half + 1) * HALF)
+            nc.gpsimd.tensor_tensor(out=ys[i][:, cols], in0=us[i][:, cols], in1=xs[i][:, cols], op=ALU.add)
+
+        def residual_v(i):
+            new_y(i)
             nc.vector.scalar_tensor_tensor(
-                out=ys[i][:],
-                in0=us[i][:],
-                scalar=1.0,
-                in1=xs[(n, j)][:],
-                op0=ALU.mult,
-                op1=ALU.add,
-                accum_out=sums[:, i : i + 1],
+                out=ys[i][:], in0=us[i][:], scalar=1.0, in1=xs[i][:], op0=ALU.mult, op1=ALU.add,
+                accum_out=sums[:, i, 0:1],
             )
 
-        def normalise(i, pieces):
-            n, j = divmod(i, NJ)
+        def stats(i, parts):
             col = slice(i, i + 1)
-            nc.scalar.activation(out=negmean[:, col], in_=sums[:, col], func=ACT.Copy, scale=-1.0 / T)
+            if parts == 3:
+                nc.scalar.activation(
+                    out=junk3[:, i, 0:3], in_=sums[:, i, 0:3], func=ACT.Copy, scale=-1.0 / T, accum_out=negmean[:, col]
+                )
+            else:
+                nc.scalar.activation(out=negmean[:, col], in_=sums[:, i, 0:1], func=ACT.Copy, scale=-1.0 / T)
             sq = work.tile([P, T], BF16, tag="sq", name="sq%d" % i)
             nc.scalar.activation(
                 out=sq[:], in_=ys[i][:], func=ACT.Square, bias=negmean[:, col], scale=1.0, accum_out=ssq[:, col]
@@ -192,16 +211,47 @@ def tile_transformerencoderblock_pa_kernel(tc, h_attn, x, masks, Wo, bo, out_0, 
                 out=rstd[:, col], in_=ssq[:, col], func=ACT.Abs_reciprocal_sqrt, bias=eps_t[:, 0:1], scale=1.0 / T
             )
             nc.scalar.activation(out=nbias[:, col], in_=negmean[:, col], func=ACT.Copy, scale=rstd[:, col])
-            o0[i] = keep.tile([P, T], F32, name="o0_%d" % i)
+
+        def neg_mean(i):
+            nc.gpsimd.tensor_scalar(
+                out=negmean[:, i : i + 1], in0=sums[:, i, 0:1], scalar1=-1.0 / T, scalar2=0.0, op0=ALU.mult, op1=ALU.add
+            )
+
+        def squares(i):
+            col = slice(i, i + 1)
+            sq = work.tile([P, T], BF16, tag="sq", name="sq%d" % i)
+            nc.scalar.activation(
+                out=sq[:], in_=ys[i][:], func=ACT.Square, bias=negmean[:, col], scale=1.0, accum_out=ssq[:, col]
+            )
+
+        def inv_std(i):
+            col = slice(i, i + 1)
+            nc.scalar.activation(
+                out=rstd[:, col], in_=ssq[:, col], func=ACT.Abs_reciprocal_sqrt, bias=eps_t[:, 0:1], scale=1.0 / T
+            )
+
+        def neg_bias(i):
+            col = slice(i, i + 1)
+            nc.gpsimd.tensor_tensor(out=nbias[:, col], in0=negmean[:, col], in1=rstd[:, col], op=ALU.mult)
+
+        def normalise(i, k, pieces, eng):
+            col = slice(i, i + 1)
+            if i not in o0:
+                o0[i] = keep.tile([P, T], F32, name="o0_%d" % i)
             w = T // pieces
-            for k in range(pieces):
+            cols = slice(k * w, (k + 1) * w)
+            if eng == "S":
                 nc.scalar.activation(
-                    out=o0[i][:, k * w : (k + 1) * w],
-                    in_=ys[i][:, k * w : (k + 1) * w],
-                    func=ACT.Identity,
-                    bias=nbias[:, col],
-                    scale=rstd[:, col],
+                    out=o0[i][:, cols], in_=ys[i][:, cols], func=ACT.Identity, bias=nbias[:, col], scale=rstd[:, col]
                 )
+            else:
+                nc.gpsimd.tensor_scalar(
+                    out=o0[i][:, cols], in0=ys[i][:, cols], scalar1=rstd[:, col], scalar2=nbias[:, col],
+                    op0=ALU.mult, op1=ALU.add,
+                )
+
+        def store_0(i):
+            n, j = divmod(i, NJ)
             nc.sync.dma_start(out=out_0[n].rearrange("(p j) t -> p j t", j=NJ)[:, j, :], in_=o0[i][:])
 
         def row_amax(i, c0, c1, col):
@@ -209,73 +259,23 @@ def tile_transformerencoderblock_pa_kernel(tc, h_attn, x, masks, Wo, bo, out_0, 
                 out=amx[:, col : col + 1], in_=o0[i][:, c0:c1], axis=AX.X, op=ALU.max, apply_absolute_value=True
             )
 
-        vcopy = nc.vector.tensor_copy
-        scopy = nc.scalar.copy
-
-        transposes("w0", wraw[0])
-        copy_out("w0", vcopy, wg, 0)
-        transposes("h0_0", hraw[(0, 0)])
-        new_hg(0, 0)
-        copy_out("h0_0", scopy, hg[(0, 0)], 0)
-        quantise_w(0)
-        spread_mask(0, 0, ps_a, "acc", vcopy)
-        nc.vector.tensor_copy(out=bo32[:], in_=bo_bf[:])
-        transposes("h0_1", hraw[(0, 1)])
-        copy_out("h0_1", vcopy, hg[(0, 0)], 1)
-        spread_mask(0, 1, ps_a, "acc", scopy)
-        transposes("w1", wraw[1])
-        copy_out("w1", scopy, wg, 1)
-        quantise(0, 0)
-        new_hg(0, 1)
-        transposes("h0_2", hraw[(0, 2)])
-        copy_out("h0_2", scopy, hg[(0, 1)], 0)
-        transposes("h0_3", hraw[(0, 3)])
-        copy_out("h0_3", scopy, hg[(0, 1)], 1)
-        project(0, 0)
-        project(1, 0)
-        quantise_w(1)
-        project(2, 0)
-        project(3, 0)
-        quantise(0, 1)
-
-        for i in range(NU):
-            n, j = divmod(i, NJ)
-            if n > 0:
-                project(i, 0)
-            project(i, 1)
-            residual(i)
-            if n + 1 < NSEQ:
-                if j < 2:
-                    new_hg(n + 1, j)
-                    for cc in range(2):
-                        key = "h%d_%d" % (n + 1, 2 * j + cc)
-                        transposes(key, hraw[(n + 1, 2 * j + cc)])
-                        copy_out(key, scopy, hg[(n + 1, j)], cc)
-                    spread_mask(n + 1, j, ps_t, "tp", scopy)
-                else:
-                    quantise(n + 1, j - 2)
-            normalise(i, 2 if i == NU - 1 else 1)
-            if i >= 2:
-                row_amax(i - 2, 0, T, i - 2)
-        row_amax(NU - 2, 0, T, NU - 2)
-        row_amax(NU - 1, 0, HALF, NU - 1)
-        row_amax(NU - 1, HALF, T, NU)
-
-        am1 = keep.tile([P, 1], F32, name="am1")
-        nc.vector.tensor_reduce(out=am1[:], in_=amx[:], axis=AX.X, op=ALU.max)
-        pt = ps_t.tile([P, P], F32, tag="tp", name="pt")
-        nc.tensor.transpose(pt[:], am1[:, 0:1].to_broadcast([P, P]), ident[:])
-        am2 = keep.tile([P, 1], F32, name="am2")
-        nc.vector.tensor_reduce(out=am2[:], in_=pt[:], axis=AX.X, op=ALU.max)
-        rc = keep.tile([P, 1], F32, name="rc")
-        nc.vector.reciprocal(out=rc[:], in_=am2[:])
         r448 = keep.tile([P, 1], F32, name="r448")
-        nc.vector.tensor_scalar(out=r448[:], in0=rc[:], scalar1=448.0, scalar2=None, op0=ALU.mult)
 
-        for i in range(NU):
+        def one_amax():
+            am1 = keep.tile([P, 1], F32, name="am1")
+            nc.vector.tensor_reduce(out=am1[:], in_=amx[:], axis=AX.X, op=ALU.max)
+            pt = ps_t.tile([P, P], F32, tag="tp", name="pt")
+            nc.tensor.transpose(pt[:], am1[:, 0:1].to_broadcast([P, P]), ident[:])
+            am2 = keep.tile([P, 1], F32, name="am2")
+            nc.vector.tensor_reduce(out=am2[:], in_=pt[:], axis=AX.X, op=ALU.max)
+            rc = keep.tile([P, 1], F32, name="rc")
+            nc.vector.reciprocal(out=rc[:], in_=am2[:])
+            nc.vector.tensor_scalar(out=r448[:], in0=rc[:], scalar1=448.0, scalar2=None, op0=ALU.mult)
+
+        def cast(i, eng):
             n, j = divmod(i, NJ)
             f8 = keep.tile([P, T], FP8, name="f8_%d" % i)
-            if i % 3 == 2:
+            if eng == "S":
                 nc.scalar.activation(
                     out=f8[:], in_=o0[i][:], func=ACT.Identity, scale=r448[:, 0:1], bias=zero_t[:, 0:1], saturate=False
                 )
@@ -286,3 +286,240 @@ def tile_transformerencoderblock_pa_kernel(tc, h_attn, x, masks, Wo, bo, out_0, 
             nc.sync.dma_start(
                 out=out_1[n].rearrange("(p j) t -> p j t", j=NJ)[:, j, :], in_=f8[:].bitcast(U8)
             )
+
+        nc.vector.memset(eps_t[:], EPS)
+        nc.vector.memset(mrow[0][:], 0.0)
+        nc.vector.memset(zero_t[:], 0.0)
+        nc.scalar.activation(out=warm[:], in_=eps_t[:], func=ACT.Abs_reciprocal_sqrt)
+        make_identity(nc, ident[:])
+        nc.gpsimd.memset(ones[:], 1.0)
+        load_w(0)
+        load_h(0, 0)
+        load_mask(0)
+        nc.sync.dma_start(out=bo_bf[:], in_=bo.rearrange("(p j) -> p j", j=NJ))
+        load_h(0, 1)
+        load_w(1)
+        load_h(0, 2)
+        load_h(0, 3)
+        load_x(0)
+        load_x(1)
+        load_x(2)
+        load_x(3)
+        load_h(1, 0)
+        load_h(1, 1)
+        load_h(1, 2)
+        load_h(1, 3)
+        load_mask_spread(1)
+        load_x(4)
+        load_x(5)
+        load_x(6)
+        load_x(7)
+        load_h(2, 0)
+        load_h(2, 1)
+        load_h(2, 2)
+        load_h(2, 3)
+        load_mask_spread(2)
+        load_x(8)
+        load_x(9)
+        load_x(10)
+        load_x(11)
+        transposes("w0")
+        copy_out("w0", "V", wg, 0)
+        transposes("h0_0")
+        copy_out_h(0, 0, "S")
+        transposes("h0_1")
+        copy_out_h(0, 1, "V")
+        quantise_w(0)
+        mask_mm(0, 0, "acc")
+        mask_copy(0, 0, "S")
+        nc.vector.tensor_copy(out=bo32[:], in_=bo_bf[:])
+        quantise(0, 0)
+        transposes("w1")
+        copy_out("w1", "S", wg, 1)
+        transposes("h0_2")
+        copy_out_h(0, 2, "S")
+        project(0, 0)
+        project(1, 0)
+        transposes("h0_3")
+        copy_out_h(0, 3, "S")
+        mask_mm(0, 1, "acc")
+        mask_copy(0, 1, "S")
+        bias_mask(0, 0, False)
+        quantise_w(1)
+        bias_mask(1, 0, False)
+        project(2, 0)
+        project(3, 0)
+        bias_mask(2, 0, False)
+        quantise(0, 1)
+        bias_mask(3, 0, False)
+        project(0, 1)
+        project(1, 1)
+        project(2, 1)
+        project(3, 1)
+        bias_mask(0, 1, False)
+        transposes("h1_0")
+        transposes("h1_1")
+        transposes("h1_2")
+        transposes("h1_3")
+        bias_mask(1, 1, False)
+        residual_v(0)
+        copy_out_h(1, 0, "S")
+        copy_out_h(1, 1, "S")
+        copy_out_h(1, 2, "S")
+        copy_out_h(1, 3, "S")
+        neg_mean(0)
+        squares(0)
+        inv_std(0)
+        neg_bias(0)
+        transposes("h2_0")
+        bias_mask(2, 1, False)
+        quantise(1, 0)
+        residual_v(1)
+        copy_out_h(2, 0, "S")
+        neg_mean(1)
+        normalise(0, 0, 1, "S")
+        store_0(0)
+        squares(1)
+        inv_std(1)
+        neg_bias(1)
+        transposes("h2_1")
+        bias_mask(3, 1, False)
+        quantise(1, 1)
+        residual_v(2)
+        copy_out_h(2, 1, "S")
+        neg_mean(2)
+        normalise(1, 0, 1, "S")
+        store_0(1)
+        squares(2)
+        inv_std(2)
+        neg_bias(2)
+        project(4, 0)
+        project(4, 1)
+        transposes("h2_2")
+        bias_mask(4, 0, False)
+        bias_mask(4, 1, False)
+        residual_v(3)
+        copy_out_h(2, 2, "S")
+        neg_mean(3)
+        normalise(2, 0, 1, "S")
+        store_0(2)
+        squares(3)
+        inv_std(3)
+        neg_bias(3)
+        row_amax(0, 0, T, 0)
+        project(5, 0)
+        project(5, 1)
+        transposes("h2_3")
+        bias_mask(5, 0, False)
+        bias_mask(5, 1, False)
+        residual_v(4)
+        copy_out_h(2, 3, "S")
+        neg_mean(4)
+        normalise(3, 0, 1, "S")
+        store_0(3)
+        squares(4)
+        inv_std(4)
+        neg_bias(4)
+        row_amax(1, 0, T, 1)
+        project(6, 0)
+        project(6, 1)
+        bias_mask(6, 0, False)
+        bias_mask(6, 1, False)
+        quantise(2, 0)
+        residual_v(5)
+        neg_mean(5)
+        normalise(4, 0, 1, "S")
+        store_0(4)
+        squares(5)
+        inv_std(5)
+        neg_bias(5)
+        row_amax(2, 0, T, 2)
+        project(7, 0)
+        project(7, 1)
+        bias_mask(7, 0, False)
+        bias_mask(7, 1, False)
+        quantise(2, 1)
+        residual_v(6)
+        neg_mean(6)
+        normalise(5, 0, 1, "S")
+        store_0(5)
+        squares(6)
+        inv_std(6)
+        neg_bias(6)
+        row_amax(3, 0, T, 3)
+        project(8, 0)
+        project(8, 1)
+        bias_mask(8, 0, False)
+        bias_mask(8, 1, False)
+        residual_v(7)
+        neg_mean(7)
+        normalise(6, 0, 1, "S")
+        store_0(6)
+        squares(7)
+        inv_std(7)
+        neg_bias(7)
+        row_amax(4, 0, T, 4)
+        project(9, 0)
+        project(9, 1)
+        bias_mask(9, 0, False)
+        bias_mask(9, 1, False)
+        residual_v(8)
+        neg_mean(8)
+        normalise(7, 0, 1, "S")
+        store_0(7)
+        squares(8)
+        inv_std(8)
+        neg_bias(8)
+        row_amax(5, 0, T, 5)
+        project(10, 0)
+        project(10, 1)
+        bias_mask(10, 0, False)
+        bias_mask(10, 1, False)
+        residual_v(9)
+        neg_mean(9)
+        normalise(8, 0, 1, "S")
+        store_0(8)
+        squares(9)
+        inv_std(9)
+        neg_bias(9)
+        row_amax(6, 0, T, 6)
+        project(11, 0)
+        project(11, 1)
+        bias_mask(11, 0, False)
+        bias_mask(11, 1, False)
+        residual_v(10)
+        neg_mean(10)
+        normalise(9, 0, 1, "S")
+        store_0(9)
+        squares(10)
+        inv_std(10)
+        neg_bias(10)
+        row_amax(7, 0, T, 7)
+        residual_v(11)
+        neg_mean(11)
+        normalise(10, 0, 1, "S")
+        store_0(10)
+        squares(11)
+        inv_std(11)
+        neg_bias(11)
+        normalise(11, 0, 2, "S")
+        normalise(11, 1, 2, "S")
+        store_0(11)
+        row_amax(8, 0, T, 8)
+        row_amax(9, 0, T, 9)
+        row_amax(10, 0, T, 10)
+        row_amax(11, 0, HALF, 11)
+        row_amax(11, HALF, T, NU)
+        one_amax()
+        cast(0, "V")
+        cast(1, "V")
+        cast(2, "S")
+        cast(3, "V")
+        cast(4, "V")
+        cast(5, "S")
+        cast(6, "V")
+        cast(7, "V")
+        cast(8, "S")
+        cast(9, "V")
+        cast(10, "V")
+        cast(11, "S")

@@ -29,7 +29,7 @@ def tile_transformerencoderblock_pa_kernel(tc, h_attn, x, masks, Wo, bo, out_0, 
         keep = ctx.enter_context(tc.tile_pool(name="keep", bufs=1))
         work = ctx.enter_context(tc.tile_pool(name="work", bufs=3))
         upool = ctx.enter_context(tc.tile_pool(name="upool", bufs=5))
-        ypool = ctx.enter_context(tc.tile_pool(name="ypool", bufs=3))
+        ypool = ctx.enter_context(tc.tile_pool(name="ypool", bufs=6))
         ps_t = ctx.enter_context(tc.psum_pool(name="ps_t", bufs=4))
         ps_a = ctx.enter_context(tc.psum_pool(name="ps_a", bufs=4))
         ctx.enter_context(tc.manual_schedule())
@@ -48,6 +48,7 @@ def tile_transformerencoderblock_pa_kernel(tc, h_attn, x, masks, Wo, bo, out_0, 
         mask_bc = keep.tile([P, NSEQ * T], F32, name="mask_bc")
         bo32 = keep.tile([P, NJ], F32, name="bo32")
         mask_dma = {}
+        wz = keep.tile([P, 256], F32, name="wz")
         wg = keep.tile([P, 4 * E], BF16, name="wg", align_bytes=64)
         wc = keep.tile([P, E], U32, name="wc", align_bytes=64)
         wsc = keep.tile([P, E], U8, name="wsc", align_bytes=64)
@@ -87,6 +88,10 @@ def tile_transformerencoderblock_pa_kernel(tc, h_attn, x, masks, Wo, bo, out_0, 
 
         def load_mask(n):
             nc.sync.dma_start(out=mrow[n][0:1, :], in_=masks[n])
+
+        def warm_pe():
+            jp = ps_a.tile([P, HALF], F32, tag="acc", name="jp")
+            nc.tensor.matmul(out=jp[:, 0:256], lhsT=wz[:, 0:P], rhs=wz[:], start=True, stop=True)
 
         def load_mask_spread(n):
             mask_dma[n] = keep.tile([P, T], BF16, name="mask_dma%d" % n)
@@ -213,26 +218,25 @@ def tile_transformerencoderblock_pa_kernel(tc, h_attn, x, masks, Wo, bo, out_0, 
             nc.scalar.activation(out=nbias[:, col], in_=negmean[:, col], func=ACT.Copy, scale=rstd[:, col])
 
         def neg_mean(i):
-            nc.gpsimd.tensor_scalar(
-                out=negmean[:, i : i + 1], in0=sums[:, i, 0:1], scalar1=-1.0 / T, scalar2=0.0, op0=ALU.mult, op1=ALU.add
-            )
+            nc.scalar.activation(out=negmean[:, i : i + 1], in_=sums[:, i, 0:1], func=ACT.Copy, scale=-1.0 / T)
 
         def squares(i):
             col = slice(i, i + 1)
             sq = work.tile([P, T], BF16, tag="sq", name="sq%d" % i)
             nc.scalar.activation(
-                out=sq[:], in_=ys[i][:], func=ACT.Square, bias=negmean[:, col], scale=1.0, accum_out=ssq[:, col]
+                out=sq[:], in_=ys[i][:], func=ACT.Square, bias=sums[:, i, 0:1], scale=-1.0 * T, accum_out=ssq[:, col]
             )
 
         def inv_std(i):
             col = slice(i, i + 1)
             nc.scalar.activation(
-                out=rstd[:, col], in_=ssq[:, col], func=ACT.Abs_reciprocal_sqrt, bias=eps_t[:, 0:1], scale=1.0 / T
+                out=rstd[:, col], in_=ssq[:, col], func=ACT.Abs_reciprocal_sqrt, bias=eps_t[:, 0:1],
+                scale=1.0 / (T * T * T),
             )
 
         def neg_bias(i):
             col = slice(i, i + 1)
-            nc.gpsimd.tensor_tensor(out=nbias[:, col], in0=negmean[:, col], in1=rstd[:, col], op=ALU.mult)
+            nc.scalar.activation(out=nbias[:, col], in_=negmean[:, col], func=ACT.Copy, scale=rstd[:, col])
 
         def normalise(i, k, pieces, eng):
             col = slice(i, i + 1)
@@ -263,14 +267,15 @@ def tile_transformerencoderblock_pa_kernel(tc, h_attn, x, masks, Wo, bo, out_0, 
 
         def one_amax():
             am1 = keep.tile([P, 1], F32, name="am1")
-            nc.vector.tensor_reduce(out=am1[:], in_=amx[:], axis=AX.X, op=ALU.max)
+            amxs = keep.tile([P, NU + 1], F32, name="amxs")
+            nc.vector.tensor_scalar(
+                out=amxs[:], in0=amx[:], scalar1=1.0 / 448.0, scalar2=None, op0=ALU.mult, op1=ALU.max, accum_out=am1[:]
+            )
             pt = ps_t.tile([P, P], F32, tag="tp", name="pt")
             nc.tensor.transpose(pt[:], am1[:, 0:1].to_broadcast([P, P]), ident[:])
             am2 = keep.tile([P, 1], F32, name="am2")
             nc.vector.tensor_reduce(out=am2[:], in_=pt[:], axis=AX.X, op=ALU.max)
-            rc = keep.tile([P, 1], F32, name="rc")
-            nc.vector.reciprocal(out=rc[:], in_=am2[:])
-            nc.vector.tensor_scalar(out=r448[:], in0=rc[:], scalar1=448.0, scalar2=None, op0=ALU.mult)
+            nc.vector.reciprocal(out=r448[:], in_=am2[:])
 
         def cast(i, eng):
             n, j = divmod(i, NJ)
@@ -287,9 +292,12 @@ def tile_transformerencoderblock_pa_kernel(tc, h_attn, x, masks, Wo, bo, out_0, 
                 out=out_1[n].rearrange("(p j) t -> p j t", j=NJ)[:, j, :], in_=f8[:].bitcast(U8)
             )
 
+        nc.vector.memset(wz[:], 0.0)
         nc.vector.memset(eps_t[:], EPS)
         nc.vector.memset(mrow[0][:], 0.0)
         nc.vector.memset(zero_t[:], 0.0)
+        nc.vector.memset(mrow[1][:], 0.0)
+        nc.vector.memset(mrow[2][:], 0.0)
         nc.scalar.activation(out=warm[:], in_=eps_t[:], func=ACT.Abs_reciprocal_sqrt)
         make_identity(nc, ident[:])
         nc.gpsimd.memset(ones[:], 1.0)
@@ -305,32 +313,35 @@ def tile_transformerencoderblock_pa_kernel(tc, h_attn, x, masks, Wo, bo, out_0, 
         load_x(1)
         load_x(2)
         load_x(3)
+        load_mask(1)
         load_h(1, 0)
         load_h(1, 1)
         load_h(1, 2)
         load_h(1, 3)
-        load_mask_spread(1)
         load_x(4)
         load_x(5)
         load_x(6)
         load_x(7)
+        load_mask(2)
         load_h(2, 0)
         load_h(2, 1)
         load_h(2, 2)
         load_h(2, 3)
-        load_mask_spread(2)
         load_x(8)
         load_x(9)
         load_x(10)
         load_x(11)
+        warm_pe()
+        warm_pe()
         transposes("w0")
         copy_out("w0", "V", wg, 0)
         transposes("h0_0")
         copy_out_h(0, 0, "S")
         transposes("h0_1")
-        copy_out_h(0, 1, "V")
         quantise_w(0)
+        copy_out_h(0, 1, "V")
         mask_mm(0, 0, "acc")
+        warm_pe()
         mask_copy(0, 0, "S")
         nc.vector.tensor_copy(out=bo32[:], in_=bo_bf[:])
         quantise(0, 0)
@@ -371,69 +382,81 @@ def tile_transformerencoderblock_pa_kernel(tc, h_attn, x, masks, Wo, bo, out_0, 
         squares(0)
         inv_std(0)
         neg_bias(0)
-        transposes("h2_0")
+        mask_mm(1, 0, "tp")
+        mask_mm(1, 1, "tp")
         bias_mask(2, 1, False)
         quantise(1, 0)
         residual_v(1)
-        copy_out_h(2, 0, "S")
+        mask_copy(1, 0, "S")
+        mask_copy(1, 1, "S")
         neg_mean(1)
-        normalise(0, 0, 1, "S")
-        store_0(0)
         squares(1)
+        normalise(0, 0, 2, "S")
         inv_std(1)
+        normalise(0, 1, 2, "S")
+        store_0(0)
         neg_bias(1)
-        transposes("h2_1")
         bias_mask(3, 1, False)
         quantise(1, 1)
         residual_v(2)
-        copy_out_h(2, 1, "S")
         neg_mean(2)
-        normalise(1, 0, 1, "S")
-        store_0(1)
         squares(2)
+        normalise(1, 0, 2, "S")
         inv_std(2)
+        normalise(1, 1, 2, "S")
+        store_0(1)
         neg_bias(2)
         project(4, 0)
         project(4, 1)
-        transposes("h2_2")
+        transposes("h2_0")
+        transposes("h2_1")
         bias_mask(4, 0, False)
         bias_mask(4, 1, False)
         residual_v(3)
-        copy_out_h(2, 2, "S")
+        copy_out_h(2, 0, "S")
+        copy_out_h(2, 1, "S")
         neg_mean(3)
-        normalise(2, 0, 1, "S")
-        store_0(2)
         squares(3)
+        normalise(2, 0, 2, "S")
         inv_std(3)
+        normalise(2, 1, 2, "S")
+        store_0(2)
         neg_bias(3)
-        row_amax(0, 0, T, 0)
         project(5, 0)
         project(5, 1)
+        transposes("h2_2")
         transposes("h2_3")
         bias_mask(5, 0, False)
         bias_mask(5, 1, False)
         residual_v(4)
+        copy_out_h(2, 2, "S")
         copy_out_h(2, 3, "S")
         neg_mean(4)
-        normalise(3, 0, 1, "S")
-        store_0(3)
         squares(4)
+        normalise(3, 0, 2, "S")
         inv_std(4)
+        normalise(3, 1, 2, "S")
+        store_0(3)
         neg_bias(4)
-        row_amax(1, 0, T, 1)
+        row_amax(0, 0, T, 0)
         project(6, 0)
         project(6, 1)
+        mask_mm(2, 0, "tp")
+        mask_mm(2, 1, "tp")
         bias_mask(6, 0, False)
         bias_mask(6, 1, False)
         quantise(2, 0)
         residual_v(5)
+        mask_copy(2, 0, "S")
+        mask_copy(2, 1, "S")
         neg_mean(5)
-        normalise(4, 0, 1, "S")
-        store_0(4)
         squares(5)
+        normalise(4, 0, 2, "S")
         inv_std(5)
+        normalise(4, 1, 2, "S")
+        store_0(4)
         neg_bias(5)
-        row_amax(2, 0, T, 2)
+        row_amax(1, 0, T, 1)
         project(7, 0)
         project(7, 1)
         bias_mask(7, 0, False)
@@ -441,70 +464,77 @@ def tile_transformerencoderblock_pa_kernel(tc, h_attn, x, masks, Wo, bo, out_0, 
         quantise(2, 1)
         residual_v(6)
         neg_mean(6)
-        normalise(5, 0, 1, "S")
-        store_0(5)
         squares(6)
+        normalise(5, 0, 2, "S")
         inv_std(6)
+        normalise(5, 1, 2, "S")
+        store_0(5)
         neg_bias(6)
-        row_amax(3, 0, T, 3)
+        row_amax(2, 0, T, 2)
         project(8, 0)
         project(8, 1)
         bias_mask(8, 0, False)
         bias_mask(8, 1, False)
         residual_v(7)
         neg_mean(7)
-        normalise(6, 0, 1, "S")
-        store_0(6)
         squares(7)
+        normalise(6, 0, 2, "S")
         inv_std(7)
+        normalise(6, 1, 2, "S")
+        store_0(6)
         neg_bias(7)
-        row_amax(4, 0, T, 4)
+        row_amax(3, 0, T, 3)
         project(9, 0)
         project(9, 1)
         bias_mask(9, 0, False)
         bias_mask(9, 1, False)
         residual_v(8)
         neg_mean(8)
-        normalise(7, 0, 1, "S")
-        store_0(7)
         squares(8)
+        normalise(7, 0, 2, "S")
         inv_std(8)
+        normalise(7, 1, 2, "S")
+        store_0(7)
         neg_bias(8)
-        row_amax(5, 0, T, 5)
+        row_amax(4, 0, T, 4)
         project(10, 0)
         project(10, 1)
         bias_mask(10, 0, False)
         bias_mask(10, 1, False)
         residual_v(9)
         neg_mean(9)
-        normalise(8, 0, 1, "S")
-        store_0(8)
         squares(9)
+        normalise(8, 0, 2, "S")
         inv_std(9)
+        normalise(8, 1, 2, "S")
+        store_0(8)
         neg_bias(9)
-        row_amax(6, 0, T, 6)
+        row_amax(5, 0, T, 5)
         project(11, 0)
         project(11, 1)
         bias_mask(11, 0, False)
         bias_mask(11, 1, False)
         residual_v(10)
         neg_mean(10)
-        normalise(9, 0, 1, "S")
-        store_0(9)
         squares(10)
+        normalise(9, 0, 2, "S")
         inv_std(10)
+        normalise(9, 1, 2, "S")
+        store_0(9)
         neg_bias(10)
-        row_amax(7, 0, T, 7)
+        row_amax(6, 0, T, 6)
         residual_v(11)
         neg_mean(11)
-        normalise(10, 0, 1, "S")
-        store_0(10)
         squares(11)
+        normalise(10, 0, 2, "S")
         inv_std(11)
+        normalise(10, 1, 2, "S")
+        store_0(10)
         neg_bias(11)
         normalise(11, 0, 2, "S")
         normalise(11, 1, 2, "S")
         store_0(11)
+        row_amax(7, 0, T, 7)
         row_amax(8, 0, T, 8)
         row_amax(9, 0, T, 9)
         row_amax(10, 0, T, 10)

@@ -12,7 +12,6 @@ FP8 = mybir.dt.float8_e4m3fn
 ALU = mybir.AluOpType
 ACT = mybir.ActivationFunctionType
 AX = mybir.AxisListType
-ENG = mybir.EngineType
 
 NSEQ, T, C, E = 3, 1024, 512, 512
 P = 128
@@ -21,6 +20,14 @@ NU = NSEQ * NJ
 HALF = 512
 EPS = 1e-5
 FLOPS = 2 * NSEQ * T * C * E
+
+G_UNITS = ()
+SX_ON_S = ()
+D_ON_V = ()
+V_COPIES = ("w0", "w1")
+AM_LAG = 4
+PIECES = (((0, 256), (256, 256), (512, 512)), ((0, 512), (512, 512)), ((0, 512), (512, 512)))
+SX_LEAD = 1
 
 
 def tile_transformerencoderblock_pa_kernel(tc, h_attn, x, masks, Wo, bo, out_0, out_1):
@@ -47,7 +54,6 @@ def tile_transformerencoderblock_pa_kernel(tc, h_attn, x, masks, Wo, bo, out_0, 
         bo_bf = keep.tile([P, NJ], BF16, name="bo_bf")
         mask_bc = keep.tile([P, NSEQ * T], F32, name="mask_bc")
         bo32 = keep.tile([P, NJ], F32, name="bo32")
-        mask_dma = {}
         wz = keep.tile([P, 256], F32, name="wz")
         wg = keep.tile([P, 4 * E], BF16, name="wg", align_bytes=64)
         wc = keep.tile([P, E], U32, name="wc", align_bytes=64)
@@ -93,15 +99,6 @@ def tile_transformerencoderblock_pa_kernel(tc, h_attn, x, masks, Wo, bo, out_0, 
             jp = ps_a.tile([P, HALF], F32, tag="acc", name="jp")
             nc.tensor.matmul(out=jp[:, 0:256], lhsT=wz[:, 0:P], rhs=wz[:], start=True, stop=True)
 
-        def load_mask_spread(n):
-            mask_dma[n] = keep.tile([P, T], BF16, name="mask_dma%d" % n)
-            nc.sync.dma_start(out=mask_dma[n][:], in_=masks[n, 0].partition_broadcast(P))
-
-        def mask_of(n, half):
-            if n in mask_dma:
-                return mask_dma[n][:, half * HALF : (half + 1) * HALF]
-            return mask_bc[:, n * T + half * HALF : n * T + (half + 1) * HALF]
-
         def mask_mm(n, half, where):
             pool = ps_a if where == "acc" else ps_t
             pms[(n, half)] = pool.tile([P, HALF], F32, tag=where, name="pm%d_%d" % (n, half))
@@ -140,82 +137,71 @@ def tile_transformerencoderblock_pa_kernel(tc, h_attn, x, masks, Wo, bo, out_0, 
                 in_=wg[:, b * 1024 : (b + 1) * 1024],
             )
 
-        def quantise(n, half):
-            hc[(n, half)] = keep.tile([P, HALF], U32, name="hc%d_%d" % (n, half), align_bytes=64)
-            hs[(n, half)] = keep.tile([P, HALF], U8, name="hs%d_%d" % (n, half), align_bytes=64)
+        def quantise(n, pc):
+            c0, w = PIECES[n][pc]
+            half = c0 // HALF
+            if (n, half) not in hc:
+                hc[(n, half)] = keep.tile([P, HALF], U32, name="hc%d_%d" % (n, half), align_bytes=64)
+                hs[(n, half)] = keep.tile([P, HALF], U8, name="hs%d_%d" % (n, half), align_bytes=64)
+            a = c0 - half * HALF
             nc.vector.quantize_mx(
-                out=hc[(n, half)][:].bitcast(FP8X4), scales=hs[(n, half)][:], in_=hg[(n, half)][:]
+                out=hc[(n, half)][:, a : a + w].bitcast(FP8X4), scales=hs[(n, half)][:, a : a + w],
+                in_=hg[(n, half)][:, 4 * a : 4 * (a + w)],
             )
 
-        def sum_x(i, eng):
-            jx = work.tile([P, T], BF16, tag="jx" + eng, name="jx%d" % i)
-            if eng == "V":
+        def sum_x(i):
+            if i in SX_ON_S:
+                jx = work.tile([P, T], BF16, tag="jxS", name="jx%d" % i)
+                nc.scalar.activation(out=jx[:], in_=xs[i][:], func=ACT.Copy, accum_out=sums[:, i, 2:3])
+            else:
+                jx = work.tile([P, T], BF16, tag="jxV", name="jx%d" % i)
                 nc.vector.tensor_scalar(
                     out=jx[:], in0=xs[i][:], scalar1=1.0, scalar2=None, op0=ALU.mult, op1=ALU.add,
                     accum_out=sums[:, i, 2:3],
                 )
-            else:
-                nc.scalar.activation(out=jx[:], in_=xs[i][:], func=ACT.Copy, accum_out=sums[:, i, 2:3])
 
-        def project(i, half):
+        def project(i, pc):
             n, j = divmod(i, NJ)
-            accs[(i, half)] = ps_a.tile([P, HALF], F32, tag="acc", name="acc%d_%d" % (i, half))
+            c0, w = PIECES[n][pc]
+            half = c0 // HALF
+            a = c0 - half * HALF
+            accs[(i, pc)] = ps_a.tile([P, HALF], F32, tag="acc", name="acc%d_%d" % (i, pc))
             nc.tensor.matmul_mx(
-                out=accs[(i, half)][:],
+                out=accs[(i, pc)][:, 0:w],
                 lhsT=wc[:, j * P : (j + 1) * P].bitcast(FP8X4),
                 lhsT_scale=wsc[:, j * P : (j + 1) * P],
-                rhs=hc[(n, half)][:].bitcast(FP8X4),
-                rhs_scale=hs[(n, half)][:],
+                rhs=hc[(n, half)][:, a : a + w].bitcast(FP8X4),
+                rhs_scale=hs[(n, half)][:, a : a + w],
                 start=True,
                 stop=True,
             )
 
-        def bias_mask(i, half, with_sum):
+        def bias_mask(i, pc):
             n, j = divmod(i, NJ)
+            c0, w = PIECES[n][pc]
             if i not in us:
                 us[i] = upool.tile([P, T], F32, tag="u", name="u%d" % i)
             nc.vector.scalar_tensor_tensor(
-                out=us[i][:, half * HALF : (half + 1) * HALF],
-                in0=accs[(i, half)][:],
+                out=us[i][:, c0 : c0 + w],
+                in0=accs[(i, pc)][:, 0:w],
                 scalar=bo32[:, j : j + 1],
-                in1=mask_of(n, half),
+                in1=mask_bc[:, n * T + c0 : n * T + c0 + w],
                 op0=ALU.add,
                 op1=ALU.mult,
-                accum_out=(sums[:, i, half : half + 1] if with_sum else None),
             )
 
-        def new_y(i):
+        def add_g(i, half):
             if i not in ys:
                 ys[i] = ypool.tile([P, T], F32, tag="y", name="y%d" % i)
-
-        def residual_g(i, half):
-            new_y(i)
             cols = slice(half * HALF, (half + 1) * HALF)
             nc.gpsimd.tensor_tensor(out=ys[i][:, cols], in0=us[i][:, cols], in1=xs[i][:, cols], op=ALU.add)
 
-        def residual_v(i):
-            new_y(i)
+        def add_v(i):
+            ys[i] = ypool.tile([P, T], F32, tag="y", name="y%d" % i)
             nc.vector.scalar_tensor_tensor(
                 out=ys[i][:], in0=us[i][:], scalar=1.0, in1=xs[i][:], op0=ALU.mult, op1=ALU.add,
                 accum_out=sums[:, i, 0:1],
             )
-
-        def stats(i, parts):
-            col = slice(i, i + 1)
-            if parts == 3:
-                nc.scalar.activation(
-                    out=junk3[:, i, 0:3], in_=sums[:, i, 0:3], func=ACT.Copy, scale=-1.0 / T, accum_out=negmean[:, col]
-                )
-            else:
-                nc.scalar.activation(out=negmean[:, col], in_=sums[:, i, 0:1], func=ACT.Copy, scale=-1.0 / T)
-            sq = work.tile([P, T], BF16, tag="sq", name="sq%d" % i)
-            nc.scalar.activation(
-                out=sq[:], in_=ys[i][:], func=ACT.Square, bias=negmean[:, col], scale=1.0, accum_out=ssq[:, col]
-            )
-            nc.scalar.activation(
-                out=rstd[:, col], in_=ssq[:, col], func=ACT.Abs_reciprocal_sqrt, bias=eps_t[:, 0:1], scale=1.0 / T
-            )
-            nc.scalar.activation(out=nbias[:, col], in_=negmean[:, col], func=ACT.Copy, scale=rstd[:, col])
 
         def neg_mean(i):
             nc.scalar.activation(out=negmean[:, i : i + 1], in_=sums[:, i, 0:1], func=ACT.Copy, scale=-1.0 / T)
@@ -238,20 +224,19 @@ def tile_transformerencoderblock_pa_kernel(tc, h_attn, x, masks, Wo, bo, out_0, 
             col = slice(i, i + 1)
             nc.scalar.activation(out=nbias[:, col], in_=negmean[:, col], func=ACT.Copy, scale=rstd[:, col])
 
-        def normalise(i, k, pieces, eng):
+        def normalise(i, k):
             col = slice(i, i + 1)
             if i not in o0:
                 o0[i] = keep.tile([P, T], F32, name="o0_%d" % i)
-            w = T // pieces
-            cols = slice(k * w, (k + 1) * w)
-            if eng == "S":
-                nc.scalar.activation(
-                    out=o0[i][:, cols], in_=ys[i][:, cols], func=ACT.Identity, bias=nbias[:, col], scale=rstd[:, col]
-                )
-            else:
-                nc.gpsimd.tensor_scalar(
+            cols = slice(k * HALF, (k + 1) * HALF)
+            if i in D_ON_V:
+                nc.vector.tensor_scalar(
                     out=o0[i][:, cols], in0=ys[i][:, cols], scalar1=rstd[:, col], scalar2=nbias[:, col],
                     op0=ALU.mult, op1=ALU.add,
+                )
+            else:
+                nc.scalar.activation(
+                    out=o0[i][:, cols], in_=ys[i][:, cols], func=ACT.Identity, bias=nbias[:, col], scale=rstd[:, col]
                 )
 
         def store_0(i):
@@ -305,251 +290,165 @@ def tile_transformerencoderblock_pa_kernel(tc, h_attn, x, masks, Wo, bo, out_0, 
         load_h(0, 0)
         load_mask(0)
         nc.sync.dma_start(out=bo_bf[:], in_=bo.rearrange("(p j) -> p j", j=NJ))
-        load_h(0, 1)
         load_w(1)
+        load_h(0, 1)
         load_h(0, 2)
         load_h(0, 3)
-        load_x(0)
-        load_x(1)
-        load_x(2)
-        load_x(3)
-        load_mask(1)
-        load_h(1, 0)
-        load_h(1, 1)
-        load_h(1, 2)
-        load_h(1, 3)
-        load_x(4)
-        load_x(5)
-        load_x(6)
-        load_x(7)
-        load_mask(2)
-        load_h(2, 0)
-        load_h(2, 1)
-        load_h(2, 2)
-        load_h(2, 3)
-        load_x(8)
-        load_x(9)
-        load_x(10)
-        load_x(11)
-        warm_pe()
-        warm_pe()
-        transposes("w0")
-        copy_out("w0", "V", wg, 0)
-        transposes("h0_0")
-        copy_out_h(0, 0, "S")
-        transposes("h0_1")
-        quantise_w(0)
-        copy_out_h(0, 1, "V")
-        mask_mm(0, 0, "acc")
-        warm_pe()
-        mask_copy(0, 0, "S")
-        nc.vector.tensor_copy(out=bo32[:], in_=bo_bf[:])
-        quantise(0, 0)
-        transposes("w1")
-        copy_out("w1", "S", wg, 1)
-        transposes("h0_2")
-        copy_out_h(0, 2, "S")
-        project(0, 0)
-        project(1, 0)
-        transposes("h0_3")
-        copy_out_h(0, 3, "S")
-        mask_mm(0, 1, "acc")
-        mask_copy(0, 1, "S")
-        bias_mask(0, 0, False)
-        quantise_w(1)
-        bias_mask(1, 0, False)
-        project(2, 0)
-        project(3, 0)
-        bias_mask(2, 0, False)
-        quantise(0, 1)
-        bias_mask(3, 0, False)
-        project(0, 1)
-        project(1, 1)
-        project(2, 1)
-        project(3, 1)
-        bias_mask(0, 1, False)
-        transposes("h1_0")
-        transposes("h1_1")
-        transposes("h1_2")
-        transposes("h1_3")
-        bias_mask(1, 1, False)
-        residual_v(0)
-        copy_out_h(1, 0, "S")
-        copy_out_h(1, 1, "S")
-        copy_out_h(1, 2, "S")
-        copy_out_h(1, 3, "S")
-        neg_mean(0)
-        squares(0)
-        inv_std(0)
-        neg_bias(0)
-        mask_mm(1, 0, "tp")
-        mask_mm(1, 1, "tp")
-        bias_mask(2, 1, False)
-        quantise(1, 0)
-        residual_v(1)
-        mask_copy(1, 0, "S")
-        mask_copy(1, 1, "S")
-        neg_mean(1)
-        squares(1)
-        normalise(0, 0, 2, "S")
-        inv_std(1)
-        normalise(0, 1, 2, "S")
-        store_0(0)
-        neg_bias(1)
-        bias_mask(3, 1, False)
-        quantise(1, 1)
-        residual_v(2)
-        neg_mean(2)
-        squares(2)
-        normalise(1, 0, 2, "S")
-        inv_std(2)
-        normalise(1, 1, 2, "S")
-        store_0(1)
-        neg_bias(2)
-        project(4, 0)
-        project(4, 1)
-        transposes("h2_0")
-        transposes("h2_1")
-        bias_mask(4, 0, False)
-        bias_mask(4, 1, False)
-        residual_v(3)
-        copy_out_h(2, 0, "S")
-        copy_out_h(2, 1, "S")
-        neg_mean(3)
-        squares(3)
-        normalise(2, 0, 2, "S")
-        inv_std(3)
-        normalise(2, 1, 2, "S")
-        store_0(2)
-        neg_bias(3)
-        project(5, 0)
-        project(5, 1)
-        transposes("h2_2")
-        transposes("h2_3")
-        bias_mask(5, 0, False)
-        bias_mask(5, 1, False)
-        residual_v(4)
-        copy_out_h(2, 2, "S")
-        copy_out_h(2, 3, "S")
-        neg_mean(4)
-        squares(4)
-        normalise(3, 0, 2, "S")
-        inv_std(4)
-        normalise(3, 1, 2, "S")
-        store_0(3)
-        neg_bias(4)
-        row_amax(0, 0, T, 0)
-        project(6, 0)
-        project(6, 1)
-        mask_mm(2, 0, "tp")
-        mask_mm(2, 1, "tp")
-        bias_mask(6, 0, False)
-        bias_mask(6, 1, False)
-        quantise(2, 0)
-        residual_v(5)
-        mask_copy(2, 0, "S")
-        mask_copy(2, 1, "S")
-        neg_mean(5)
-        squares(5)
-        normalise(4, 0, 2, "S")
-        inv_std(5)
-        normalise(4, 1, 2, "S")
-        store_0(4)
-        neg_bias(5)
-        row_amax(1, 0, T, 1)
-        project(7, 0)
-        project(7, 1)
-        bias_mask(7, 0, False)
-        bias_mask(7, 1, False)
-        quantise(2, 1)
-        residual_v(6)
-        neg_mean(6)
-        squares(6)
-        normalise(5, 0, 2, "S")
-        inv_std(6)
-        normalise(5, 1, 2, "S")
-        store_0(5)
-        neg_bias(6)
-        row_amax(2, 0, T, 2)
-        project(8, 0)
-        project(8, 1)
-        bias_mask(8, 0, False)
-        bias_mask(8, 1, False)
-        residual_v(7)
-        neg_mean(7)
-        squares(7)
-        normalise(6, 0, 2, "S")
-        inv_std(7)
-        normalise(6, 1, 2, "S")
-        store_0(6)
-        neg_bias(7)
-        row_amax(3, 0, T, 3)
-        project(9, 0)
-        project(9, 1)
-        bias_mask(9, 0, False)
-        bias_mask(9, 1, False)
-        residual_v(8)
-        neg_mean(8)
-        squares(8)
-        normalise(7, 0, 2, "S")
-        inv_std(8)
-        normalise(7, 1, 2, "S")
-        store_0(7)
-        neg_bias(8)
-        row_amax(4, 0, T, 4)
-        project(10, 0)
-        project(10, 1)
-        bias_mask(10, 0, False)
-        bias_mask(10, 1, False)
-        residual_v(9)
-        neg_mean(9)
-        squares(9)
-        normalise(8, 0, 2, "S")
-        inv_std(9)
-        normalise(8, 1, 2, "S")
-        store_0(8)
-        neg_bias(9)
-        row_amax(5, 0, T, 5)
-        project(11, 0)
-        project(11, 1)
-        bias_mask(11, 0, False)
-        bias_mask(11, 1, False)
-        residual_v(10)
-        neg_mean(10)
-        squares(10)
-        normalise(9, 0, 2, "S")
-        inv_std(10)
-        normalise(9, 1, 2, "S")
-        store_0(9)
-        neg_bias(10)
-        row_amax(6, 0, T, 6)
-        residual_v(11)
-        neg_mean(11)
-        squares(11)
-        normalise(10, 0, 2, "S")
-        inv_std(11)
-        normalise(10, 1, 2, "S")
-        store_0(10)
-        neg_bias(11)
-        normalise(11, 0, 2, "S")
-        normalise(11, 1, 2, "S")
-        store_0(11)
-        row_amax(7, 0, T, 7)
-        row_amax(8, 0, T, 8)
-        row_amax(9, 0, T, 9)
-        row_amax(10, 0, T, 10)
-        row_amax(11, 0, HALF, 11)
-        row_amax(11, HALF, T, NU)
+        for n in range(NSEQ):
+            if n > 0:
+                load_mask(n)
+                for c in range(4):
+                    load_h(n, c)
+            for j in range(NJ):
+                load_x(n * NJ + j)
+
+        ops = {}
+
+        def op(name, fn, args, needs):
+            ops[name] = (fn, args, list(needs))
+
+        def rotate(makers, readers_of, bufs):
+            for m in range(bufs, len(makers)):
+                ops[makers[m]][2].extend(readers_of(makers[m - bufs]))
+
+        def eng_of(key):
+            return "V" if key in V_COPIES else "S"
+
+        def widen_bo():
+            nc.vector.tensor_copy(out=bo32[:], in_=bo_bf[:])
+
+        op(("BO",), widen_bo, (), ())
+        for w in range(2):
+            op(("WARM", w), warm_pe, (), ())
+        for b in range(2):
+            op(("T", "w%d" % b), transposes, ("w%d" % b,), ())
+            op(("C", "w%d" % b), copy_out, ("w%d" % b, eng_of("w%d" % b), wg, b), (("T", "w%d" % b),))
+            op(("QW", b), quantise_w, (b,), (("C", "w%d" % b),))
+        for n in range(NSEQ):
+            for c in range(4):
+                key = "h%d_%d" % (n, c)
+                op(("T", key), transposes, (key,), ())
+                op(("C", key), copy_out_h, (n, c, eng_of(key)), (("T", key),) + ((("C", "h%d_%d" % (n, c - 1)),) if c % 2 else ()))
+            for pc in range(len(PIECES[n])):
+                c0, w = PIECES[n][pc]
+                op(("Q", n, pc), quantise, (n, pc), [("C", "h%d_%d" % (n, c)) for c in range(c0 // 256, (c0 + w) // 256)])
+            for half in range(2):
+                op(("MM", n, half), mask_mm, (n, half, "acc" if n == 0 else "tp"), ())
+                op(("C", "m%d_%d" % (n, half)), mask_copy, (n, half, eng_of("m%d_%d" % (n, half))), (("MM", n, half),))
+        for i in range(NU):
+            n, j = divmod(i, NJ)
+            for pc in range(len(PIECES[n])):
+                op(("P", i, pc), project, (i, pc), (("Q", n, pc), ("QW", j // 2)))
+                op(("U", i, pc), bias_mask, (i, pc), (("P", i, pc), ("C", "m%d_%d" % (n, PIECES[n][pc][0] // HALF)), ("BO",)))
+            for half in range(2):
+                op(("D", i, half), normalise, (i, half), (("NB", i),))
+            op(("YV", i), add_v, (i,), [("U", i, pc) for pc in range(len(PIECES[n]))])
+            op(("SX", i), sum_x, (i,), ())
+            made = (("YG", i, 0), ("YG", i, 1), ("SX", i)) if i in G_UNITS else (("YV", i),)
+            op(("NM", i), neg_mean, (i,), made)
+            op(("SQ", i), squares, (i,), made)
+            op(("IS", i), inv_std, (i,), (("SQ", i),))
+            op(("NB", i), neg_bias, (i,), (("IS", i), ("NM", i)))
+            op(("ST", i), store_0, (i,), (("D", i, 0), ("D", i, 1)))
+            if i < NU - 1:
+                op(("AM", i), row_amax, (i, 0, T, i), (("D", i, 0), ("D", i, 1)))
+        op(("AM", NU - 1, 0), row_amax, (NU - 1, 0, HALF, NU - 1), (("D", NU - 1, 0),))
+        op(("AM", NU - 1, 1), row_amax, (NU - 1, HALF, T, NU), (("D", NU - 1, 1),))
+
+        q_pe = [("WARM", 0), ("WARM", 1), ("T", "w0"), ("T", "h0_0"), ("MM", 0, 0), ("T", "w1"), ("T", "h0_1"),
+                ("P", 0, 0), ("P", 1, 0), ("T", "h0_2"), ("P", 2, 0), ("P", 3, 0), ("T", "h0_3"), ("MM", 0, 1)]
+        q_pe += [("P", j, 1) for j in range(NJ)] + [("P", j, 2) for j in range(NJ)] + [("T", "h1_%d" % c) for c in range(4)] + [("MM", 1, 0), ("MM", 1, 1)]
+        q_pe += [("P", 4, 0), ("P", 4, 1), ("T", "h2_0"), ("T", "h2_1"), ("P", 5, 0), ("P", 5, 1), ("T", "h2_2"), ("T", "h2_3")]
+        q_pe += [("P", 6, 0), ("P", 6, 1), ("MM", 2, 0), ("MM", 2, 1)] + [("P", i, half) for i in range(7, NU) for half in range(2)]
+
+        q_g = [nm for nm in [("YG", 0, 0), ("YG", 1, 0), ("YG", 2, 0), ("YG", 0, 1), ("YG", 1, 1), ("YG", 2, 1), ("YG", 3, 0), ("YG", 3, 1)] if nm[1] in G_UNITS]
+        q_g += [("YG", i, half) for i in G_UNITS if i >= NJ for half in range(2)]
+
+        def v_add(i):
+            if i in G_UNITS:
+                return [] if i in SX_ON_S else [("SX", i)]
+            return [("YV", i)]
+
+        q_v = [("C", "w0"), ("QW", 0), ("BO",), ("Q", 0, 0), ("C", "w1"), ("QW", 1)] + [("U", j, 0) for j in range(NJ)] + [("Q", 0, 1), ("Q", 0, 2)]
+        q_v += [("U", j, 1) for j in range(NJ)] + [("U", j, 2) for j in range(NJ)] + v_add(0) + [("Q", 1, 0)] + v_add(1) + [("Q", 1, 1)] + v_add(2)
+        q_v += [("C", k) for k in ("m1_0", "m1_1") if k in V_COPIES]
+        late = []
+        for i in range(NU):
+            if i in D_ON_V:
+                late += [("D", i, 0), ("D", i, 1)]
+            late += [("AM", i)] if i < NU - 1 else [("AM", i, 0), ("AM", i, 1)]
+        for i in range(NJ, NU + 1):
+            if i < NU:
+                q_v += [("U", i, 0), ("U", i, 1)]
+            if i == 6:
+                q_v += [("C", k) for k in ("m2_0",) if k in V_COPIES] + [("Q", 2, 0)]
+            if i == 7:
+                q_v += [("C", k) for k in ("m2_1",) if k in V_COPIES] + [("Q", 2, 1)]
+            q_v += v_add(i - 1)
+            if i - 1 - AM_LAG >= 0:
+                q_v += [late[i - 1 - AM_LAG]]
+        q_v += late[NU - AM_LAG :]
+
+        q_s = [("C", "h0_0"), ("C", "m0_0"), ("C", "h0_1"), ("C", "h0_2"), ("C", "h0_3"), ("C", "m0_1")]
+        q_s += [("C", "h1_%d" % c) for c in range(4)]
+        for k in range(NU + 1):
+            if k == 1:
+                q_s += [("C", c) for c in ("m1_0", "m1_1") if c not in V_COPIES]
+            if k == 3:
+                q_s += [("C", "h2_0"), ("C", "h2_1")]
+            if k == 4:
+                q_s += [("C", "h2_2"), ("C", "h2_3")]
+            if k == 5:
+                q_s += [("C", c) for c in ("m2_0", "m2_1") if c not in V_COPIES]
+            if k + SX_LEAD < NU and k + SX_LEAD in SX_ON_S:
+                q_s += [("SX", k + SX_LEAD)]
+            if k < NU:
+                q_s += [("NM", k), ("SQ", k)]
+            if k > 0:
+                q_s += [("D", k - 1, 0)]
+            if k < NU:
+                q_s += [("IS", k)]
+            if k > 0:
+                q_s += [("D", k - 1, 1)]
+            if k < NU:
+                q_s += [("NB", k)]
+        q_sp = [("ST", i) for i in range(NU)]
+
+        def psum_reader(nm):
+            if nm[0] == "T":
+                return [("C", nm[1])]
+            if nm[0] == "MM":
+                return [("C", "m%d_%d" % (nm[1], nm[2]))]
+            if nm[0] == "P":
+                return [("U", nm[1], nm[2])]
+            return []
+
+        def in_acc(nm):
+            return nm[0] in ("WARM", "P") or (nm[0] == "MM" and nm[1] == 0)
+
+        rotate([nm for nm in q_pe if in_acc(nm)], psum_reader, 4)
+        rotate([nm for nm in q_pe if not in_acc(nm)], psum_reader, 4)
+        rotate([("U", i, 0) for i in range(NU)], lambda nm: [("YV", nm[1])], 5)
+        rotate([("YG", i, 0) if i in G_UNITS else ("YV", i) for i in range(NU)],
+               lambda nm: [("SQ", nm[1]), ("D", nm[1], 0), ("D", nm[1], 1)], 6)
+        rotate([("C", "h%d_%d" % (n, c)) for n in range(NSEQ) for c in (0, 2)],
+               lambda nm: [("Q", int(nm[1][1]), pc) for pc in range(len(PIECES[int(nm[1][1])]))], 3)
+
+        queues = [q_pe, q_v, q_g, q_s, q_sp]
+        heads = [0, 0, 0, 0, 0]
+        done = set()
+        left = sum(len(q) for q in queues)
+        while left > 0:
+            before = left
+            for k in range(5):
+                q = queues[k]
+                while heads[k] < len(q) and all(nm in done for nm in ops[q[heads[k]]][2]):
+                    fn, args, needs = ops[q[heads[k]]]
+                    fn(*args)
+                    done.add(q[heads[k]])
+                    heads[k] += 1
+                    left -= 1
+            assert left < before
         one_amax()
-        cast(0, "V")
-        cast(1, "V")
-        cast(2, "S")
-        cast(3, "V")
-        cast(4, "V")
-        cast(5, "S")
-        cast(6, "V")
-        cast(7, "V")
-        cast(8, "S")
-        cast(9, "V")
-        cast(10, "V")
-        cast(11, "S")
+        for i in range(NU):
+            cast(i, "S" if i % 3 == 2 else "V")

@@ -21,13 +21,14 @@ HALF = 512
 EPS = 1e-5
 FLOPS = 2 * NSEQ * T * C * E
 
-G_UNITS = ()
-SX_ON_S = ()
+G_UNITS = (5, 9)
+SX_ON_S = (5, 9)
 D_ON_V = ()
 V_COPIES = ("w0", "w1")
 AM_LAG = 4
+MASK_DMA = (1, 2)
 PIECES = (((0, 256), (256, 256), (512, 512)), ((0, 512), (512, 512)), ((0, 512), (512, 512)))
-SX_LEAD = 1
+SX_LEAD = 4
 
 
 def tile_transformerencoderblock_pa_kernel(tc, h_attn, x, masks, Wo, bo, out_0, out_1):
@@ -94,6 +95,12 @@ def tile_transformerencoderblock_pa_kernel(tc, h_attn, x, masks, Wo, bo, out_0, 
 
         def load_mask(n):
             nc.sync.dma_start(out=mrow[n][0:1, :], in_=masks[n])
+
+        mask_sp = {}
+
+        def load_mask_spread(n):
+            mask_sp[n] = keep.tile([P, T], BF16, name="mask_sp%d" % n)
+            nc.sync.dma_start(out=mask_sp[n][:], in_=masks[n, 0].partition_broadcast(P))
 
         def warm_pe():
             jp = ps_a.tile([P, HALF], F32, tag="acc", name="jp")
@@ -185,9 +192,10 @@ def tile_transformerencoderblock_pa_kernel(tc, h_attn, x, masks, Wo, bo, out_0, 
                 out=us[i][:, c0 : c0 + w],
                 in0=accs[(i, pc)][:, 0:w],
                 scalar=bo32[:, j : j + 1],
-                in1=mask_bc[:, n * T + c0 : n * T + c0 + w],
+                in1=(mask_sp[n][:, c0 : c0 + w] if n in MASK_DMA else mask_bc[:, n * T + c0 : n * T + c0 + w]),
                 op0=ALU.add,
                 op1=ALU.mult,
+                accum_out=(sums[:, i, pc : pc + 1] if i in G_UNITS else None),
             )
 
         def add_g(i, half):
@@ -204,20 +212,30 @@ def tile_transformerencoderblock_pa_kernel(tc, h_attn, x, masks, Wo, bo, out_0, 
             )
 
         def neg_mean(i):
-            nc.scalar.activation(out=negmean[:, i : i + 1], in_=sums[:, i, 0:1], func=ACT.Copy, scale=-1.0 / T)
+            if i in G_UNITS:
+                nc.scalar.activation(
+                    out=junk3[:, i, 0:3], in_=sums[:, i, 0:3], func=ACT.Copy, scale=-1.0 / T, accum_out=negmean[:, i : i + 1]
+                )
+            else:
+                nc.scalar.activation(out=negmean[:, i : i + 1], in_=sums[:, i, 0:1], func=ACT.Copy, scale=-1.0 / T)
 
         def squares(i):
             col = slice(i, i + 1)
             sq = work.tile([P, T], BF16, tag="sq", name="sq%d" % i)
-            nc.scalar.activation(
-                out=sq[:], in_=ys[i][:], func=ACT.Square, bias=sums[:, i, 0:1], scale=-1.0 * T, accum_out=ssq[:, col]
-            )
+            if i in G_UNITS:
+                nc.scalar.activation(
+                    out=sq[:], in_=ys[i][:], func=ACT.Square, bias=negmean[:, col], scale=1.0, accum_out=ssq[:, col]
+                )
+            else:
+                nc.scalar.activation(
+                    out=sq[:], in_=ys[i][:], func=ACT.Square, bias=sums[:, i, 0:1], scale=-1.0 * T, accum_out=ssq[:, col]
+                )
 
         def inv_std(i):
             col = slice(i, i + 1)
             nc.scalar.activation(
                 out=rstd[:, col], in_=ssq[:, col], func=ACT.Abs_reciprocal_sqrt, bias=eps_t[:, 0:1],
-                scale=1.0 / (T * T * T),
+                scale=(1.0 / T if i in G_UNITS else 1.0 / (T * T * T)),
             )
 
         def neg_bias(i):
@@ -296,9 +314,12 @@ def tile_transformerencoderblock_pa_kernel(tc, h_attn, x, masks, Wo, bo, out_0, 
         load_h(0, 3)
         for n in range(NSEQ):
             if n > 0:
-                load_mask(n)
+                if n not in MASK_DMA:
+                    load_mask(n)
                 for c in range(4):
                     load_h(n, c)
+                if n in MASK_DMA:
+                    load_mask_spread(n)
             for j in range(NJ):
                 load_x(n * NJ + j)
 
@@ -339,14 +360,15 @@ def tile_transformerencoderblock_pa_kernel(tc, h_attn, x, masks, Wo, bo, out_0, 
             n, j = divmod(i, NJ)
             for pc in range(len(PIECES[n])):
                 op(("P", i, pc), project, (i, pc), (("Q", n, pc), ("QW", j // 2)))
-                op(("U", i, pc), bias_mask, (i, pc), (("P", i, pc), ("C", "m%d_%d" % (n, PIECES[n][pc][0] // HALF)), ("BO",)))
+                op(("U", i, pc), bias_mask, (i, pc), [("P", i, pc), ("BO",)] + ([] if n in MASK_DMA else [("C", "m%d_%d" % (n, PIECES[n][pc][0] // HALF))]))
             for half in range(2):
                 op(("D", i, half), normalise, (i, half), (("NB", i),))
+                op(("YG", i, half), add_g, (i, half), (("U", i, half),))
             op(("YV", i), add_v, (i,), [("U", i, pc) for pc in range(len(PIECES[n]))])
             op(("SX", i), sum_x, (i,), ())
             made = (("YG", i, 0), ("YG", i, 1), ("SX", i)) if i in G_UNITS else (("YV", i),)
             op(("NM", i), neg_mean, (i,), made)
-            op(("SQ", i), squares, (i,), made)
+            op(("SQ", i), squares, (i,), made + ((("NM", i),) if i in G_UNITS else ()))
             op(("IS", i), inv_std, (i,), (("SQ", i),))
             op(("NB", i), neg_bias, (i,), (("IS", i), ("NM", i)))
             op(("ST", i), store_0, (i,), (("D", i, 0), ("D", i, 1)))
@@ -357,9 +379,9 @@ def tile_transformerencoderblock_pa_kernel(tc, h_attn, x, masks, Wo, bo, out_0, 
 
         q_pe = [("WARM", 0), ("WARM", 1), ("T", "w0"), ("T", "h0_0"), ("MM", 0, 0), ("T", "w1"), ("T", "h0_1"),
                 ("P", 0, 0), ("P", 1, 0), ("T", "h0_2"), ("P", 2, 0), ("P", 3, 0), ("T", "h0_3"), ("MM", 0, 1)]
-        q_pe += [("P", j, 1) for j in range(NJ)] + [("P", j, 2) for j in range(NJ)] + [("T", "h1_%d" % c) for c in range(4)] + [("MM", 1, 0), ("MM", 1, 1)]
+        q_pe += [("P", j, 1) for j in range(NJ)] + [("P", j, 2) for j in range(NJ)] + [("T", "h1_%d" % c) for c in range(4)] + [("MM", 1, half) for half in range(2) if 1 not in MASK_DMA]
         q_pe += [("P", 4, 0), ("P", 4, 1), ("T", "h2_0"), ("T", "h2_1"), ("P", 5, 0), ("P", 5, 1), ("T", "h2_2"), ("T", "h2_3")]
-        q_pe += [("P", 6, 0), ("P", 6, 1), ("MM", 2, 0), ("MM", 2, 1)] + [("P", i, half) for i in range(7, NU) for half in range(2)]
+        q_pe += [("P", 6, 0), ("P", 6, 1)] + [("MM", 2, half) for half in range(2) if 2 not in MASK_DMA] + [("P", i, half) for i in range(7, NU) for half in range(2)]
 
         q_g = [nm for nm in [("YG", 0, 0), ("YG", 1, 0), ("YG", 2, 0), ("YG", 0, 1), ("YG", 1, 1), ("YG", 2, 1), ("YG", 3, 0), ("YG", 3, 1)] if nm[1] in G_UNITS]
         q_g += [("YG", i, half) for i in G_UNITS if i >= NJ for half in range(2)]
@@ -377,34 +399,44 @@ def tile_transformerencoderblock_pa_kernel(tc, h_attn, x, masks, Wo, bo, out_0, 
             if i in D_ON_V:
                 late += [("D", i, 0), ("D", i, 1)]
             late += [("AM", i)] if i < NU - 1 else [("AM", i, 0), ("AM", i, 1)]
+        n_am = 0
         for i in range(NJ, NU + 1):
+            if i in G_UNITS:
+                q_v += v_add(i - 1)
             if i < NU:
                 q_v += [("U", i, 0), ("U", i, 1)]
             if i == 6:
-                q_v += [("C", k) for k in ("m2_0",) if k in V_COPIES] + [("Q", 2, 0)]
+                q_v += [("Q", 2, 0)]
             if i == 7:
-                q_v += [("C", k) for k in ("m2_1",) if k in V_COPIES] + [("Q", 2, 1)]
-            q_v += v_add(i - 1)
+                q_v += [("Q", 2, 1)]
+            if i not in G_UNITS:
+                q_v += v_add(i - 1)
             if i - 1 - AM_LAG >= 0:
-                q_v += [late[i - 1 - AM_LAG]]
-        q_v += late[NU - AM_LAG :]
+                q_v += [late[n_am]]
+                n_am += 1
+        q_v += late[n_am:]
 
         q_s = [("C", "h0_0"), ("C", "m0_0"), ("C", "h0_1"), ("C", "h0_2"), ("C", "h0_3"), ("C", "m0_1")]
         q_s += [("C", "h1_%d" % c) for c in range(4)]
         for k in range(NU + 1):
             if k == 1:
-                q_s += [("C", c) for c in ("m1_0", "m1_1") if c not in V_COPIES]
+                q_s += [("C", c) for c in ("m1_0", "m1_1") if c not in V_COPIES and 1 not in MASK_DMA]
             if k == 3:
                 q_s += [("C", "h2_0"), ("C", "h2_1")]
             if k == 4:
                 q_s += [("C", "h2_2"), ("C", "h2_3")]
             if k == 5:
-                q_s += [("C", c) for c in ("m2_0", "m2_1") if c not in V_COPIES]
+                q_s += [("C", c) for c in ("m2_0", "m2_1") if c not in V_COPIES and 2 not in MASK_DMA]
             if k + SX_LEAD < NU and k + SX_LEAD in SX_ON_S:
                 q_s += [("SX", k + SX_LEAD)]
-            if k < NU:
+            if k < NU and k in G_UNITS:
+                q_s += [("NM", k)]
+                if k > 0:
+                    q_s += [("D", k - 1, 0)]
+                q_s += [("SQ", k)]
+            if k < NU and k not in G_UNITS:
                 q_s += [("NM", k), ("SQ", k)]
-            if k > 0:
+            if k > 0 and k not in G_UNITS:
                 q_s += [("D", k - 1, 0)]
             if k < NU:
                 q_s += [("IS", k)]
@@ -428,7 +460,8 @@ def tile_transformerencoderblock_pa_kernel(tc, h_attn, x, masks, Wo, bo, out_0, 
 
         rotate([nm for nm in q_pe if in_acc(nm)], psum_reader, 4)
         rotate([nm for nm in q_pe if not in_acc(nm)], psum_reader, 4)
-        rotate([("U", i, 0) for i in range(NU)], lambda nm: [("YV", nm[1])], 5)
+        rotate([("U", i, 0) for i in range(NU)],
+               lambda nm: [("YG", nm[1], 0), ("YG", nm[1], 1)] if nm[1] in G_UNITS else [("YV", nm[1])], 5)
         rotate([("YG", i, 0) if i in G_UNITS else ("YV", i) for i in range(NU)],
                lambda nm: [("SQ", nm[1]), ("D", nm[1], 0), ("D", nm[1], 1)], 6)
         rotate([("C", "h%d_%d" % (n, c)) for n in range(NSEQ) for c in (0, 2)],

@@ -21,14 +21,19 @@ HALF = 512
 EPS = 1e-5
 FLOPS = 2 * NSEQ * T * C * E
 
-G_UNITS = (5, 9)
-SX_ON_S = (5, 9)
+G_UNITS = (5, 7, 9, 11)
+SX_ON_S = (5, 7, 9, 11)
 D_ON_V = ()
 V_COPIES = ("w0", "w1")
 AM_LAG = 4
 MASK_DMA = (1, 2)
+FOLD = (5, 7, 9)
+D_ON_G = (3, 5, 7, 9)
+DG_LAG = 2
+Q2_AT = 7
+FX_LEAD = 1
 PIECES = (((0, 256), (256, 256), (512, 512)), ((0, 512), (512, 512)), ((0, 512), (512, 512)))
-SX_LEAD = 4
+SX_LEAD = 2
 
 
 def tile_transformerencoderblock_pa_kernel(tc, h_attn, x, masks, Wo, bo, out_0, out_1):
@@ -156,6 +161,20 @@ def tile_transformerencoderblock_pa_kernel(tc, h_attn, x, masks, Wo, bo, out_0, 
                 in_=hg[(n, half)][:, 4 * a : 4 * (a + w)],
             )
 
+        ident_bf = keep.tile([P, P], BF16, name="ident_bf")
+        folds = {}
+
+        def fold_x(i):
+            folds[i] = ps_t.tile([P, P], F32, tag="tp", name="fold%d" % i)
+            for b in range(T // P):
+                nc.tensor.matmul(
+                    out=folds[i][:], lhsT=ident_bf[:], rhs=xs[i][:, b * P : (b + 1) * P], start=(b == 0), stop=(b == T // P - 1)
+                )
+
+        def sum_fold(i):
+            jf = work.tile([P, P], F32, tag="jf", name="jf%d" % i)
+            nc.scalar.activation(out=jf[:], in_=folds[i][:], func=ACT.Copy, accum_out=sums[:, i, 2:3])
+
         def sum_x(i):
             if i in SX_ON_S:
                 jx = work.tile([P, T], BF16, tag="jxS", name="jx%d" % i)
@@ -247,7 +266,12 @@ def tile_transformerencoderblock_pa_kernel(tc, h_attn, x, masks, Wo, bo, out_0, 
             if i not in o0:
                 o0[i] = keep.tile([P, T], F32, name="o0_%d" % i)
             cols = slice(k * HALF, (k + 1) * HALF)
-            if i in D_ON_V:
+            if i in D_ON_G and k == 1:
+                nc.gpsimd.tensor_scalar(
+                    out=o0[i][:, cols], in0=ys[i][:, cols], scalar1=rstd[:, col], scalar2=nbias[:, col],
+                    op0=ALU.mult, op1=ALU.add,
+                )
+            elif i in D_ON_V:
                 nc.vector.tensor_scalar(
                     out=o0[i][:, cols], in0=ys[i][:, cols], scalar1=rstd[:, col], scalar2=nbias[:, col],
                     op0=ALU.mult, op1=ALU.add,
@@ -303,6 +327,7 @@ def tile_transformerencoderblock_pa_kernel(tc, h_attn, x, masks, Wo, bo, out_0, 
         nc.vector.memset(mrow[2][:], 0.0)
         nc.scalar.activation(out=warm[:], in_=eps_t[:], func=ACT.Abs_reciprocal_sqrt)
         make_identity(nc, ident[:])
+        make_identity(nc, ident_bf[:])
         nc.gpsimd.memset(ones[:], 1.0)
         load_w(0)
         load_h(0, 0)
@@ -331,6 +356,9 @@ def tile_transformerencoderblock_pa_kernel(tc, h_attn, x, masks, Wo, bo, out_0, 
         def rotate(makers, readers_of, bufs):
             for m in range(bufs, len(makers)):
                 ops[makers[m]][2].extend(readers_of(makers[m - bufs]))
+
+        def d_ops(i):
+            return [("D", i, 0), ("D", i, 1)]
 
         def eng_of(key):
             return "V" if key in V_COPIES else "S"
@@ -365,15 +393,19 @@ def tile_transformerencoderblock_pa_kernel(tc, h_attn, x, masks, Wo, bo, out_0, 
                 op(("D", i, half), normalise, (i, half), (("NB", i),))
                 op(("YG", i, half), add_g, (i, half), (("U", i, half),))
             op(("YV", i), add_v, (i,), [("U", i, pc) for pc in range(len(PIECES[n]))])
-            op(("SX", i), sum_x, (i,), ())
+            op(("FX", i), fold_x, (i,), ())
+            if i in FOLD:
+                op(("SX", i), sum_fold, (i,), (("FX", i),))
+            else:
+                op(("SX", i), sum_x, (i,), ())
             made = (("YG", i, 0), ("YG", i, 1), ("SX", i)) if i in G_UNITS else (("YV", i),)
             op(("NM", i), neg_mean, (i,), made)
             op(("SQ", i), squares, (i,), made + ((("NM", i),) if i in G_UNITS else ()))
             op(("IS", i), inv_std, (i,), (("SQ", i),))
             op(("NB", i), neg_bias, (i,), (("IS", i), ("NM", i)))
-            op(("ST", i), store_0, (i,), (("D", i, 0), ("D", i, 1)))
+            op(("ST", i), store_0, (i,), d_ops(i))
             if i < NU - 1:
-                op(("AM", i), row_amax, (i, 0, T, i), (("D", i, 0), ("D", i, 1)))
+                op(("AM", i), row_amax, (i, 0, T, i), d_ops(i))
         op(("AM", NU - 1, 0), row_amax, (NU - 1, 0, HALF, NU - 1), (("D", NU - 1, 0),))
         op(("AM", NU - 1, 1), row_amax, (NU - 1, HALF, T, NU), (("D", NU - 1, 1),))
 
@@ -382,9 +414,12 @@ def tile_transformerencoderblock_pa_kernel(tc, h_attn, x, masks, Wo, bo, out_0, 
         q_pe += [("P", j, 1) for j in range(NJ)] + [("P", j, 2) for j in range(NJ)] + [("T", "h1_%d" % c) for c in range(4)] + [("MM", 1, half) for half in range(2) if 1 not in MASK_DMA]
         q_pe += [("P", 4, 0), ("P", 4, 1), ("T", "h2_0"), ("T", "h2_1"), ("P", 5, 0), ("P", 5, 1), ("T", "h2_2"), ("T", "h2_3")]
         q_pe += [("P", 6, 0), ("P", 6, 1)] + [("MM", 2, half) for half in range(2) if 2 not in MASK_DMA] + [("P", i, half) for i in range(7, NU) for half in range(2)]
+        for i in FOLD:
+            q_pe.insert(q_pe.index(("P", i - FX_LEAD, 1)) + 1, ("FX", i))
 
         q_g = [nm for nm in [("YG", 0, 0), ("YG", 1, 0), ("YG", 2, 0), ("YG", 0, 1), ("YG", 1, 1), ("YG", 2, 1), ("YG", 3, 0), ("YG", 3, 1)] if nm[1] in G_UNITS]
-        q_g += [("YG", i, half) for i in G_UNITS if i >= NJ for half in range(2)]
+        for i in G_UNITS:
+            q_g += [("YG", i, 0), ("YG", i, 1)] + ([("D", i - DG_LAG, 1)] if i - DG_LAG in D_ON_G else [])
 
         def v_add(i):
             if i in G_UNITS:
@@ -396,19 +431,17 @@ def tile_transformerencoderblock_pa_kernel(tc, h_attn, x, masks, Wo, bo, out_0, 
         q_v += [("C", k) for k in ("m1_0", "m1_1") if k in V_COPIES]
         late = []
         for i in range(NU):
-            if i in D_ON_V:
-                late += [("D", i, 0), ("D", i, 1)]
+            if i + 1 in D_ON_V:
+                late += [("D", i + 1, 0), ("D", i + 1, 1)]
             late += [("AM", i)] if i < NU - 1 else [("AM", i, 0), ("AM", i, 1)]
         n_am = 0
         for i in range(NJ, NU + 1):
             if i in G_UNITS:
                 q_v += v_add(i - 1)
+            if i == Q2_AT:
+                q_v += [("Q", 2, 0), ("Q", 2, 1)]
             if i < NU:
                 q_v += [("U", i, 0), ("U", i, 1)]
-            if i == 6:
-                q_v += [("Q", 2, 0)]
-            if i == 7:
-                q_v += [("Q", 2, 1)]
             if i not in G_UNITS:
                 q_v += v_add(i - 1)
             if i - 1 - AM_LAG >= 0:
@@ -431,16 +464,16 @@ def tile_transformerencoderblock_pa_kernel(tc, h_attn, x, masks, Wo, bo, out_0, 
                 q_s += [("SX", k + SX_LEAD)]
             if k < NU and k in G_UNITS:
                 q_s += [("NM", k)]
-                if k > 0:
+                if k > 0 and k - 1 not in D_ON_V:
                     q_s += [("D", k - 1, 0)]
                 q_s += [("SQ", k)]
             if k < NU and k not in G_UNITS:
                 q_s += [("NM", k), ("SQ", k)]
-            if k > 0 and k not in G_UNITS:
+            if k > 0 and k not in G_UNITS and k - 1 not in D_ON_V:
                 q_s += [("D", k - 1, 0)]
             if k < NU:
                 q_s += [("IS", k)]
-            if k > 0:
+            if k > 0 and k - 1 not in D_ON_V + D_ON_G:
                 q_s += [("D", k - 1, 1)]
             if k < NU:
                 q_s += [("NB", k)]
@@ -453,6 +486,8 @@ def tile_transformerencoderblock_pa_kernel(tc, h_attn, x, masks, Wo, bo, out_0, 
                 return [("C", "m%d_%d" % (nm[1], nm[2]))]
             if nm[0] == "P":
                 return [("U", nm[1], nm[2])]
+            if nm[0] == "FX":
+                return [("SX", nm[1])]
             return []
 
         def in_acc(nm):
@@ -463,7 +498,7 @@ def tile_transformerencoderblock_pa_kernel(tc, h_attn, x, masks, Wo, bo, out_0, 
         rotate([("U", i, 0) for i in range(NU)],
                lambda nm: [("YG", nm[1], 0), ("YG", nm[1], 1)] if nm[1] in G_UNITS else [("YV", nm[1])], 5)
         rotate([("YG", i, 0) if i in G_UNITS else ("YV", i) for i in range(NU)],
-               lambda nm: [("SQ", nm[1]), ("D", nm[1], 0), ("D", nm[1], 1)], 6)
+               lambda nm: [("SQ", nm[1])] + d_ops(nm[1]), 6)
         rotate([("C", "h%d_%d" % (n, c)) for n in range(NSEQ) for c in (0, 2)],
                lambda nm: [("Q", int(nm[1][1]), pc) for pc in range(len(PIECES[int(nm[1][1])]))], 3)
 

@@ -21,8 +21,8 @@ HALF = 512
 EPS = 1e-5
 FLOPS = 2 * NSEQ * T * C * E
 
-G_UNITS = (5, 7, 9, 11)
-SX_ON_S = (5, 7, 9, 11)
+G_UNITS = (3, 5, 7, 9, 11)
+SX_ON_S = (3, 5, 7, 9)
 D_ON_V = ()
 V_COPIES = ("w0", "w1")
 AM_LAG = 4
@@ -31,7 +31,7 @@ FOLD = (5, 7, 9)
 D_ON_G = (3, 5, 7, 9)
 DG_LAG = 2
 Q2_AT = 7
-FX_LEAD = 1
+FX_LEAD = 0
 PIECES = (((0, 256), (256, 256), (512, 512)), ((0, 512), (512, 512)), ((0, 512), (512, 512)))
 SX_LEAD = 2
 
@@ -173,17 +173,17 @@ def tile_transformerencoderblock_pa_kernel(tc, h_attn, x, masks, Wo, bo, out_0, 
 
         def sum_fold(i):
             jf = work.tile([P, P], F32, tag="jf", name="jf%d" % i)
-            nc.scalar.activation(out=jf[:], in_=folds[i][:], func=ACT.Copy, accum_out=sums[:, i, 2:3])
+            nc.scalar.activation(out=jf[:], in_=folds[i][:], func=ACT.Copy, accum_out=sums[:, i, len(PIECES[i // NJ]) : len(PIECES[i // NJ]) + 1])
 
         def sum_x(i):
             if i in SX_ON_S:
                 jx = work.tile([P, T], BF16, tag="jxS", name="jx%d" % i)
-                nc.scalar.activation(out=jx[:], in_=xs[i][:], func=ACT.Copy, accum_out=sums[:, i, 2:3])
+                nc.scalar.activation(out=jx[:], in_=xs[i][:], func=ACT.Copy, accum_out=sums[:, i, len(PIECES[i // NJ]) : len(PIECES[i // NJ]) + 1])
             else:
                 jx = work.tile([P, T], BF16, tag="jxV", name="jx%d" % i)
                 nc.vector.tensor_scalar(
                     out=jx[:], in0=xs[i][:], scalar1=1.0, scalar2=None, op0=ALU.mult, op1=ALU.add,
-                    accum_out=sums[:, i, 2:3],
+                    accum_out=sums[:, i, len(PIECES[i // NJ]) : len(PIECES[i // NJ]) + 1],
                 )
 
         def project(i, pc):
@@ -232,8 +232,10 @@ def tile_transformerencoderblock_pa_kernel(tc, h_attn, x, masks, Wo, bo, out_0, 
 
         def neg_mean(i):
             if i in G_UNITS:
+                parts = len(PIECES[i // NJ]) + 1
                 nc.scalar.activation(
-                    out=junk3[:, i, 0:3], in_=sums[:, i, 0:3], func=ACT.Copy, scale=-1.0 / T, accum_out=negmean[:, i : i + 1]
+                    out=junk3[:, i, 0:parts], in_=sums[:, i, 0:parts], func=ACT.Copy, scale=-1.0 / T,
+                    accum_out=negmean[:, i : i + 1],
                 )
             else:
                 nc.scalar.activation(out=negmean[:, i : i + 1], in_=sums[:, i, 0:1], func=ACT.Copy, scale=-1.0 / T)
@@ -263,8 +265,6 @@ def tile_transformerencoderblock_pa_kernel(tc, h_attn, x, masks, Wo, bo, out_0, 
 
         def normalise(i, k):
             col = slice(i, i + 1)
-            if i not in o0:
-                o0[i] = keep.tile([P, T], F32, name="o0_%d" % i)
             cols = slice(k * HALF, (k + 1) * HALF)
             if i in D_ON_G and k == 1:
                 nc.gpsimd.tensor_scalar(
@@ -281,27 +281,36 @@ def tile_transformerencoderblock_pa_kernel(tc, h_attn, x, masks, Wo, bo, out_0, 
                     out=o0[i][:, cols], in_=ys[i][:, cols], func=ACT.Identity, bias=nbias[:, col], scale=rstd[:, col]
                 )
 
+        for i in range(NU - 1):
+            o0[i] = keep.tile([P, T], F32, name="o0_%d" % i)
+        o0[NU - 1] = keep.tile([P, T + NU], F32, name="o0_%d" % (NU - 1))
+        am1 = keep.tile([P, 1], F32, name="am1")
+
         def store_0(i):
             n, j = divmod(i, NJ)
-            nc.sync.dma_start(out=out_0[n].rearrange("(p j) t -> p j t", j=NJ)[:, j, :], in_=o0[i][:])
+            nc.sync.dma_start(out=out_0[n].rearrange("(p j) t -> p j t", j=NJ)[:, j, :], in_=o0[i][:, 0:T])
 
         def row_amax(i, c0, c1, col):
-            nc.vector.tensor_reduce(
-                out=amx[:, col : col + 1], in_=o0[i][:, c0:c1], axis=AX.X, op=ALU.max, apply_absolute_value=True
-            )
+            if col == NU:
+                nc.vector.tensor_reduce(
+                    out=am1[:], in_=o0[i][:, c0 : T + NU], axis=AX.X, op=ALU.max, apply_absolute_value=True
+                )
+            else:
+                nc.vector.tensor_reduce(
+                    out=o0[NU - 1][:, T + col : T + col + 1], in_=o0[i][:, c0:c1], axis=AX.X, op=ALU.max,
+                    apply_absolute_value=True,
+                )
 
         r448 = keep.tile([P, 1], F32, name="r448")
 
         def one_amax():
-            am1 = keep.tile([P, 1], F32, name="am1")
-            amxs = keep.tile([P, NU + 1], F32, name="amxs")
-            nc.vector.tensor_scalar(
-                out=amxs[:], in0=amx[:], scalar1=1.0 / 448.0, scalar2=None, op0=ALU.mult, op1=ALU.max, accum_out=am1[:]
-            )
             pt = ps_t.tile([P, P], F32, tag="tp", name="pt")
             nc.tensor.transpose(pt[:], am1[:, 0:1].to_broadcast([P, P]), ident[:])
             am2 = keep.tile([P, 1], F32, name="am2")
-            nc.vector.tensor_reduce(out=am2[:], in_=pt[:], axis=AX.X, op=ALU.max)
+            pts = keep.tile([P, P], F32, name="pts")
+            nc.vector.tensor_scalar(
+                out=pts[:], in0=pt[:], scalar1=1.0 / 448.0, scalar2=None, op0=ALU.mult, op1=ALU.max, accum_out=am2[:]
+            )
             nc.vector.reciprocal(out=r448[:], in_=am2[:])
 
         def cast(i, eng):
@@ -309,11 +318,11 @@ def tile_transformerencoderblock_pa_kernel(tc, h_attn, x, masks, Wo, bo, out_0, 
             f8 = keep.tile([P, T], FP8, name="f8_%d" % i)
             if eng == "S":
                 nc.scalar.activation(
-                    out=f8[:], in_=o0[i][:], func=ACT.Identity, scale=r448[:, 0:1], bias=zero_t[:, 0:1], saturate=False
+                    out=f8[:], in_=o0[i][:, 0:T], func=ACT.Identity, scale=r448[:, 0:1], bias=zero_t[:, 0:1], saturate=False
                 )
             else:
                 nc.vector.tensor_scalar(
-                    out=f8[:], in0=o0[i][:], scalar1=r448[:, 0:1], scalar2=None, op0=ALU.mult, saturate=False
+                    out=f8[:], in0=o0[i][:, 0:T], scalar1=r448[:, 0:1], scalar2=None, op0=ALU.mult, saturate=False
                 )
             nc.sync.dma_start(
                 out=out_1[n].rearrange("(p j) t -> p j t", j=NJ)[:, j, :], in_=f8[:].bitcast(U8)
@@ -331,7 +340,10 @@ def tile_transformerencoderblock_pa_kernel(tc, h_attn, x, masks, Wo, bo, out_0, 
         nc.gpsimd.memset(ones[:], 1.0)
         load_w(0)
         load_h(0, 0)
-        load_mask(0)
+        if 0 in MASK_DMA:
+            load_mask_spread(0)
+        else:
+            load_mask(0)
         nc.sync.dma_start(out=bo_bf[:], in_=bo.rearrange("(p j) -> p j", j=NJ))
         load_w(1)
         load_h(0, 1)
@@ -391,7 +403,8 @@ def tile_transformerencoderblock_pa_kernel(tc, h_attn, x, masks, Wo, bo, out_0, 
                 op(("U", i, pc), bias_mask, (i, pc), [("P", i, pc), ("BO",)] + ([] if n in MASK_DMA else [("C", "m%d_%d" % (n, PIECES[n][pc][0] // HALF))]))
             for half in range(2):
                 op(("D", i, half), normalise, (i, half), (("NB", i),))
-                op(("YG", i, half), add_g, (i, half), (("U", i, half),))
+                op(("YG", i, half), add_g, (i, half),
+                   [("U", i, pc) for pc in range(len(PIECES[n])) if PIECES[n][pc][0] // HALF == half])
             op(("YV", i), add_v, (i,), [("U", i, pc) for pc in range(len(PIECES[n]))])
             op(("FX", i), fold_x, (i,), ())
             if i in FOLD:
@@ -407,17 +420,20 @@ def tile_transformerencoderblock_pa_kernel(tc, h_attn, x, masks, Wo, bo, out_0, 
             if i < NU - 1:
                 op(("AM", i), row_amax, (i, 0, T, i), d_ops(i))
         op(("AM", NU - 1, 0), row_amax, (NU - 1, 0, HALF, NU - 1), (("D", NU - 1, 0),))
-        op(("AM", NU - 1, 1), row_amax, (NU - 1, HALF, T, NU), (("D", NU - 1, 1),))
+        op(("AM", NU - 1, 1), row_amax, (NU - 1, HALF, T, NU), [("D", NU - 1, 1), ("AM", NU - 1, 0)] + [("AM", i) for i in range(NU - 1)])
 
         q_pe = [("WARM", 0), ("WARM", 1), ("T", "w0"), ("T", "h0_0"), ("MM", 0, 0), ("T", "w1"), ("T", "h0_1"),
                 ("P", 0, 0), ("P", 1, 0), ("T", "h0_2"), ("P", 2, 0), ("P", 3, 0), ("T", "h0_3"), ("MM", 0, 1)]
-        q_pe += [("P", j, 1) for j in range(NJ)] + [("P", j, 2) for j in range(NJ)] + [("T", "h1_%d" % c) for c in range(4)] + [("MM", 1, half) for half in range(2) if 1 not in MASK_DMA]
-        q_pe += [("P", 4, 0), ("P", 4, 1), ("T", "h2_0"), ("T", "h2_1"), ("P", 5, 0), ("P", 5, 1), ("T", "h2_2"), ("T", "h2_3")]
-        q_pe += [("P", 6, 0), ("P", 6, 1)] + [("MM", 2, half) for half in range(2) if 2 not in MASK_DMA] + [("P", i, half) for i in range(7, NU) for half in range(2)]
+        if 0 in MASK_DMA:
+            q_pe.remove(("MM", 0, 0))
+            q_pe.remove(("MM", 0, 1))
+        q_pe += [("P", j, 1) for j in (3, 0, 1, 2)] + [("P", j, 2) for j in (3, 0, 1, 2)] + [("T", "h1_%d" % c) for c in range(4)] + [("MM", 1, half) for half in range(2) if 1 not in MASK_DMA]
+        q_pe += [("P", 4, 0), ("P", 4, 1), ("T", "h2_0"), ("T", "h2_1"), ("P", 5, 0), ("P", 5, 1), ("T", "h2_2")]
+        q_pe += [("P", 6, 0), ("P", 6, 1), ("T", "h2_3")] + [("MM", 2, half) for half in range(2) if 2 not in MASK_DMA] + [("P", i, half) for i in range(7, NU) for half in range(2)]
         for i in FOLD:
             q_pe.insert(q_pe.index(("P", i - FX_LEAD, 1)) + 1, ("FX", i))
 
-        q_g = [nm for nm in [("YG", 0, 0), ("YG", 1, 0), ("YG", 2, 0), ("YG", 0, 1), ("YG", 1, 1), ("YG", 2, 1), ("YG", 3, 0), ("YG", 3, 1)] if nm[1] in G_UNITS]
+        q_g = []
         for i in G_UNITS:
             q_g += [("YG", i, 0), ("YG", i, 1)] + ([("D", i - DG_LAG, 1)] if i - DG_LAG in D_ON_G else [])
 
@@ -427,7 +443,7 @@ def tile_transformerencoderblock_pa_kernel(tc, h_attn, x, masks, Wo, bo, out_0, 
             return [("YV", i)]
 
         q_v = [("C", "w0"), ("QW", 0), ("BO",), ("Q", 0, 0), ("C", "w1"), ("QW", 1)] + [("U", j, 0) for j in range(NJ)] + [("Q", 0, 1), ("Q", 0, 2)]
-        q_v += [("U", j, 1) for j in range(NJ)] + [("U", j, 2) for j in range(NJ)] + v_add(0) + [("Q", 1, 0)] + v_add(1) + [("Q", 1, 1)] + v_add(2)
+        q_v += [("U", j, 1) for j in (3, 0, 1, 2)] + [("U", j, 2) for j in (3, 0, 1, 2)] + v_add(0) + [("Q", 1, 0)] + v_add(1) + [("Q", 1, 1)] + v_add(2)
         q_v += [("C", k) for k in ("m1_0", "m1_1") if k in V_COPIES]
         late = []
         for i in range(NU):
@@ -450,7 +466,10 @@ def tile_transformerencoderblock_pa_kernel(tc, h_attn, x, masks, Wo, bo, out_0, 
         q_v += late[n_am:]
 
         q_s = [("C", "h0_0"), ("C", "m0_0"), ("C", "h0_1"), ("C", "h0_2"), ("C", "h0_3"), ("C", "m0_1")]
-        q_s += [("C", "h1_%d" % c) for c in range(4)]
+        if 0 in MASK_DMA:
+            q_s.remove(("C", "m0_0"))
+            q_s.remove(("C", "m0_1"))
+        q_s += [("SX", i) for i in SX_ON_S if i < NJ] + [("C", "h1_%d" % c) for c in range(4)]
         for k in range(NU + 1):
             if k == 1:
                 q_s += [("C", c) for c in ("m1_0", "m1_1") if c not in V_COPIES and 1 not in MASK_DMA]
@@ -460,7 +479,7 @@ def tile_transformerencoderblock_pa_kernel(tc, h_attn, x, masks, Wo, bo, out_0, 
                 q_s += [("C", "h2_2"), ("C", "h2_3")]
             if k == 5:
                 q_s += [("C", c) for c in ("m2_0", "m2_1") if c not in V_COPIES and 2 not in MASK_DMA]
-            if k + SX_LEAD < NU and k + SX_LEAD in SX_ON_S:
+            if NJ <= k + SX_LEAD < NU and k + SX_LEAD in SX_ON_S:
                 q_s += [("SX", k + SX_LEAD)]
             if k < NU and k in G_UNITS:
                 q_s += [("NM", k)]

@@ -22,15 +22,18 @@ EPS = 1e-5
 FLOPS = 2 * NSEQ * T * C * E
 
 G_UNITS = (3, 5, 7, 9, 11)
-SX_ON_S = (3, 5, 7, 9)
+SX_ON_S = (3, 5, 7, 9, 11)
 D_ON_V = ()
 V_COPIES = ("w0", "w1")
 AM_LAG = 4
 MASK_DMA = (1, 2)
-FOLD = (5, 7, 9)
-D_ON_G = (3, 5, 7, 9)
-DG_LAG = 2
+FOLD = (5, 7, 9, 11)
+D_AFTER = {5: (2,), 7: (4,), 9: (6,), 11: (9, 10, 11)}
+D_ON_G = (2, 4, 6, 9, 10, 11)
+DG_LAG = 3
 Q2_AT = 7
+WARMS = 1
+M01_DMA = True
 FX_LEAD = 0
 PIECES = (((0, 256), (256, 256), (512, 512)), ((0, 512), (512, 512)), ((0, 512), (512, 512)))
 SX_LEAD = 2
@@ -106,6 +109,11 @@ def tile_transformerencoderblock_pa_kernel(tc, h_attn, x, masks, Wo, bo, out_0, 
         def load_mask_spread(n):
             mask_sp[n] = keep.tile([P, T], BF16, name="mask_sp%d" % n)
             nc.sync.dma_start(out=mask_sp[n][:], in_=masks[n, 0].partition_broadcast(P))
+
+        mask_0b = keep.tile([P, HALF], BF16, name="mask_0b")
+
+        def load_mask_0b():
+            nc.sync.dma_start(out=mask_0b[:], in_=masks[0, 0, HALF:T].partition_broadcast(P))
 
         def warm_pe():
             jp = ps_a.tile([P, HALF], F32, tag="acc", name="jp")
@@ -202,6 +210,13 @@ def tile_transformerencoderblock_pa_kernel(tc, h_attn, x, masks, Wo, bo, out_0, 
                 stop=True,
             )
 
+        def mask_of(n, c0, w):
+            if n in MASK_DMA:
+                return mask_sp[n][:, c0 : c0 + w]
+            if M01_DMA and c0 >= HALF:
+                return mask_0b[:, c0 - HALF : c0 - HALF + w]
+            return mask_bc[:, n * T + c0 : n * T + c0 + w]
+
         def bias_mask(i, pc):
             n, j = divmod(i, NJ)
             c0, w = PIECES[n][pc]
@@ -211,7 +226,7 @@ def tile_transformerencoderblock_pa_kernel(tc, h_attn, x, masks, Wo, bo, out_0, 
                 out=us[i][:, c0 : c0 + w],
                 in0=accs[(i, pc)][:, 0:w],
                 scalar=bo32[:, j : j + 1],
-                in1=(mask_sp[n][:, c0 : c0 + w] if n in MASK_DMA else mask_bc[:, n * T + c0 : n * T + c0 + w]),
+                in1=mask_of(n, c0, w),
                 op0=ALU.add,
                 op1=ALU.mult,
                 accum_out=(sums[:, i, pc : pc + 1] if i in G_UNITS else None),
@@ -349,6 +364,8 @@ def tile_transformerencoderblock_pa_kernel(tc, h_attn, x, masks, Wo, bo, out_0, 
         load_h(0, 1)
         load_h(0, 2)
         load_h(0, 3)
+        if M01_DMA:
+            load_mask_0b()
         for n in range(NSEQ):
             if n > 0:
                 if n not in MASK_DMA:
@@ -400,7 +417,7 @@ def tile_transformerencoderblock_pa_kernel(tc, h_attn, x, masks, Wo, bo, out_0, 
             n, j = divmod(i, NJ)
             for pc in range(len(PIECES[n])):
                 op(("P", i, pc), project, (i, pc), (("Q", n, pc), ("QW", j // 2)))
-                op(("U", i, pc), bias_mask, (i, pc), [("P", i, pc), ("BO",)] + ([] if n in MASK_DMA else [("C", "m%d_%d" % (n, PIECES[n][pc][0] // HALF))]))
+                op(("U", i, pc), bias_mask, (i, pc), [("P", i, pc), ("BO",)] + ([] if n in MASK_DMA or (M01_DMA and PIECES[n][pc][0] >= HALF) else [("C", "m%d_%d" % (n, PIECES[n][pc][0] // HALF))]))
             for half in range(2):
                 op(("D", i, half), normalise, (i, half), (("NB", i),))
                 op(("YG", i, half), add_g, (i, half),
@@ -424,9 +441,10 @@ def tile_transformerencoderblock_pa_kernel(tc, h_attn, x, masks, Wo, bo, out_0, 
 
         q_pe = [("WARM", 0), ("WARM", 1), ("T", "w0"), ("T", "h0_0"), ("MM", 0, 0), ("T", "w1"), ("T", "h0_1"),
                 ("P", 0, 0), ("P", 1, 0), ("T", "h0_2"), ("P", 2, 0), ("P", 3, 0), ("T", "h0_3"), ("MM", 0, 1)]
-        if 0 in MASK_DMA:
-            q_pe.remove(("MM", 0, 0))
+        if M01_DMA:
             q_pe.remove(("MM", 0, 1))
+        for w in range(WARMS, 2):
+            q_pe.remove(("WARM", w))
         q_pe += [("P", j, 1) for j in (3, 0, 1, 2)] + [("P", j, 2) for j in (3, 0, 1, 2)] + [("T", "h1_%d" % c) for c in range(4)] + [("MM", 1, half) for half in range(2) if 1 not in MASK_DMA]
         q_pe += [("P", 4, 0), ("P", 4, 1), ("T", "h2_0"), ("T", "h2_1"), ("P", 5, 0), ("P", 5, 1), ("T", "h2_2")]
         q_pe += [("P", 6, 0), ("P", 6, 1), ("T", "h2_3")] + [("MM", 2, half) for half in range(2) if 2 not in MASK_DMA] + [("P", i, half) for i in range(7, NU) for half in range(2)]
@@ -435,7 +453,7 @@ def tile_transformerencoderblock_pa_kernel(tc, h_attn, x, masks, Wo, bo, out_0, 
 
         q_g = []
         for i in G_UNITS:
-            q_g += [("YG", i, 0), ("YG", i, 1)] + ([("D", i - DG_LAG, 1)] if i - DG_LAG in D_ON_G else [])
+            q_g += [("YG", i, 0), ("YG", i, 1)] + [("D", d, 1) for d in D_AFTER.get(i, ())]
 
         def v_add(i):
             if i in G_UNITS:
@@ -466,8 +484,7 @@ def tile_transformerencoderblock_pa_kernel(tc, h_attn, x, masks, Wo, bo, out_0, 
         q_v += late[n_am:]
 
         q_s = [("C", "h0_0"), ("C", "m0_0"), ("C", "h0_1"), ("C", "h0_2"), ("C", "h0_3"), ("C", "m0_1")]
-        if 0 in MASK_DMA:
-            q_s.remove(("C", "m0_0"))
+        if M01_DMA:
             q_s.remove(("C", "m0_1"))
         q_s += [("SX", i) for i in SX_ON_S if i < NJ] + [("C", "h1_%d" % c) for c in range(4)]
         for k in range(NU + 1):

@@ -22,18 +22,18 @@ EPS = 1e-5
 FLOPS = 2 * NSEQ * T * C * E
 
 G_UNITS = (3, 5, 7, 9, 11)
-SX_ON_S = (3, 5, 7, 9, 11)
+SX_ON_S = (3, 5, 7, 9)
 D_ON_V = ()
 V_COPIES = ("w0", "w1")
 AM_LAG = 4
 MASK_DMA = (1, 2)
-FOLD = (5, 7, 9, 11)
+FOLD = (5, 7, 9)
 D_AFTER = {5: (2,), 7: (4,), 9: (6,), 11: (9, 10, 11)}
 D_ON_G = (2, 4, 6, 9, 10, 11)
 DG_LAG = 3
 Q2_AT = 7
-WARMS = 1
-M01_DMA = True
+WARMS = 2
+M01_DMA = False
 FX_LEAD = 0
 PIECES = (((0, 256), (256, 256), (512, 512)), ((0, 512), (512, 512)), ((0, 512), (512, 512)))
 SX_LEAD = 2

@@ -18,137 +18,114 @@ P = 128
 NJ = E // P
 NU = NSEQ * NJ
 HALF = 512
+CHUNK = 256
 EPS = 1e-5
 FLOPS = 2 * NSEQ * T * C * E
 
-G_UNITS = (3, 5, 7, 9, 11)
-SX_ON_S = (3, 5, 7, 9)
-D_ON_V = ()
-V_COPIES = ("w0", "w1")
-AM_LAG = 4
-MASK_DMA = (1, 2)
-FOLD = (5, 7, 9)
-D_AFTER = {5: (2,), 7: (4,), 9: (6,), 11: (9, 10, 11)}
-D_ON_G = (2, 4, 6, 9, 10, 11)
-DG_LAG = 3
-Q2_AT = 7
-WARMS = 2
-M01_DMA = False
-FX_LEAD = 0
 PIECES = (((0, 256), (256, 256), (512, 512)), ((0, 512), (512, 512)), ((0, 512), (512, 512)))
-SX_LEAD = 2
+GPSIMD_ADDS = (3, 5, 7, 9, 11)
+GPSIMD_HALVES = {5: (2,), 7: (4,), 9: (6,), 11: (9, 10, 11)}
+HALVES_ON_GPSIMD = (2, 4, 6, 9, 10, 11)
+FOLDED = (5, 7, 9)
+AMAX_BEHIND = 4
+U_BUFS, Y_BUFS, HG_BUFS, BANKS = 5, 6, 3, 4
 
 
 def tile_transformerencoderblock_pa_kernel(tc, h_attn, x, masks, Wo, bo, out_0, out_1):
     nc = tc.nc
     with ExitStack() as ctx:
         keep = ctx.enter_context(tc.tile_pool(name="keep", bufs=1))
-        work = ctx.enter_context(tc.tile_pool(name="work", bufs=3))
-        upool = ctx.enter_context(tc.tile_pool(name="upool", bufs=5))
-        ypool = ctx.enter_context(tc.tile_pool(name="ypool", bufs=6))
-        ps_t = ctx.enter_context(tc.psum_pool(name="ps_t", bufs=4))
-        ps_a = ctx.enter_context(tc.psum_pool(name="ps_a", bufs=4))
+        work = ctx.enter_context(tc.tile_pool(name="work", bufs=HG_BUFS))
+        upool = ctx.enter_context(tc.tile_pool(name="upool", bufs=U_BUFS))
+        ypool = ctx.enter_context(tc.tile_pool(name="ypool", bufs=Y_BUFS))
+        ps_t = ctx.enter_context(tc.psum_pool(name="ps_t", bufs=BANKS))
+        ps_a = ctx.enter_context(tc.psum_pool(name="ps_a", bufs=BANKS))
         ctx.enter_context(tc.manual_schedule())
 
-        mrow = [keep.tile([P, T], BF16, name="mrow%d" % n) for n in range(NSEQ)]
+        mrow = keep.tile([P, T], BF16, name="mrow")
+        mask_0 = keep.tile([P, T], F32, name="mask_0")
+        mask_n = {n: keep.tile([P, T], BF16, name="mask_%d" % n) for n in (1, 2)}
         eps_t = keep.tile([P, 1], F32, name="eps_t")
         zero_t = keep.tile([P, 1], F32, name="zero_t")
         warm = keep.tile([P, 1], F32, name="warm")
         ident = keep.tile([P, P], F32, name="ident")
+        ident_bf = keep.tile([P, P], BF16, name="ident_bf")
         ones = keep.tile([P, P], BF16, name="ones")
-        wraw = [keep.tile([P, 2, C], BF16, name="wraw%d" % b) for b in range(2)]
-        wview = Wo.rearrange("(p j) c -> p j c", j=NJ)
-        raw = {}
-        xs = {}
+        zeros = keep.tile([P, 256], F32, name="zeros")
         bo_bf = keep.tile([P, NJ], BF16, name="bo_bf")
-        mask_bc = keep.tile([P, NSEQ * T], F32, name="mask_bc")
         bo32 = keep.tile([P, NJ], F32, name="bo32")
-        wz = keep.tile([P, 256], F32, name="wz")
+        raw = {}
+        for b in range(2):
+            raw["w%d" % b] = keep.tile([P, 2, C], BF16, name="w%d" % b)
+        for n in range(NSEQ):
+            for c in range(T // CHUNK):
+                raw["h%d_%d" % (n, c)] = keep.tile([P, 2, C], BF16, name="h%d_%d" % (n, c))
+        xs = [keep.tile([P, T], BF16, name="x%d" % i) for i in range(NU)]
         wg = keep.tile([P, 4 * E], BF16, name="wg", align_bytes=64)
         wc = keep.tile([P, E], U32, name="wc", align_bytes=64)
         wsc = keep.tile([P, E], U8, name="wsc", align_bytes=64)
         hg = {}
         hc = {}
         hs = {}
-        tps = {}
-        pms = {}
-        accs = {}
+        for n in range(NSEQ):
+            for half in range(2):
+                hc[(n, half)] = keep.tile([P, HALF], U32, name="hc%d_%d" % (n, half), align_bytes=64)
+                hs[(n, half)] = keep.tile([P, HALF], U8, name="hs%d_%d" % (n, half), align_bytes=64)
+        turned = {}
+        spread = {}
+        prod = {}
+        folds = {}
+        us = {}
+        ys = {}
         sums = keep.tile([P, NU, 4], F32, name="sums")
-        junk3 = keep.tile([P, NU, 4], F32, name="junk3")
+        scaled = keep.tile([P, NU, 4], F32, name="scaled")
         negmean = keep.tile([P, NU], F32, name="negmean")
         ssq = keep.tile([P, NU], F32, name="ssq")
         rstd = keep.tile([P, NU], F32, name="rstd")
         nbias = keep.tile([P, NU], F32, name="nbias")
-        amx = keep.tile([P, NU + 1], F32, name="amx")
-        us = {}
-        ys = {}
-        o0 = {}
-        copies = {"V": nc.vector.tensor_copy, "S": nc.scalar.copy}
+        o0 = [keep.tile([P, T + (NU if i == NU - 1 else 0)], F32, name="o0_%d" % i) for i in range(NU)]
+        row_max = keep.tile([P, 1], F32, name="row_max")
+        inv_scale = keep.tile([P, 1], F32, name="inv_scale")
+
+        def rows_of(dram, i):
+            n, j = divmod(i, NJ)
+            return dram[n].rearrange("(p j) t -> p j t", j=NJ)[:, j, :]
+
 
         def load_w(b):
-            raw["w%d" % b] = wraw[b]
-            nc.sync.dma_start(out=wraw[b][:], in_=wview[:, 2 * b : 2 * b + 2, :])
+            nc.sync.dma_start(out=raw["w%d" % b][:], in_=Wo.rearrange("(p j) c -> p j c", j=NJ)[:, 2 * b : 2 * b + 2, :])
 
         def load_h(n, c):
-            raw["h%d_%d" % (n, c)] = keep.tile([P, 2, C], BF16, name="h%d_%d" % (n, c))
             nc.sync.dma_start(
                 out=raw["h%d_%d" % (n, c)][:],
-                in_=h_attn[n, c * 256 : (c + 1) * 256, :].rearrange("(i p) c -> p i c", p=P),
+                in_=h_attn[n, c * CHUNK : (c + 1) * CHUNK, :].rearrange("(i p) c -> p i c", p=P),
             )
 
         def load_x(i):
-            n, j = divmod(i, NJ)
-            xs[i] = keep.tile([P, T], BF16, name="x%d" % i)
-            nc.sync.dma_start(out=xs[i][:], in_=x[n].rearrange("(p j) t -> p j t", j=NJ)[:, j, :])
+            nc.sync.dma_start(out=xs[i][:], in_=rows_of(x, i))
 
-        def load_mask(n):
-            nc.sync.dma_start(out=mrow[n][0:1, :], in_=masks[n])
-
-        mask_sp = {}
-
-        def load_mask_spread(n):
-            mask_sp[n] = keep.tile([P, T], BF16, name="mask_sp%d" % n)
-            nc.sync.dma_start(out=mask_sp[n][:], in_=masks[n, 0].partition_broadcast(P))
-
-        mask_0b = keep.tile([P, HALF], BF16, name="mask_0b")
-
-        def load_mask_0b():
-            nc.sync.dma_start(out=mask_0b[:], in_=masks[0, 0, HALF:T].partition_broadcast(P))
-
-        def warm_pe():
-            jp = ps_a.tile([P, HALF], F32, tag="acc", name="jp")
-            nc.tensor.matmul(out=jp[:, 0:256], lhsT=wz[:, 0:P], rhs=wz[:], start=True, stop=True)
-
-        def mask_mm(n, half, where):
-            pool = ps_a if where == "acc" else ps_t
-            pms[(n, half)] = pool.tile([P, HALF], F32, tag=where, name="pm%d_%d" % (n, half))
-            nc.tensor.matmul(
-                out=pms[(n, half)][:], lhsT=ones[:], rhs=mrow[n][:, half * HALF : (half + 1) * HALF],
-                start=True, stop=True,
-            )
-
-        def mask_copy(n, half, eng):
-            copies[eng](out=mask_bc[:, n * T + half * HALF : n * T + (half + 1) * HALF], in_=pms[(n, half)][:])
 
         def transposes(key):
             words = raw[key][:].bitcast(F32)
-            tp = ps_t.tile([P, 2, 2, P], F32, tag="tp", name="tp_%s" % key)
+            turned[key] = ps_t.tile([P, 2, 2, P], F32, tag="tp", name="tp_%s" % key)
             for i in range(2):
                 for u in range(2):
-                    nc.tensor.transpose(tp[:, i, u, :], words[:, i, u:256:2], ident[:])
-            tps[key] = tp
+                    nc.tensor.transpose(turned[key][:, i, u, :], words[:, i, u:256:2], ident[:])
 
-        def copy_out(key, eng, dst, part):
-            copies[eng](
+        def copy_out(copy, key, dst, part):
+            copy(
                 out=dst[:].bitcast(F32)[:, part * 512 : (part + 1) * 512].rearrange("p (i t u) -> p i t u", i=2, u=2),
-                in_=tps[key][:].rearrange("p i u t -> p i t u"),
+                in_=turned[key][:].rearrange("p i u t -> p i t u"),
             )
 
-        def copy_out_h(n, c, eng):
-            half, cc = divmod(c, 2)
-            if cc == 0:
+        def copy_out_w(b):
+            copy_out(nc.vector.tensor_copy, "w%d" % b, wg, b)
+
+        def copy_out_h(n, c):
+            half, part = divmod(c, 2)
+            if part == 0:
                 hg[(n, half)] = work.tile([P, 4 * HALF], BF16, tag="hg", name="hg%d_%d" % (n, half), align_bytes=64)
-            copy_out("h%d_%d" % (n, c), eng, hg[(n, half)], cc)
+            copy_out(nc.scalar.copy, "h%d_%d" % (n, c), hg[(n, half)], part)
 
         def quantise_w(b):
             nc.vector.quantize_mx(
@@ -158,19 +135,27 @@ def tile_transformerencoderblock_pa_kernel(tc, h_attn, x, masks, Wo, bo, out_0, 
             )
 
         def quantise(n, pc):
-            c0, w = PIECES[n][pc]
-            half = c0 // HALF
-            if (n, half) not in hc:
-                hc[(n, half)] = keep.tile([P, HALF], U32, name="hc%d_%d" % (n, half), align_bytes=64)
-                hs[(n, half)] = keep.tile([P, HALF], U8, name="hs%d_%d" % (n, half), align_bytes=64)
-            a = c0 - half * HALF
+            first, frames = PIECES[n][pc]
+            half, a = divmod(first, HALF)
             nc.vector.quantize_mx(
-                out=hc[(n, half)][:, a : a + w].bitcast(FP8X4), scales=hs[(n, half)][:, a : a + w],
-                in_=hg[(n, half)][:, 4 * a : 4 * (a + w)],
+                out=hc[(n, half)][:, a : a + frames].bitcast(FP8X4),
+                scales=hs[(n, half)][:, a : a + frames],
+                in_=hg[(n, half)][:, 4 * a : 4 * (a + frames)],
             )
 
-        ident_bf = keep.tile([P, P], BF16, name="ident_bf")
-        folds = {}
+
+        def dummy_matmul():
+            idle = ps_a.tile([P, HALF], F32, tag="acc", name="idle")
+            nc.tensor.matmul(out=idle[:, 0:256], lhsT=zeros[:, 0:P], rhs=zeros[:], start=True, stop=True)
+
+        def spread_mask(half):
+            spread[half] = ps_a.tile([P, HALF], F32, tag="acc", name="spread%d" % half)
+            nc.tensor.matmul(
+                out=spread[half][:], lhsT=ones[:], rhs=mrow[:, half * HALF : (half + 1) * HALF], start=True, stop=True
+            )
+
+        def copy_mask(half):
+            nc.scalar.copy(out=mask_0[:, half * HALF : (half + 1) * HALF], in_=spread[half][:])
 
         def fold_x(i):
             folds[i] = ps_t.tile([P, P], F32, tag="tp", name="fold%d" % i)
@@ -179,77 +164,78 @@ def tile_transformerencoderblock_pa_kernel(tc, h_attn, x, masks, Wo, bo, out_0, 
                     out=folds[i][:], lhsT=ident_bf[:], rhs=xs[i][:, b * P : (b + 1) * P], start=(b == 0), stop=(b == T // P - 1)
                 )
 
-        def sum_fold(i):
-            jf = work.tile([P, P], F32, tag="jf", name="jf%d" % i)
-            nc.scalar.activation(out=jf[:], in_=folds[i][:], func=ACT.Copy, accum_out=sums[:, i, len(PIECES[i // NJ]) : len(PIECES[i // NJ]) + 1])
 
-        def sum_x(i):
-            if i in SX_ON_S:
-                jx = work.tile([P, T], BF16, tag="jxS", name="jx%d" % i)
-                nc.scalar.activation(out=jx[:], in_=xs[i][:], func=ACT.Copy, accum_out=sums[:, i, len(PIECES[i // NJ]) : len(PIECES[i // NJ]) + 1])
-            else:
-                jx = work.tile([P, T], BF16, tag="jxV", name="jx%d" % i)
-                nc.vector.tensor_scalar(
-                    out=jx[:], in0=xs[i][:], scalar1=1.0, scalar2=None, op0=ALU.mult, op1=ALU.add,
-                    accum_out=sums[:, i, len(PIECES[i // NJ]) : len(PIECES[i // NJ]) + 1],
-                )
+        def widen_bo():
+            nc.vector.tensor_copy(out=bo32[:], in_=bo_bf[:])
 
         def project(i, pc):
             n, j = divmod(i, NJ)
-            c0, w = PIECES[n][pc]
-            half = c0 // HALF
-            a = c0 - half * HALF
-            accs[(i, pc)] = ps_a.tile([P, HALF], F32, tag="acc", name="acc%d_%d" % (i, pc))
+            first, frames = PIECES[n][pc]
+            half, a = divmod(first, HALF)
+            prod[(i, pc)] = ps_a.tile([P, HALF], F32, tag="acc", name="prod%d_%d" % (i, pc))
             nc.tensor.matmul_mx(
-                out=accs[(i, pc)][:, 0:w],
+                out=prod[(i, pc)][:, 0:frames],
                 lhsT=wc[:, j * P : (j + 1) * P].bitcast(FP8X4),
                 lhsT_scale=wsc[:, j * P : (j + 1) * P],
-                rhs=hc[(n, half)][:, a : a + w].bitcast(FP8X4),
-                rhs_scale=hs[(n, half)][:, a : a + w],
+                rhs=hc[(n, half)][:, a : a + frames].bitcast(FP8X4),
+                rhs_scale=hs[(n, half)][:, a : a + frames],
                 start=True,
                 stop=True,
             )
 
-        def mask_of(n, c0, w):
-            if n in MASK_DMA:
-                return mask_sp[n][:, c0 : c0 + w]
-            if M01_DMA and c0 >= HALF:
-                return mask_0b[:, c0 - HALF : c0 - HALF + w]
-            return mask_bc[:, n * T + c0 : n * T + c0 + w]
-
         def bias_mask(i, pc):
             n, j = divmod(i, NJ)
-            c0, w = PIECES[n][pc]
-            if i not in us:
+            first, frames = PIECES[n][pc]
+            if pc == 0:
                 us[i] = upool.tile([P, T], F32, tag="u", name="u%d" % i)
+            mask = mask_0 if n == 0 else mask_n[n]
             nc.vector.scalar_tensor_tensor(
-                out=us[i][:, c0 : c0 + w],
-                in0=accs[(i, pc)][:, 0:w],
+                out=us[i][:, first : first + frames],
+                in0=prod[(i, pc)][:, 0:frames],
                 scalar=bo32[:, j : j + 1],
-                in1=mask_of(n, c0, w),
+                in1=mask[:, first : first + frames],
                 op0=ALU.add,
                 op1=ALU.mult,
-                accum_out=(sums[:, i, pc : pc + 1] if i in G_UNITS else None),
+                accum_out=(sums[:, i, pc : pc + 1] if i in GPSIMD_ADDS else None),
             )
 
-        def add_g(i, half):
-            if i not in ys:
+        def add_on_gpsimd(i, half):
+            if half == 0:
                 ys[i] = ypool.tile([P, T], F32, tag="y", name="y%d" % i)
             cols = slice(half * HALF, (half + 1) * HALF)
             nc.gpsimd.tensor_tensor(out=ys[i][:, cols], in0=us[i][:, cols], in1=xs[i][:, cols], op=ALU.add)
 
-        def add_v(i):
+        def add_on_vector(i):
             ys[i] = ypool.tile([P, T], F32, tag="y", name="y%d" % i)
             nc.vector.scalar_tensor_tensor(
                 out=ys[i][:], in0=us[i][:], scalar=1.0, in1=xs[i][:], op0=ALU.mult, op1=ALU.add,
                 accum_out=sums[:, i, 0:1],
             )
 
+        def sum_x_column(i):
+            pieces = len(PIECES[i // NJ])
+            return sums[:, i, pieces : pieces + 1]
+
+        def sum_x_scalar(i):
+            unused = work.tile([P, T], BF16, tag="sx_s", name="sx%d" % i)
+            nc.scalar.activation(out=unused[:], in_=xs[i][:], func=ACT.Copy, accum_out=sum_x_column(i))
+
+        def sum_x_vector(i):
+            unused = work.tile([P, T], BF16, tag="sx_v", name="sx%d" % i)
+            nc.vector.tensor_scalar(
+                out=unused[:], in0=xs[i][:], scalar1=1.0, scalar2=None, op0=ALU.mult, op1=ALU.add,
+                accum_out=sum_x_column(i),
+            )
+
+        def sum_fold(i):
+            unused = work.tile([P, P], F32, tag="sx_f", name="sx%d" % i)
+            nc.scalar.activation(out=unused[:], in_=folds[i][:], func=ACT.Copy, accum_out=sum_x_column(i))
+
         def neg_mean(i):
-            if i in G_UNITS:
+            if i in GPSIMD_ADDS:
                 parts = len(PIECES[i // NJ]) + 1
                 nc.scalar.activation(
-                    out=junk3[:, i, 0:parts], in_=sums[:, i, 0:parts], func=ACT.Copy, scale=-1.0 / T,
+                    out=scaled[:, i, 0:parts], in_=sums[:, i, 0:parts], func=ACT.Copy, scale=-1.0 / T,
                     accum_out=negmean[:, i : i + 1],
                 )
             else:
@@ -257,37 +243,32 @@ def tile_transformerencoderblock_pa_kernel(tc, h_attn, x, masks, Wo, bo, out_0, 
 
         def squares(i):
             col = slice(i, i + 1)
-            sq = work.tile([P, T], BF16, tag="sq", name="sq%d" % i)
-            if i in G_UNITS:
+            unused = work.tile([P, T], BF16, tag="sq", name="sq%d" % i)
+            if i in GPSIMD_ADDS:
                 nc.scalar.activation(
-                    out=sq[:], in_=ys[i][:], func=ACT.Square, bias=negmean[:, col], scale=1.0, accum_out=ssq[:, col]
+                    out=unused[:], in_=ys[i][:], func=ACT.Square, bias=negmean[:, col], scale=1.0, accum_out=ssq[:, col]
                 )
             else:
                 nc.scalar.activation(
-                    out=sq[:], in_=ys[i][:], func=ACT.Square, bias=sums[:, i, 0:1], scale=-1.0 * T, accum_out=ssq[:, col]
+                    out=unused[:], in_=ys[i][:], func=ACT.Square, bias=sums[:, i, 0:1], scale=-1.0 * T, accum_out=ssq[:, col]
                 )
 
         def inv_std(i):
             col = slice(i, i + 1)
             nc.scalar.activation(
                 out=rstd[:, col], in_=ssq[:, col], func=ACT.Abs_reciprocal_sqrt, bias=eps_t[:, 0:1],
-                scale=(1.0 / T if i in G_UNITS else 1.0 / (T * T * T)),
+                scale=(1.0 / T if i in GPSIMD_ADDS else 1.0 / (T * T * T)),
             )
 
         def neg_bias(i):
             col = slice(i, i + 1)
             nc.scalar.activation(out=nbias[:, col], in_=negmean[:, col], func=ACT.Copy, scale=rstd[:, col])
 
-        def normalise(i, k):
+        def normalise(i, half):
             col = slice(i, i + 1)
-            cols = slice(k * HALF, (k + 1) * HALF)
-            if i in D_ON_G and k == 1:
+            cols = slice(half * HALF, (half + 1) * HALF)
+            if half == 1 and i in HALVES_ON_GPSIMD:
                 nc.gpsimd.tensor_scalar(
-                    out=o0[i][:, cols], in0=ys[i][:, cols], scalar1=rstd[:, col], scalar2=nbias[:, col],
-                    op0=ALU.mult, op1=ALU.add,
-                )
-            elif i in D_ON_V:
-                nc.vector.tensor_scalar(
                     out=o0[i][:, cols], in0=ys[i][:, cols], scalar1=rstd[:, col], scalar2=nbias[:, col],
                     op0=ALU.mult, op1=ALU.add,
                 )
@@ -296,263 +277,221 @@ def tile_transformerencoderblock_pa_kernel(tc, h_attn, x, masks, Wo, bo, out_0, 
                     out=o0[i][:, cols], in_=ys[i][:, cols], func=ACT.Identity, bias=nbias[:, col], scale=rstd[:, col]
                 )
 
-        for i in range(NU - 1):
-            o0[i] = keep.tile([P, T], F32, name="o0_%d" % i)
-        o0[NU - 1] = keep.tile([P, T + NU], F32, name="o0_%d" % (NU - 1))
-        am1 = keep.tile([P, 1], F32, name="am1")
-
         def store_0(i):
-            n, j = divmod(i, NJ)
-            nc.sync.dma_start(out=out_0[n].rearrange("(p j) t -> p j t", j=NJ)[:, j, :], in_=o0[i][:, 0:T])
+            nc.sync.dma_start(out=rows_of(out_0, i), in_=o0[i][:, 0:T])
 
-        def row_amax(i, c0, c1, col):
-            if col == NU:
-                nc.vector.tensor_reduce(
-                    out=am1[:], in_=o0[i][:, c0 : T + NU], axis=AX.X, op=ALU.max, apply_absolute_value=True
-                )
-            else:
-                nc.vector.tensor_reduce(
-                    out=o0[NU - 1][:, T + col : T + col + 1], in_=o0[i][:, c0:c1], axis=AX.X, op=ALU.max,
-                    apply_absolute_value=True,
-                )
-
-        r448 = keep.tile([P, 1], F32, name="r448")
-
-        def one_amax():
-            pt = ps_t.tile([P, P], F32, tag="tp", name="pt")
-            nc.tensor.transpose(pt[:], am1[:, 0:1].to_broadcast([P, P]), ident[:])
-            am2 = keep.tile([P, 1], F32, name="am2")
-            pts = keep.tile([P, P], F32, name="pts")
-            nc.vector.tensor_scalar(
-                out=pts[:], in0=pt[:], scalar1=1.0 / 448.0, scalar2=None, op0=ALU.mult, op1=ALU.max, accum_out=am2[:]
+        def row_amax(i, first, last, slot):
+            nc.vector.tensor_reduce(
+                out=o0[NU - 1][:, T + slot : T + slot + 1], in_=o0[i][:, first:last], axis=AX.X, op=ALU.max,
+                apply_absolute_value=True,
             )
-            nc.vector.reciprocal(out=r448[:], in_=am2[:])
 
-        def cast(i, eng):
-            n, j = divmod(i, NJ)
+        def last_amax():
+            nc.vector.tensor_reduce(
+                out=row_max[:], in_=o0[NU - 1][:, HALF : T + NU], axis=AX.X, op=ALU.max, apply_absolute_value=True
+            )
+
+
+        def one_scale():
+            across = ps_t.tile([P, P], F32, tag="tp", name="across")
+            nc.tensor.transpose(across[:], row_max[:, 0:1].to_broadcast([P, P]), ident[:])
+            scale = keep.tile([P, 1], F32, name="scale")
+            unused = keep.tile([P, P], F32, name="across_scaled")
+            nc.vector.tensor_scalar(
+                out=unused[:], in0=across[:], scalar1=1.0 / 448.0, scalar2=None, op0=ALU.mult, op1=ALU.max, accum_out=scale[:]
+            )
+            nc.vector.reciprocal(out=inv_scale[:], in_=scale[:])
+
+        def cast(i):
             f8 = keep.tile([P, T], FP8, name="f8_%d" % i)
-            if eng == "S":
+            if i % 3 == 2:
                 nc.scalar.activation(
-                    out=f8[:], in_=o0[i][:, 0:T], func=ACT.Identity, scale=r448[:, 0:1], bias=zero_t[:, 0:1], saturate=False
+                    out=f8[:], in_=o0[i][:, 0:T], func=ACT.Identity, scale=inv_scale[:, 0:1], bias=zero_t[:, 0:1],
+                    saturate=False,
                 )
             else:
                 nc.vector.tensor_scalar(
-                    out=f8[:], in0=o0[i][:, 0:T], scalar1=r448[:, 0:1], scalar2=None, op0=ALU.mult, saturate=False
+                    out=f8[:], in0=o0[i][:, 0:T], scalar1=inv_scale[:, 0:1], scalar2=None, op0=ALU.mult, saturate=False
                 )
-            nc.sync.dma_start(
-                out=out_1[n].rearrange("(p j) t -> p j t", j=NJ)[:, j, :], in_=f8[:].bitcast(U8)
-            )
+            nc.sync.dma_start(out=rows_of(out_1, i), in_=f8[:].bitcast(U8))
 
-        nc.vector.memset(wz[:], 0.0)
+
+        nc.vector.memset(zeros[:], 0.0)
         nc.vector.memset(eps_t[:], EPS)
-        nc.vector.memset(mrow[0][:], 0.0)
+        nc.vector.memset(mrow[:], 0.0)
         nc.vector.memset(zero_t[:], 0.0)
-        nc.vector.memset(mrow[1][:], 0.0)
-        nc.vector.memset(mrow[2][:], 0.0)
         nc.scalar.activation(out=warm[:], in_=eps_t[:], func=ACT.Abs_reciprocal_sqrt)
         make_identity(nc, ident[:])
         make_identity(nc, ident_bf[:])
         nc.gpsimd.memset(ones[:], 1.0)
         load_w(0)
         load_h(0, 0)
-        if 0 in MASK_DMA:
-            load_mask_spread(0)
-        else:
-            load_mask(0)
+        nc.sync.dma_start(out=mrow[0:1, :], in_=masks[0])
         nc.sync.dma_start(out=bo_bf[:], in_=bo.rearrange("(p j) -> p j", j=NJ))
         load_w(1)
-        load_h(0, 1)
-        load_h(0, 2)
-        load_h(0, 3)
-        if M01_DMA:
-            load_mask_0b()
+        for c in range(1, T // CHUNK):
+            load_h(0, c)
         for n in range(NSEQ):
             if n > 0:
-                if n not in MASK_DMA:
-                    load_mask(n)
-                for c in range(4):
+                for c in range(T // CHUNK):
                     load_h(n, c)
-                if n in MASK_DMA:
-                    load_mask_spread(n)
             for j in range(NJ):
                 load_x(n * NJ + j)
+            if n > 0:
+                nc.sync.dma_start(out=mask_n[n][:], in_=masks[n, 0].partition_broadcast(P))
+
 
         ops = {}
 
         def op(name, fn, args, needs):
             ops[name] = (fn, args, list(needs))
 
+        op(("BO",), widen_bo, (), ())
+        for w in range(2):
+            op(("DUMMY", w), dummy_matmul, (), ())
+        for b in range(2):
+            op(("T", "w%d" % b), transposes, ("w%d" % b,), ())
+            op(("C", "w%d" % b), copy_out_w, (b,), [("T", "w%d" % b)])
+            op(("QW", b), quantise_w, (b,), [("C", "w%d" % b)])
+        for half in range(2):
+            op(("MM", half), spread_mask, (half,), ())
+            op(("CM", half), copy_mask, (half,), [("MM", half)])
+        for n in range(NSEQ):
+            for c in range(T // CHUNK):
+                key = "h%d_%d" % (n, c)
+                op(("T", key), transposes, (key,), ())
+                op(("C", key), copy_out_h, (n, c), [("T", key)] + ([("C", "h%d_%d" % (n, c - 1))] if c % 2 else []))
+            for pc in range(len(PIECES[n])):
+                first, frames = PIECES[n][pc]
+                op(("Q", n, pc), quantise, (n, pc), [("C", "h%d_%d" % (n, c)) for c in range(first // CHUNK, (first + frames) // CHUNK)])
+        for i in range(NU):
+            n, j = divmod(i, NJ)
+            pieces = range(len(PIECES[n]))
+            for pc in pieces:
+                op(("P", i, pc), project, (i, pc), [("Q", n, pc), ("QW", j // 2)])
+                op(("U", i, pc), bias_mask, (i, pc), [("P", i, pc), ("BO",)] + ([("CM", PIECES[n][pc][0] // HALF)] if n == 0 else []))
+            if i in GPSIMD_ADDS:
+                for half in range(2):
+                    op(("Y", i, half), add_on_gpsimd, (i, half), [("U", i, pc) for pc in pieces if PIECES[n][pc][0] // HALF == half])
+                y_made = [("Y", i, 0), ("Y", i, 1)]
+                op(("NM", i), neg_mean, (i,), y_made + [("SX", i)])
+                op(("SQ", i), squares, (i,), y_made + [("NM", i)])
+            else:
+                op(("Y", i), add_on_vector, (i,), [("U", i, pc) for pc in pieces])
+                y_made = [("Y", i)]
+                op(("NM", i), neg_mean, (i,), y_made)
+                op(("SQ", i), squares, (i,), y_made)
+            op(("IS", i), inv_std, (i,), [("SQ", i)])
+            op(("NB", i), neg_bias, (i,), [("IS", i), ("NM", i)])
+            for half in range(2):
+                op(("D", i, half), normalise, (i, half), [("NB", i)])
+            op(("ST", i), store_0, (i,), [("D", i, 0), ("D", i, 1)])
+            if i < NU - 1:
+                op(("AM", i), row_amax, (i, 0, T, i), [("D", i, 0), ("D", i, 1)])
+        for i in FOLDED:
+            op(("FX", i), fold_x, (i,), ())
+            op(("SX", i), sum_fold, (i,), [("FX", i)])
+        op(("SX", 3), sum_x_scalar, (3,), ())
+        op(("SX", NU - 1), sum_x_vector, (NU - 1,), ())
+        op(("AM", NU - 1), row_amax, (NU - 1, 0, HALF, NU - 1), [("D", NU - 1, 0)])
+        op(("AM", NU), last_amax, (), [("D", NU - 1, 1)] + [("AM", i) for i in range(NU)])
+
+
+        def adds_of(i):
+            if i == NU - 1:
+                return [("SX", i)]
+            return [] if i in GPSIMD_ADDS else [("Y", i)]
+
+        unit3_first = (3, 0, 1, 2)
+
+        q_pe = [("DUMMY", 0), ("DUMMY", 1), ("T", "w0"), ("T", "h0_0"), ("MM", 0), ("T", "w1"), ("T", "h0_1"),
+                ("P", 0, 0), ("P", 1, 0), ("T", "h0_2"), ("P", 2, 0), ("P", 3, 0), ("T", "h0_3"), ("MM", 1)]
+        q_pe += [("P", j, pc) for pc in (1, 2) for j in unit3_first] + [("T", "h1_%d" % c) for c in range(4)]
+        q_pe += [("P", 4, 0), ("P", 4, 1), ("T", "h2_0"), ("T", "h2_1"), ("P", 5, 0), ("P", 5, 1), ("FX", 5), ("T", "h2_2")]
+        q_pe += [("P", 6, 0), ("P", 6, 1), ("T", "h2_3")]
+        for i in range(7, NU):
+            q_pe += [("P", i, 0), ("P", i, 1)] + ([("FX", i)] if i in FOLDED else [])
+
+        q_g = []
+        for i in GPSIMD_ADDS:
+            q_g += [("Y", i, 0), ("Y", i, 1)] + [("D", d, 1) for d in GPSIMD_HALVES.get(i, ())]
+
+        q_v = [("C", "w0"), ("QW", 0), ("BO",), ("Q", 0, 0), ("C", "w1"), ("QW", 1)] + [("U", j, 0) for j in range(NJ)]
+        q_v += [("Q", 0, 1), ("Q", 0, 2)] + [("U", j, pc) for pc in (1, 2) for j in unit3_first]
+        q_v += adds_of(0) + [("Q", 1, 0)] + adds_of(1) + [("Q", 1, 1)] + adds_of(2)
+        for i in range(NJ, NU + 1):
+            if i in GPSIMD_ADDS:
+                q_v += adds_of(i - 1)
+            if i == 7:
+                q_v += [("Q", 2, 0), ("Q", 2, 1)]
+            if i < NU:
+                q_v += [("U", i, 0), ("U", i, 1)]
+            if i not in GPSIMD_ADDS:
+                q_v += adds_of(i - 1)
+            if i - 1 - AMAX_BEHIND >= 0:
+                q_v += [("AM", i - 1 - AMAX_BEHIND)]
+        q_v += [("AM", i) for i in range(NU - AMAX_BEHIND, NU + 1)]
+
+        q_s = [("C", "h0_0"), ("CM", 0), ("C", "h0_1"), ("C", "h0_2"), ("C", "h0_3"), ("CM", 1), ("SX", 3)]
+        q_s += [("C", "h1_%d" % c) for c in range(4)]
+        for k in range(NU + 1):
+            if k in (3, 4):
+                q_s += [("C", "h2_%d" % (2 * k - 6)), ("C", "h2_%d" % (2 * k - 5))]
+            if k + 2 in FOLDED:
+                q_s += [("SX", k + 2)]
+            first_half = [("D", k - 1, 0)] if k > 0 else []
+            if k == NU:
+                q_s += first_half
+            elif k in GPSIMD_ADDS:
+                q_s += [("NM", k)] + first_half + [("SQ", k)]
+            else:
+                q_s += [("NM", k), ("SQ", k)] + first_half
+            if k < NU:
+                q_s += [("IS", k)]
+            if k > 0 and k - 1 not in HALVES_ON_GPSIMD:
+                q_s += [("D", k - 1, 1)]
+            if k < NU:
+                q_s += [("NB", k)]
+
+        q_sp = [("ST", i) for i in range(NU)]
+
+
         def rotate(makers, readers_of, bufs):
             for m in range(bufs, len(makers)):
                 ops[makers[m]][2].extend(readers_of(makers[m - bufs]))
 
-        def d_ops(i):
-            return [("D", i, 0), ("D", i, 1)]
+        def psum_readers(name):
+            return {"T": [("C", name[1])], "MM": [("CM", name[1])], "FX": [("SX", name[1])], "DUMMY": []}.get(
+                name[0], [("U",) + name[1:]]
+            )
 
-        def eng_of(key):
-            return "V" if key in V_COPIES else "S"
+        def y_makers(i):
+            return [("Y", i, 0), ("Y", i, 1)] if i in GPSIMD_ADDS else [("Y", i)]
 
-        def widen_bo():
-            nc.vector.tensor_copy(out=bo32[:], in_=bo_bf[:])
-
-        op(("BO",), widen_bo, (), ())
-        for w in range(2):
-            op(("WARM", w), warm_pe, (), ())
-        for b in range(2):
-            op(("T", "w%d" % b), transposes, ("w%d" % b,), ())
-            op(("C", "w%d" % b), copy_out, ("w%d" % b, eng_of("w%d" % b), wg, b), (("T", "w%d" % b),))
-            op(("QW", b), quantise_w, (b,), (("C", "w%d" % b),))
-        for n in range(NSEQ):
-            for c in range(4):
-                key = "h%d_%d" % (n, c)
-                op(("T", key), transposes, (key,), ())
-                op(("C", key), copy_out_h, (n, c, eng_of(key)), (("T", key),) + ((("C", "h%d_%d" % (n, c - 1)),) if c % 2 else ()))
-            for pc in range(len(PIECES[n])):
-                c0, w = PIECES[n][pc]
-                op(("Q", n, pc), quantise, (n, pc), [("C", "h%d_%d" % (n, c)) for c in range(c0 // 256, (c0 + w) // 256)])
-            for half in range(2):
-                op(("MM", n, half), mask_mm, (n, half, "acc" if n == 0 else "tp"), ())
-                op(("C", "m%d_%d" % (n, half)), mask_copy, (n, half, eng_of("m%d_%d" % (n, half))), (("MM", n, half),))
-        for i in range(NU):
-            n, j = divmod(i, NJ)
-            for pc in range(len(PIECES[n])):
-                op(("P", i, pc), project, (i, pc), (("Q", n, pc), ("QW", j // 2)))
-                op(("U", i, pc), bias_mask, (i, pc), [("P", i, pc), ("BO",)] + ([] if n in MASK_DMA or (M01_DMA and PIECES[n][pc][0] >= HALF) else [("C", "m%d_%d" % (n, PIECES[n][pc][0] // HALF))]))
-            for half in range(2):
-                op(("D", i, half), normalise, (i, half), (("NB", i),))
-                op(("YG", i, half), add_g, (i, half),
-                   [("U", i, pc) for pc in range(len(PIECES[n])) if PIECES[n][pc][0] // HALF == half])
-            op(("YV", i), add_v, (i,), [("U", i, pc) for pc in range(len(PIECES[n]))])
-            op(("FX", i), fold_x, (i,), ())
-            if i in FOLD:
-                op(("SX", i), sum_fold, (i,), (("FX", i),))
-            else:
-                op(("SX", i), sum_x, (i,), ())
-            made = (("YG", i, 0), ("YG", i, 1), ("SX", i)) if i in G_UNITS else (("YV", i),)
-            op(("NM", i), neg_mean, (i,), made)
-            op(("SQ", i), squares, (i,), made + ((("NM", i),) if i in G_UNITS else ()))
-            op(("IS", i), inv_std, (i,), (("SQ", i),))
-            op(("NB", i), neg_bias, (i,), (("IS", i), ("NM", i)))
-            op(("ST", i), store_0, (i,), d_ops(i))
-            if i < NU - 1:
-                op(("AM", i), row_amax, (i, 0, T, i), d_ops(i))
-        op(("AM", NU - 1, 0), row_amax, (NU - 1, 0, HALF, NU - 1), (("D", NU - 1, 0),))
-        op(("AM", NU - 1, 1), row_amax, (NU - 1, HALF, T, NU), [("D", NU - 1, 1), ("AM", NU - 1, 0)] + [("AM", i) for i in range(NU - 1)])
-
-        q_pe = [("WARM", 0), ("WARM", 1), ("T", "w0"), ("T", "h0_0"), ("MM", 0, 0), ("T", "w1"), ("T", "h0_1"),
-                ("P", 0, 0), ("P", 1, 0), ("T", "h0_2"), ("P", 2, 0), ("P", 3, 0), ("T", "h0_3"), ("MM", 0, 1)]
-        if M01_DMA:
-            q_pe.remove(("MM", 0, 1))
-        for w in range(WARMS, 2):
-            q_pe.remove(("WARM", w))
-        q_pe += [("P", j, 1) for j in (3, 0, 1, 2)] + [("P", j, 2) for j in (3, 0, 1, 2)] + [("T", "h1_%d" % c) for c in range(4)] + [("MM", 1, half) for half in range(2) if 1 not in MASK_DMA]
-        q_pe += [("P", 4, 0), ("P", 4, 1), ("T", "h2_0"), ("T", "h2_1"), ("P", 5, 0), ("P", 5, 1), ("T", "h2_2")]
-        q_pe += [("P", 6, 0), ("P", 6, 1), ("T", "h2_3")] + [("MM", 2, half) for half in range(2) if 2 not in MASK_DMA] + [("P", i, half) for i in range(7, NU) for half in range(2)]
-        for i in FOLD:
-            q_pe.insert(q_pe.index(("P", i - FX_LEAD, 1)) + 1, ("FX", i))
-
-        q_g = []
-        for i in G_UNITS:
-            q_g += [("YG", i, 0), ("YG", i, 1)] + [("D", d, 1) for d in D_AFTER.get(i, ())]
-
-        def v_add(i):
-            if i in G_UNITS:
-                return [] if i in SX_ON_S else [("SX", i)]
-            return [("YV", i)]
-
-        q_v = [("C", "w0"), ("QW", 0), ("BO",), ("Q", 0, 0), ("C", "w1"), ("QW", 1)] + [("U", j, 0) for j in range(NJ)] + [("Q", 0, 1), ("Q", 0, 2)]
-        q_v += [("U", j, 1) for j in (3, 0, 1, 2)] + [("U", j, 2) for j in (3, 0, 1, 2)] + v_add(0) + [("Q", 1, 0)] + v_add(1) + [("Q", 1, 1)] + v_add(2)
-        q_v += [("C", k) for k in ("m1_0", "m1_1") if k in V_COPIES]
-        late = []
-        for i in range(NU):
-            if i + 1 in D_ON_V:
-                late += [("D", i + 1, 0), ("D", i + 1, 1)]
-            late += [("AM", i)] if i < NU - 1 else [("AM", i, 0), ("AM", i, 1)]
-        n_am = 0
-        for i in range(NJ, NU + 1):
-            if i in G_UNITS:
-                q_v += v_add(i - 1)
-            if i == Q2_AT:
-                q_v += [("Q", 2, 0), ("Q", 2, 1)]
-            if i < NU:
-                q_v += [("U", i, 0), ("U", i, 1)]
-            if i not in G_UNITS:
-                q_v += v_add(i - 1)
-            if i - 1 - AM_LAG >= 0:
-                q_v += [late[n_am]]
-                n_am += 1
-        q_v += late[n_am:]
-
-        q_s = [("C", "h0_0"), ("C", "m0_0"), ("C", "h0_1"), ("C", "h0_2"), ("C", "h0_3"), ("C", "m0_1")]
-        if M01_DMA:
-            q_s.remove(("C", "m0_1"))
-        q_s += [("SX", i) for i in SX_ON_S if i < NJ] + [("C", "h1_%d" % c) for c in range(4)]
-        for k in range(NU + 1):
-            if k == 1:
-                q_s += [("C", c) for c in ("m1_0", "m1_1") if c not in V_COPIES and 1 not in MASK_DMA]
-            if k == 3:
-                q_s += [("C", "h2_0"), ("C", "h2_1")]
-            if k == 4:
-                q_s += [("C", "h2_2"), ("C", "h2_3")]
-            if k == 5:
-                q_s += [("C", c) for c in ("m2_0", "m2_1") if c not in V_COPIES and 2 not in MASK_DMA]
-            if NJ <= k + SX_LEAD < NU and k + SX_LEAD in SX_ON_S:
-                q_s += [("SX", k + SX_LEAD)]
-            if k < NU and k in G_UNITS:
-                q_s += [("NM", k)]
-                if k > 0 and k - 1 not in D_ON_V:
-                    q_s += [("D", k - 1, 0)]
-                q_s += [("SQ", k)]
-            if k < NU and k not in G_UNITS:
-                q_s += [("NM", k), ("SQ", k)]
-            if k > 0 and k not in G_UNITS and k - 1 not in D_ON_V:
-                q_s += [("D", k - 1, 0)]
-            if k < NU:
-                q_s += [("IS", k)]
-            if k > 0 and k - 1 not in D_ON_V + D_ON_G:
-                q_s += [("D", k - 1, 1)]
-            if k < NU:
-                q_s += [("NB", k)]
-        q_sp = [("ST", i) for i in range(NU)]
-
-        def psum_reader(nm):
-            if nm[0] == "T":
-                return [("C", nm[1])]
-            if nm[0] == "MM":
-                return [("C", "m%d_%d" % (nm[1], nm[2]))]
-            if nm[0] == "P":
-                return [("U", nm[1], nm[2])]
-            if nm[0] == "FX":
-                return [("SX", nm[1])]
-            return []
-
-        def in_acc(nm):
-            return nm[0] in ("WARM", "P") or (nm[0] == "MM" and nm[1] == 0)
-
-        rotate([nm for nm in q_pe if in_acc(nm)], psum_reader, 4)
-        rotate([nm for nm in q_pe if not in_acc(nm)], psum_reader, 4)
-        rotate([("U", i, 0) for i in range(NU)],
-               lambda nm: [("YG", nm[1], 0), ("YG", nm[1], 1)] if nm[1] in G_UNITS else [("YV", nm[1])], 5)
-        rotate([("YG", i, 0) if i in G_UNITS else ("YV", i) for i in range(NU)],
-               lambda nm: [("SQ", nm[1])] + d_ops(nm[1]), 6)
+        rotate([name for name in q_pe if name[0] in ("DUMMY", "MM", "P")], psum_readers, BANKS)
+        rotate([name for name in q_pe if name[0] in ("T", "FX")], psum_readers, BANKS)
+        rotate([("U", i, 0) for i in range(NU)], lambda name: y_makers(name[1]), U_BUFS)
+        rotate([y_makers(i)[0] for i in range(NU)], lambda name: [("SQ", name[1]), ("D", name[1], 0), ("D", name[1], 1)], Y_BUFS)
         rotate([("C", "h%d_%d" % (n, c)) for n in range(NSEQ) for c in (0, 2)],
-               lambda nm: [("Q", int(nm[1][1]), pc) for pc in range(len(PIECES[int(nm[1][1])]))], 3)
+               lambda name: [("Q", int(name[1][1]), pc) for pc in range(len(PIECES[int(name[1][1])]))], HG_BUFS)
+
 
         queues = [q_pe, q_v, q_g, q_s, q_sp]
         heads = [0, 0, 0, 0, 0]
-        done = set()
+        written = set()
         left = sum(len(q) for q in queues)
         while left > 0:
             before = left
-            for k in range(5):
+            for k in range(len(queues)):
                 q = queues[k]
-                while heads[k] < len(q) and all(nm in done for nm in ops[q[heads[k]]][2]):
+                while heads[k] < len(q) and all(name in written for name in ops[q[heads[k]]][2]):
                     fn, args, needs = ops[q[heads[k]]]
                     fn(*args)
-                    done.add(q[heads[k]])
+                    written.add(q[heads[k]])
                     heads[k] += 1
                     left -= 1
             assert left < before
-        one_amax()
+
+        one_scale()
         for i in range(NU):
-            cast(i, "S" if i % 3 == 2 else "V")
+            cast(i)

@@ -37,7 +37,6 @@ def tile_transformerencoderblock_pa_kernel(tc, h_attn, x, masks, Wo, bo, out_0, 
         keep = ctx.enter_context(tc.tile_pool(name="keep", bufs=1))
         work = ctx.enter_context(tc.tile_pool(name="work", bufs=HG_BUFS))
         upool = ctx.enter_context(tc.tile_pool(name="upool", bufs=U_BUFS))
-        ypool = ctx.enter_context(tc.tile_pool(name="ypool", bufs=Y_BUFS))
         ps_t = ctx.enter_context(tc.psum_pool(name="ps_t", bufs=BANKS))
         ps_a = ctx.enter_context(tc.psum_pool(name="ps_a", bufs=BANKS))
         ctx.enter_context(tc.manual_schedule())
@@ -76,7 +75,8 @@ def tile_transformerencoderblock_pa_kernel(tc, h_attn, x, masks, Wo, bo, out_0, 
         prod = {}
         folds = {}
         us = {}
-        ys = {}
+        y_buf = [keep.tile([P, T], F32, name="y_buf%d" % b) for b in range(Y_BUFS)]
+        ys = [y_buf[i % Y_BUFS] for i in range(NU)]
         sums = keep.tile([P, NU, 4], F32, name="sums")
         scaled = keep.tile([P, NU, 4], F32, name="scaled")
         negmean = keep.tile([P, NU], F32, name="negmean")
@@ -200,13 +200,10 @@ def tile_transformerencoderblock_pa_kernel(tc, h_attn, x, masks, Wo, bo, out_0, 
             )
 
         def add_on_gpsimd(i, half):
-            if half == 0:
-                ys[i] = ypool.tile([P, T], F32, tag="y", name="y%d" % i)
             cols = slice(half * HALF, (half + 1) * HALF)
             nc.gpsimd.tensor_tensor(out=ys[i][:, cols], in0=us[i][:, cols], in1=xs[i][:, cols], op=ALU.add)
 
         def add_on_vector(i):
-            ys[i] = ypool.tile([P, T], F32, tag="y", name="y%d" % i)
             nc.vector.scalar_tensor_tensor(
                 out=ys[i][:], in0=us[i][:], scalar=1.0, in1=xs[i][:], op0=ALU.mult, op1=ALU.add,
                 accum_out=sums[:, i, 0:1],
@@ -373,14 +370,12 @@ def tile_transformerencoderblock_pa_kernel(tc, h_attn, x, masks, Wo, bo, out_0, 
             if i in GPSIMD_ADDS:
                 for half in range(2):
                     op(("Y", i, half), add_on_gpsimd, (i, half), [("U", i, pc) for pc in pieces if PIECES[n][pc][0] // HALF == half])
-                y_made = [("Y", i, 0), ("Y", i, 1)]
-                op(("NM", i), neg_mean, (i,), y_made + [("SX", i)])
-                op(("SQ", i), squares, (i,), y_made + [("NM", i)])
+                op(("NM", i), neg_mean, (i,), [("U", i, pc) for pc in pieces] + [("SX", i)])
+                op(("SQ", i), squares, (i,), [("Y", i, 0), ("Y", i, 1), ("NM", i)])
             else:
                 op(("Y", i), add_on_vector, (i,), [("U", i, pc) for pc in pieces])
-                y_made = [("Y", i)]
-                op(("NM", i), neg_mean, (i,), y_made)
-                op(("SQ", i), squares, (i,), y_made)
+                op(("NM", i), neg_mean, (i,), [("Y", i)])
+                op(("SQ", i), squares, (i,), [("Y", i)])
             op(("IS", i), inv_std, (i,), [("SQ", i)])
             op(("NB", i), neg_bias, (i,), [("IS", i), ("NM", i)])
             for half in range(2):
@@ -398,8 +393,6 @@ def tile_transformerencoderblock_pa_kernel(tc, h_attn, x, masks, Wo, bo, out_0, 
 
 
         def adds_of(i):
-            if i == NU - 1:
-                return [("SX", i)]
             return [] if i in GPSIMD_ADDS else [("Y", i)]
 
         unit3_first = (3, 0, 1, 2)
@@ -426,6 +419,8 @@ def tile_transformerencoderblock_pa_kernel(tc, h_attn, x, masks, Wo, bo, out_0, 
                 q_v += [("Q", 2, 0), ("Q", 2, 1)]
             if i < NU:
                 q_v += [("U", i, 0), ("U", i, 1)]
+            if i == NU - 1:
+                q_v += [("SX", i)]
             if i not in GPSIMD_ADDS:
                 q_v += adds_of(i - 1)
             if i - 1 - AMAX_BEHIND >= 0:
@@ -435,21 +430,20 @@ def tile_transformerencoderblock_pa_kernel(tc, h_attn, x, masks, Wo, bo, out_0, 
         q_s = [("C", "h0_0"), ("CM", 0), ("C", "h0_1"), ("C", "h0_2"), ("C", "h0_3"), ("CM", 1), ("SX", 3)]
         q_s += [("C", "h1_%d" % c) for c in range(4)]
         for k in range(NU + 1):
-            if k in (3, 4):
-                q_s += [("C", "h2_%d" % (2 * k - 6)), ("C", "h2_%d" % (2 * k - 5))]
-            if k + 2 in FOLDED:
-                q_s += [("SX", k + 2)]
-            first_half = [("D", k - 1, 0)] if k > 0 else []
-            if k == NU:
-                q_s += first_half
-            elif k in GPSIMD_ADDS:
-                q_s += [("NM", k)] + first_half + [("SQ", k)]
-            else:
-                q_s += [("NM", k), ("SQ", k)] + first_half
+            if k < NU:
+                q_s += ([] if k in GPSIMD_ADDS else [("NM", k)]) + [("SQ", k)]
+            if k > 0:
+                q_s += [("D", k - 1, 0)]
             if k < NU:
                 q_s += [("IS", k)]
+            if k in (2, 3):
+                q_s += [("C", "h2_%d" % (2 * k - 4)), ("C", "h2_%d" % (2 * k - 3))]
             if k > 0 and k - 1 not in HALVES_ON_GPSIMD:
                 q_s += [("D", k - 1, 1)]
+            if k + 2 in FOLDED:
+                q_s += [("SX", k + 2)]
+            if k + 1 in GPSIMD_ADDS:
+                q_s += [("NM", k + 1)]
             if k < NU:
                 q_s += [("NB", k)]
 

@@ -24,9 +24,10 @@ FLOPS = 2 * NSEQ * T * C * E
 
 PIECES = (((0, 256), (256, 256), (512, 512)), ((0, 512), (512, 512)), ((0, 512), (512, 512)))
 GPSIMD_ADDS = (3, 5, 7, 9, 11)
-GPSIMD_HALVES = {5: (2,), 7: (4,), 9: (6,), 11: (9, 10, 11)}
-HALVES_ON_GPSIMD = (2, 4, 6, 9, 10, 11)
-FOLDED = (5, 7, 9)
+GPSIMD_HALVES = {5: ((2, 0), (2, 1)), 7: ((4, 0), (4, 1)), 9: ((6, 0), (6, 1)), 11: ((9, 1), (10, 1), (11, 1))}
+HALVES_ON_GPSIMD = tuple(part for parts in GPSIMD_HALVES.values() for part in parts)
+FOLDED = (9, 11)
+SX_SCALAR = (3, 5, 7)
 AMAX_BEHIND = 4
 U_BUFS, Y_BUFS, HG_BUFS, BANKS = 5, 6, 3, 4
 
@@ -264,7 +265,7 @@ def tile_transformerencoderblock_pa_kernel(tc, h_attn, x, masks, Wo, bo, out_0, 
         def normalise(i, half):
             col = slice(i, i + 1)
             cols = slice(half * HALF, (half + 1) * HALF)
-            if half == 1 and i in HALVES_ON_GPSIMD:
+            if (i, half) in HALVES_ON_GPSIMD:
                 nc.gpsimd.tensor_scalar(
                     out=o0[i][:, cols], in0=ys[i][:, cols], scalar1=rstd[:, col], scalar2=nbias[:, col],
                     op0=ALU.mult, op1=ALU.add,
@@ -332,8 +333,8 @@ def tile_transformerencoderblock_pa_kernel(tc, h_attn, x, masks, Wo, bo, out_0, 
             if n > 0:
                 for c in range(T // CHUNK):
                     load_h(n, c)
-            for j in range(NJ):
-                load_x(n * NJ + j)
+            for i in {0: (0, 1, 2, 3, 5, 7), 1: (4, 6), 2: (8, 9, 10, 11)}[n]:
+                load_x(i)
             if n > 0:
                 nc.sync.dma_start(out=mask_n[n][:], in_=masks[n, 0].partition_broadcast(P))
 
@@ -386,11 +387,23 @@ def tile_transformerencoderblock_pa_kernel(tc, h_attn, x, masks, Wo, bo, out_0, 
         for i in FOLDED:
             op(("FX", i), fold_x, (i,), ())
             op(("SX", i), sum_fold, (i,), [("FX", i)])
-        op(("SX", 3), sum_x_scalar, (3,), ())
-        op(("SX", NU - 1), sum_x_vector, (NU - 1,), ())
+        for i in SX_SCALAR:
+            op(("SX", i), sum_x_scalar, (i,), ())
         op(("AM", NU - 1), row_amax, (NU - 1, 0, HALF, NU - 1), [("D", NU - 1, 0)])
         op(("AM", NU), last_amax, (), [("D", NU - 1, 1)] + [("AM", i) for i in range(NU)])
 
+        PE_TAIL = [("P", 4, 0), ("P", 4, 1), ("T", "h2_0"), ("T", "h2_1"), ("P", 5, 0), ("P", 5, 1), ("T", "h2_2")]
+        PE_TAIL += [("P", 6, 0), ("P", 6, 1), ("T", "h2_3"), ("P", 7, 0), ("P", 7, 1), ("P", 8, 0), ("P", 8, 1), ("P", 9, 0), ("P", 9, 1), ("FX", 9)]
+        PE_TAIL += [("P", 10, 0), ("P", 10, 1), ("P", 11, 0), ("P", 11, 1), ("FX", 11)]
+        V_BLOCKS = [
+            ([("Y", 0), ("Q", 1, 0), ("Y", 1), ("Q", 1, 1), ("Y", 2)], (4,), 0),
+            ([("Y", 4)], (5,), 1), ([], (6,), 1),
+            ([("Y", 6), ("Q", 2, 0), ("Q", 2, 1)], (7,), 1), ([], (8,), 1),
+            ([("Y", 8)], (9,), 1), ([], (10,), 1),
+            ([("Y", 10)], (11,), 7),
+        ]
+        S_HEAD = [("SX", 3), ("SX", 5), ("SX", 7)] + [("C", "h1_%d" % c) for c in range(4)]
+        S_EXTRA = {2: [("C", "h2_0"), ("C", "h2_1")], 3: [("C", "h2_2"), ("C", "h2_3")], 7: [("SX", 9)], 9: [("SX", 11)]}
 
         def adds_of(i):
             return [] if i in GPSIMD_ADDS else [("Y", i)]
@@ -400,52 +413,33 @@ def tile_transformerencoderblock_pa_kernel(tc, h_attn, x, masks, Wo, bo, out_0, 
         q_pe = [("DUMMY", 0), ("DUMMY", 1), ("T", "w0"), ("T", "h0_0"), ("MM", 0), ("T", "w1"), ("T", "h0_1"),
                 ("P", 0, 0), ("P", 1, 0), ("T", "h0_2"), ("P", 2, 0), ("P", 3, 0), ("T", "h0_3"), ("MM", 1)]
         q_pe += [("P", j, pc) for pc in (1, 2) for j in unit3_first] + [("T", "h1_%d" % c) for c in range(4)]
-        q_pe += [("P", 4, 0), ("P", 4, 1), ("T", "h2_0"), ("T", "h2_1"), ("P", 5, 0), ("P", 5, 1), ("FX", 5), ("T", "h2_2")]
-        q_pe += [("P", 6, 0), ("P", 6, 1), ("T", "h2_3")]
-        for i in range(7, NU):
-            q_pe += [("P", i, 0), ("P", i, 1)] + ([("FX", i)] if i in FOLDED else [])
+        q_pe += PE_TAIL
 
         q_g = []
         for i in GPSIMD_ADDS:
-            q_g += [("Y", i, 0), ("Y", i, 1)] + [("D", d, 1) for d in GPSIMD_HALVES.get(i, ())]
+            q_g += [("Y", i, 0), ("Y", i, 1)] + [("D", d, half) for d, half in GPSIMD_HALVES.get(i, ())]
 
         q_v = [("C", "w0"), ("QW", 0), ("BO",), ("Q", 0, 0), ("C", "w1"), ("QW", 1)] + [("U", j, 0) for j in range(NJ)]
         q_v += [("Q", 0, 1), ("Q", 0, 2)] + [("U", j, pc) for pc in (1, 2) for j in unit3_first]
-        q_v += adds_of(0) + [("Q", 1, 0)] + adds_of(1) + [("Q", 1, 1)] + adds_of(2)
-        for i in range(NJ, NU + 1):
-            if i in GPSIMD_ADDS:
-                q_v += adds_of(i - 1)
-            if i == 7:
-                q_v += [("Q", 2, 0), ("Q", 2, 1)]
-            if i < NU:
+        am = 0
+        for two_port, reads, reduces in V_BLOCKS:
+            q_v += list(two_port)
+            for i in reads:
                 q_v += [("U", i, 0), ("U", i, 1)]
-            if i == NU - 1:
-                q_v += [("SX", i)]
-            if i not in GPSIMD_ADDS:
-                q_v += adds_of(i - 1)
-            if i - 1 - AMAX_BEHIND >= 0:
-                q_v += [("AM", i - 1 - AMAX_BEHIND)]
-        q_v += [("AM", i) for i in range(NU - AMAX_BEHIND, NU + 1)]
+            q_v += [("AM", am + r) for r in range(reduces)]
+            am += reduces
+        assert am == NU + 1
 
-        q_s = [("C", "h0_0"), ("CM", 0), ("C", "h0_1"), ("C", "h0_2"), ("C", "h0_3"), ("CM", 1), ("SX", 3)]
-        q_s += [("C", "h1_%d" % c) for c in range(4)]
+        q_s = [("C", "h0_0"), ("CM", 0), ("C", "h0_1"), ("C", "h0_2"), ("C", "h0_3"), ("CM", 1)] + S_HEAD
         for k in range(NU + 1):
-            if k < NU:
-                q_s += ([] if k in GPSIMD_ADDS else [("NM", k)]) + [("SQ", k)]
-            if k > 0:
-                q_s += [("D", k - 1, 0)]
-            if k < NU:
-                q_s += [("IS", k)]
-            if k in (2, 3):
-                q_s += [("C", "h2_%d" % (2 * k - 4)), ("C", "h2_%d" % (2 * k - 3))]
-            if k > 0 and k - 1 not in HALVES_ON_GPSIMD:
-                q_s += [("D", k - 1, 1)]
-            if k + 2 in FOLDED:
-                q_s += [("SX", k + 2)]
+            between = [("D", k - 1, half) for half in range(2) if k > 0 and (k - 1, half) not in HALVES_ON_GPSIMD]
+            between[1:1] = S_EXTRA.get(k, [])
             if k + 1 in GPSIMD_ADDS:
-                q_s += [("NM", k + 1)]
+                between += [("NM", k + 1)]
             if k < NU:
-                q_s += [("NB", k)]
+                q_s += ([] if k in GPSIMD_ADDS else [("NM", k)]) + [("SQ", k)] + between[0:1] + [("IS", k)] + between[1:] + [("NB", k)]
+            else:
+                q_s += between
 
         q_sp = [("ST", i) for i in range(NU)]
 

@@ -300,18 +300,25 @@ def tile_transformerencoderblock_pa_kernel(tc, h_attn, x, masks, Wo, bo, out_0, 
             )
             nc.vector.reciprocal(out=inv_scale[:], in_=scale[:])
 
+        f8 = [keep.tile([P, NJ, T], FP8, name="f8_%d" % n) for n in range(NSEQ)]
+
         def cast(i):
-            f8 = keep.tile([P, T], FP8, name="f8_%d" % i)
+            n, j = divmod(i, NJ)
             if i % 3 == 2:
                 nc.scalar.activation(
-                    out=f8[:], in_=o0[i][:, 0:T], func=ACT.Identity, scale=inv_scale[:, 0:1], bias=zero_t[:, 0:1],
+                    out=f8[n][:, j, :], in_=o0[i][:, 0:T], func=ACT.Identity, scale=inv_scale[:, 0:1], bias=zero_t[:, 0:1],
                     saturate=False,
                 )
             else:
                 nc.vector.tensor_scalar(
-                    out=f8[:], in0=o0[i][:, 0:T], scalar1=inv_scale[:, 0:1], scalar2=None, op0=ALU.mult, saturate=False
+                    out=f8[n][:, j, :], in0=o0[i][:, 0:T], scalar1=inv_scale[:, 0:1], scalar2=None, op0=ALU.mult, saturate=False
                 )
-            nc.sync.dma_start(out=rows_of(out_1, i), in_=f8[:].bitcast(U8))
+
+        def store_1(n, first, units):
+            nc.sync.dma_start(
+                out=out_1[n].rearrange("(p j) t -> p j t", j=NJ)[:, first : first + units, :],
+                in_=f8[n][:, first : first + units, :].bitcast(U8),
+            )
 
 
         nc.vector.memset(zeros[:], 0.0)
@@ -483,3 +490,7 @@ def tile_transformerencoderblock_pa_kernel(tc, h_attn, x, masks, Wo, bo, out_0, 
         one_scale()
         for i in range(NU):
             cast(i)
+            if i in (3, 7):
+                store_1(i // NJ, 0, NJ)
+            if i in (9, 11):
+                store_1(i // NJ, i % NJ - 1, 2)

@@ -149,6 +149,10 @@ def tile_transformerencoderblock_pa_kernel(tc, h_attn, x, masks, Wo, bo, out_0, 
             idle = ps_a.tile([P, HALF], F32, tag="acc", name="idle")
             nc.tensor.matmul(out=idle[:, 0:256], lhsT=zeros[:, 0:P], rhs=zeros[:], start=True, stop=True)
 
+        def late_load(i):
+            idle = ps_a.tile([P, HALF], F32, tag="acc", name="late%d" % i)
+            nc.tensor.matmul(out=idle[:, 0:256], lhsT=zeros[:, 0:P], rhs=o0[i][:, 0:256], start=True, stop=True)
+
         def spread_mask(half):
             spread[half] = ps_a.tile([P, HALF], F32, tag="acc", name="spread%d" % half)
             nc.tensor.matmul(
@@ -354,6 +358,8 @@ def tile_transformerencoderblock_pa_kernel(tc, h_attn, x, masks, Wo, bo, out_0, 
         op(("BO",), widen_bo, (), ())
         for w in range(2):
             op(("DUMMY", w), dummy_matmul, (), ())
+        for i in (NU - 2, NU - 1):
+            op(("WARM", i), late_load, (i,), [("D", i, 0)])
         for b in range(2):
             op(("T", "w%d" % b), transposes, ("w%d" % b,), ())
             op(("C", "w%d" % b), copy_out_w, (b,), [("T", "w%d" % b)])
@@ -420,7 +426,7 @@ def tile_transformerencoderblock_pa_kernel(tc, h_attn, x, masks, Wo, bo, out_0, 
         q_pe = [("DUMMY", 0), ("DUMMY", 1), ("T", "w0"), ("T", "h0_0"), ("MM", 0), ("T", "w1"), ("T", "h0_1"),
                 ("P", 0, 0), ("P", 1, 0), ("T", "h0_2"), ("P", 2, 0), ("P", 3, 0), ("T", "h0_3"), ("MM", 1)]
         q_pe += [("P", j, pc) for pc in (1, 2) for j in unit3_first] + [("T", "h1_%d" % c) for c in range(4)]
-        q_pe += PE_TAIL
+        q_pe += PE_TAIL + [("WARM", NU - 2), ("WARM", NU - 1)]
 
         q_g = []
         for i in GPSIMD_ADDS:
@@ -456,14 +462,14 @@ def tile_transformerencoderblock_pa_kernel(tc, h_attn, x, masks, Wo, bo, out_0, 
                 ops[makers[m]][2].extend(readers_of(makers[m - bufs]))
 
         def psum_readers(name):
-            return {"T": [("C", name[1])], "MM": [("CM", name[1])], "FX": [("SX", name[1])], "DUMMY": []}.get(
+            return {"T": [("C", name[1])], "MM": [("CM", name[1])], "FX": [("SX", name[1])], "DUMMY": [], "WARM": []}.get(
                 name[0], [("U",) + name[1:]]
             )
 
         def y_makers(i):
             return [("Y", i, 0), ("Y", i, 1)] if i in GPSIMD_ADDS else [("Y", i)]
 
-        rotate([name for name in q_pe if name[0] in ("DUMMY", "MM", "P")], psum_readers, BANKS)
+        rotate([name for name in q_pe if name[0] in ("DUMMY", "MM", "P", "WARM")], psum_readers, BANKS)
         rotate([name for name in q_pe if name[0] in ("T", "FX")], psum_readers, BANKS)
         rotate([("U", i, 0) for i in range(NU)], lambda name: y_makers(name[1]), U_BUFS)
         rotate([y_makers(i)[0] for i in range(NU)], lambda name: [("SQ", name[1]), ("D", name[1], 0), ("D", name[1], 1)], Y_BUFS)

@@ -424,7 +424,7 @@ def tile_transformerencoderblock_pa_kernel(tc, h_attn, x, masks, Wo, bo, out_0, 
         unit3_first = (3, 0, 1, 2)
 
         q_pe = [("DUMMY", 0), ("DUMMY", 1), ("T", "w0"), ("T", "h0_0"), ("MM", 0), ("T", "w1"), ("T", "h0_1"),
-                ("P", 0, 0), ("P", 1, 0), ("T", "h0_2"), ("P", 2, 0), ("P", 3, 0), ("T", "h0_3"), ("MM", 1)]
+                ("P", 0, 0), ("P", 1, 0), ("T", "h0_2"), ("T", "h0_3"), ("P", 2, 0), ("P", 3, 0), ("MM", 1)]
         q_pe += [("P", j, pc) for pc in (1, 2) for j in unit3_first] + [("T", "h1_%d" % c) for c in range(4)]
         q_pe += PE_TAIL + [("WARM", NU - 2), ("WARM", NU - 1)]
 
@@ -432,8 +432,8 @@ def tile_transformerencoderblock_pa_kernel(tc, h_attn, x, masks, Wo, bo, out_0, 
         for i in GPSIMD_ADDS:
             q_g += [("Y", i, 0), ("Y", i, 1)] + [("D", d, half) for d, half in GPSIMD_HALVES.get(i, ())]
 
-        q_v = [("C", "w0"), ("QW", 0), ("BO",), ("Q", 0, 0), ("C", "w1"), ("QW", 1)] + [("U", j, 0) for j in range(NJ)]
-        q_v += [("Q", 0, 1), ("Q", 0, 2)] + [("U", j, pc) for pc in (1, 2) for j in unit3_first]
+        q_v = [("C", "w0"), ("QW", 0), ("BO",), ("Q", 0, 0), ("C", "w1"), ("U", 0, 0), ("QW", 1), ("U", 1, 0), ("Q", 0, 1), ("U", 2, 0), ("U", 3, 0)]
+        q_v += [("Q", 0, 2)] + [("U", j, pc) for pc in (1, 2) for j in unit3_first]
         am = 0
         for two_port, reads, reduces in V_BLOCKS:
             q_v += list(two_port)
@@ -496,7 +496,5 @@ def tile_transformerencoderblock_pa_kernel(tc, h_attn, x, masks, Wo, bo, out_0, 
         one_scale()
         for i in range(NU):
             cast(i)
-            if i in (3, 7):
-                store_1(i // NJ, 0, NJ)
-            if i in (9, 11):
+            if i % 2 == 1:
                 store_1(i // NJ, i % NJ - 1, 2)

@@ -84,8 +84,8 @@ def tile_transformerencoderblock_pa_kernel(tc, h_attn, x, masks, Wo, bo, out_0, 
         ssq = keep.tile([P, NU], F32, name="ssq")
         rstd = keep.tile([P, NU], F32, name="rstd")
         nbias = keep.tile([P, NU], F32, name="nbias")
-        o0 = [keep.tile([P, T + (NU if i == NU - 1 else 0)], F32, name="o0_%d" % i) for i in range(NU)]
-        row_max = keep.tile([P, 1], F32, name="row_max")
+        o0 = [keep.tile([P, T + (NU - 1 if i == NU - 1 else 0)], F32, name="o0_%d" % i) for i in range(NU)]
+        row_max = keep.tile([P, 2], F32, name="row_max")
         inv_scale = keep.tile([P, 1], F32, name="inv_scale")
 
         def rows_of(dram, i):
@@ -288,17 +288,23 @@ def tile_transformerencoderblock_pa_kernel(tc, h_attn, x, masks, Wo, bo, out_0, 
                 apply_absolute_value=True,
             )
 
+        def first_half_amax():
+            nc.vector.tensor_reduce(
+                out=row_max[:, 0:1], in_=o0[NU - 1][:, 0:HALF], axis=AX.X, op=ALU.max, apply_absolute_value=True
+            )
+
         def last_amax():
             nc.vector.tensor_reduce(
-                out=row_max[:], in_=o0[NU - 1][:, HALF : T + NU], axis=AX.X, op=ALU.max, apply_absolute_value=True
+                out=row_max[:, 1:2], in_=o0[NU - 1][:, HALF : T + NU - 1], axis=AX.X, op=ALU.max, apply_absolute_value=True
             )
 
 
         def one_scale():
-            across = ps_t.tile([P, P], F32, tag="tp", name="across")
-            nc.tensor.transpose(across[:], row_max[:, 0:1].to_broadcast([P, P]), ident[:])
+            across = ps_t.tile([P, 2 * P], F32, tag="tp", name="across")
+            for c in range(2):
+                nc.tensor.transpose(across[:, c * P : (c + 1) * P], row_max[:, c : c + 1].to_broadcast([P, P]), ident[:])
             scale = keep.tile([P, 1], F32, name="scale")
-            unused = keep.tile([P, P], F32, name="across_scaled")
+            unused = keep.tile([P, 2 * P], F32, name="across_scaled")
             nc.vector.tensor_scalar(
                 out=unused[:], in0=across[:], scalar1=1.0 / 448.0, scalar2=None, op0=ALU.mult, op1=ALU.max, accum_out=scale[:]
             )
@@ -402,8 +408,8 @@ def tile_transformerencoderblock_pa_kernel(tc, h_attn, x, masks, Wo, bo, out_0, 
             op(("SX", i), sum_fold, (i,), [("FX", i)])
         for i in SX_SCALAR:
             op(("SX", i), sum_x_scalar, (i,), ())
-        op(("AM", NU - 1), row_amax, (NU - 1, 0, HALF, NU - 1), [("D", NU - 1, 0)])
-        op(("AM", NU), last_amax, (), [("D", NU - 1, 1)] + [("AM", i) for i in range(NU)])
+        op(("AM", NU - 1), first_half_amax, (), [("D", NU - 1, 0)])
+        op(("AM", NU), last_amax, (), [("D", NU - 1, 1)] + [("AM", i) for i in range(NU - 1)])
 
         PE_TAIL = [("P", 4, 0), ("P", 4, 1), ("T", "h2_0"), ("T", "h2_1"), ("P", 5, 0), ("P", 5, 1), ("T", "h2_2")]
         PE_TAIL += [("P", 6, 0), ("P", 6, 1), ("T", "h2_3"), ("P", 7, 0), ("P", 7, 1), ("P", 8, 0), ("P", 8, 1), ("P", 9, 0), ("P", 9, 1), ("FX", 9)]

from contextlib import ExitStack

import concourse.mybir as mybir
from concourse.masks import make_identity

F32 = mybir.dt.float32
BF16 = mybir.dt.bfloat16
U32 = mybir.dt.uint32
U8 = mybir.dt.uint8
FP8X4 = mybir.dt.float8_e4m3fn_x4
FP8 = mybir.dt.float8_e4m3fn
ALU = mybir.AluOpType
ACT = mybir.ActivationFunctionType
AX = mybir.AxisListType

NSEQ, T, C, E = 3, 1024, 512, 512
P = 128
NJ = E // P
NU = NSEQ * NJ
HALF = 512
CHUNK = 256
EPS = 1e-5
FLOPS = 2 * NSEQ * T * C * E

PIECES = (((0, 256), (256, 256), (512, 512)), ((0, 512), (512, 512)), ((0, 512), (512, 512)))
GPSIMD_ADDS = (3, 5, 7, 9, 11)
GPSIMD_HALVES = {5: ((2, 0), (2, 1)), 7: ((4, 0), (4, 1)), 9: ((6, 0), (6, 1)), 11: ((9, 1), (10, 1), (11, 1))}
HALVES_ON_GPSIMD = tuple(part for parts in GPSIMD_HALVES.values() for part in parts)
FOLDED = (9, 11)
SX_SCALAR = (3, 5, 7)
AMAX_BEHIND = 4
U_BUFS, Y_BUFS, HG_BUFS, BANKS = 5, 6, 3, 4


def tile_transformerencoderblock_pa_kernel(tc, h_attn, x, masks, Wo, bo, out_0, out_1):
    nc = tc.nc
    with ExitStack() as ctx:
        keep = ctx.enter_context(tc.tile_pool(name="keep", bufs=1))
        work = ctx.enter_context(tc.tile_pool(name="work", bufs=HG_BUFS))
        upool = ctx.enter_context(tc.tile_pool(name="upool", bufs=U_BUFS))
        ps_t = ctx.enter_context(tc.psum_pool(name="ps_t", bufs=BANKS))
        ps_a = ctx.enter_context(tc.psum_pool(name="ps_a", bufs=BANKS))
        ctx.enter_context(tc.manual_schedule())

        mrow = keep.tile([P, T], BF16, name="mrow")
        mask_0 = keep.tile([P, T], F32, name="mask_0")
        mask_n = {n: keep.tile([P, T], BF16, name="mask_%d" % n) for n in (1, 2)}
        eps_t = keep.tile([P, 1], F32, name="eps_t")
        zero_t = keep.tile([P, 1], F32, name="zero_t")
        warm = keep.tile([P, 1], F32, name="warm")
        ident = keep.tile([P, P], F32, name="ident")
        ident_bf = keep.tile([P, P], BF16, name="ident_bf")
        ones = keep.tile([P, P], BF16, name="ones")
        zeros = keep.tile([P, 256], F32, name="zeros")
        bo_bf = keep.tile([P, NJ], BF16, name="bo_bf")
        bo32 = keep.tile([P, NJ], F32, name="bo32")
        raw = {}
        for b in range(2):
            raw["w%d" % b] = keep.tile([P, 2, C], BF16, name="w%d" % b)
        for n in range(NSEQ):
            for c in range(T // CHUNK):
                raw["h%d_%d" % (n, c)] = keep.tile([P, 2, C], BF16, name="h%d_%d" % (n, c))
        xs = [keep.tile([P, T], BF16, name="x%d" % i) for i in range(NU)]
        wg = keep.tile([P, 4 * E], BF16, name="wg", align_bytes=64)
        wc = keep.tile([P, E], U32, name="wc", align_bytes=64)
        wsc = keep.tile([P, E], U8, name="wsc", align_bytes=64)
        hg = {}
        hc = {}
        hs = {}
        for n in range(NSEQ):
            for half in range(2):
                hc[(n, half)] = keep.tile([P, HALF], U32, name="hc%d_%d" % (n, half), align_bytes=64)
                hs[(n, half)] = keep.tile([P, HALF], U8, name="hs%d_%d" % (n, half), align_bytes=64)
        turned = {}
        spread = {}
        prod = {}
        folds = {}
        us = {}
        y_buf = [keep.tile([P, T], F32, name="y_buf%d" % b) for b in range(Y_BUFS)]
        ys = [y_buf[i % Y_BUFS] for i in range(NU)]
        sums = keep.tile([P, NU, 4], F32, name="sums")
        scaled = keep.tile([P, NU, 4], F32, name="scaled")
        negmean = keep.tile([P, NU], F32, name="negmean")
        ssq = keep.tile([P, NU], F32, name="ssq")
        rstd = keep.tile([P, NU], F32, name="rstd")
        nbias = keep.tile([P, NU], F32, name="nbias")
        o0 = [keep.tile([P, T + (NU - 1 if i == NU - 1 else 0)], F32, name="o0_%d" % i) for i in range(NU)]
        row_max = keep.tile([P, 2], F32, name="row_max")
        inv_scale = keep.tile([P, 1], F32, name="inv_scale")

        def rows_of(dram, i):
            n, j = divmod(i, NJ)
            return dram[n].rearrange("(p j) t -> p j t", j=NJ)[:, j, :]


        def load_w(b):
            nc.sync.dma_start(out=raw["w%d" % b][:], in_=Wo.rearrange("(p j) c -> p j c", j=NJ)[:, 2 * b : 2 * b + 2, :])

        def load_h(n, c):
            nc.sync.dma_start(
                out=raw["h%d_%d" % (n, c)][:],
                in_=h_attn[n, c * CHUNK : (c + 1) * CHUNK, :].rearrange("(i p) c -> p i c", p=P),
            )

        def load_x(i):
            nc.sync.dma_start(out=xs[i][:], in_=rows_of(x, i))


        def transposes(key):
            words = raw[key][:].bitcast(F32)
            turned[key] = ps_t.tile([P, 2, 2, P], F32, tag="tp", name="tp_%s" % key)
            for i in range(2):
                for u in range(2):
                    nc.tensor.transpose(turned[key][:, i, u, :], words[:, i, u:256:2], ident[:])

        def copy_out(copy, key, dst, part):
            copy(
                out=dst[:].bitcast(F32)[:, part * 512 : (part + 1) * 512].rearrange("p (i t u) -> p i t u", i=2, u=2),
                in_=turned[key][:].rearrange("p i u t -> p i t u"),
            )

        def copy_out_w(b):
            copy_out(nc.vector.tensor_copy, "w%d" % b, wg, b)

        def copy_out_h(n, c):
            half, part = divmod(c, 2)
            if part == 0:
                hg[(n, half)] = work.tile([P, 4 * HALF], BF16, tag="hg", name="hg%d_%d" % (n, half), align_bytes=64)
            copy_out(nc.scalar.copy, "h%d_%d" % (n, c), hg[(n, half)], part)

        def quantise_w(b):
            nc.vector.quantize_mx(
                out=wc[:, b * 256 : (b + 1) * 256].bitcast(FP8X4),
                scales=wsc[:, b * 256 : (b + 1) * 256],
                in_=wg[:, b * 1024 : (b + 1) * 1024],
            )

        def quantise(n, pc):
            first, frames = PIECES[n][pc]
            half, a = divmod(first, HALF)
            nc.vector.quantize_mx(
                out=hc[(n, half)][:, a : a + frames].bitcast(FP8X4),
                scales=hs[(n, half)][:, a : a + frames],
                in_=hg[(n, half)][:, 4 * a : 4 * (a + frames)],
            )


        def dummy_matmul():
            idle = ps_a.tile([P, HALF], F32, tag="acc", name="idle")
            nc.tensor.matmul(out=idle[:, 0:256], lhsT=zeros[:, 0:P], rhs=zeros[:], start=True, stop=True)

        def late_load(i):
            idle = ps_a.tile([P, HALF], F32, tag="acc", name="late%d" % i)
            nc.tensor.matmul(out=idle[:, 0:256], lhsT=zeros[:, 0:P], rhs=o0[i][:, 0:256], start=True, stop=True)

        def spread_mask(half):
            spread[half] = ps_a.tile([P, HALF], F32, tag="acc", name="spread%d" % half)
            nc.tensor.matmul(
                out=spread[half][:], lhsT=ones[:], rhs=mrow[:, half * HALF : (half + 1) * HALF], start=True, stop=True
            )

        def copy_mask(half):
            nc.scalar.copy(out=mask_0[:, half * HALF : (half + 1) * HALF], in_=spread[half][:])

        def fold_x(i):
            folds[i] = ps_t.tile([P, P], F32, tag="tp", name="fold%d" % i)
            for b in range(T // P):
                nc.tensor.matmul(
                    out=folds[i][:], lhsT=ident_bf[:], rhs=xs[i][:, b * P : (b + 1) * P], start=(b == 0), stop=(b == T // P - 1)
                )


        def widen_bo():
            nc.vector.tensor_copy(out=bo32[:], in_=bo_bf[:])

        def project(i, pc):
            n, j = divmod(i, NJ)
            first, frames = PIECES[n][pc]
            half, a = divmod(first, HALF)
            prod[(i, pc)] = ps_a.tile([P, HALF], F32, tag="acc", name="prod%d_%d" % (i, pc))
            nc.tensor.matmul_mx(
                out=prod[(i, pc)][:, 0:frames],
                lhsT=wc[:, j * P : (j + 1) * P].bitcast(FP8X4),
                lhsT_scale=wsc[:, j * P : (j + 1) * P],
                rhs=hc[(n, half)][:, a : a + frames].bitcast(FP8X4),
                rhs_scale=hs[(n, half)][:, a : a + frames],
                start=True,
                stop=True,
            )

        def bias_mask(i, pc):
            n, j = divmod(i, NJ)
            first, frames = PIECES[n][pc]
            if pc == 0:
                us[i] = upool.tile([P, T], F32, tag="u", name="u%d" % i)
            mask = mask_0 if n == 0 else mask_n[n]
            nc.vector.scalar_tensor_tensor(
                out=us[i][:, first : first + frames],
                in0=prod[(i, pc)][:, 0:frames],
                scalar=bo32[:, j : j + 1],
                in1=mask[:, first : first + frames],
                op0=ALU.add,
                op1=ALU.mult,
                accum_out=(sums[:, i, pc : pc + 1] if i in GPSIMD_ADDS else None),
            )

        def add_on_gpsimd(i, half):
            cols = slice(half * HALF, (half + 1) * HALF)
            nc.gpsimd.tensor_tensor(out=ys[i][:, cols], in0=us[i][:, cols], in1=xs[i][:, cols], op=ALU.add)

        def add_on_vector(i):
            nc.vector.scalar_tensor_tensor(
                out=ys[i][:], in0=us[i][:], scalar=1.0, in1=xs[i][:], op0=ALU.mult, op1=ALU.add,
                accum_out=sums[:, i, 0:1],
            )

        def sum_x_column(i):
            pieces = len(PIECES[i // NJ])
            return sums[:, i, pieces : pieces + 1]

        def sum_x_scalar(i):
            unused = work.tile([P, T], BF16, tag="sx_s", name="sx%d" % i)
            nc.scalar.activation(out=unused[:], in_=xs[i][:], func=ACT.Copy, accum_out=sum_x_column(i))

        def sum_x_vector(i):
            unused = work.tile([P, T], BF16, tag="sx_v", name="sx%d" % i)
            nc.vector.tensor_scalar(
                out=unused[:], in0=xs[i][:], scalar1=1.0, scalar2=None, op0=ALU.mult, op1=ALU.add,
                accum_out=sum_x_column(i),
            )

        def sum_fold(i):
            unused = work.tile([P, P], F32, tag="sx_f", name="sx%d" % i)
            nc.scalar.activation(out=unused[:], in_=folds[i][:], func=ACT.Copy, accum_out=sum_x_column(i))

        def neg_mean(i):
            if i in GPSIMD_ADDS:
                parts = len(PIECES[i // NJ]) + 1
                nc.scalar.activation(
                    out=scaled[:, i, 0:parts], in_=sums[:, i, 0:parts], func=ACT.Copy, scale=-1.0 / T,
                    accum_out=negmean[:, i : i + 1],
                )
            else:
                nc.scalar.activation(out=negmean[:, i : i + 1], in_=sums[:, i, 0:1], func=ACT.Copy, scale=-1.0 / T)

        def squares(i):
            col = slice(i, i + 1)
            unused = work.tile([P, T], BF16, tag="sq", name="sq%d" % i)
            if i in GPSIMD_ADDS:
                nc.scalar.activation(
                    out=unused[:], in_=ys[i][:], func=ACT.Square, bias=negmean[:, col], scale=1.0, accum_out=ssq[:, col]
                )
            else:
                nc.scalar.activation(
                    out=unused[:], in_=ys[i][:], func=ACT.Square, bias=sums[:, i, 0:1], scale=-1.0 * T, accum_out=ssq[:, col]
                )

        def inv_std(i):
            col = slice(i, i + 1)
            nc.scalar.activation(
                out=rstd[:, col], in_=ssq[:, col], func=ACT.Abs_reciprocal_sqrt, bias=eps_t[:, 0:1],
                scale=(1.0 / T if i in GPSIMD_ADDS else 1.0 / (T * T * T)),
            )

        def neg_bias(i):
            col = slice(i, i + 1)
            nc.scalar.activation(out=nbias[:, col], in_=negmean[:, col], func=ACT.Copy, scale=rstd[:, col])

        def normalise(i, half):
            col = slice(i, i + 1)
            cols = slice(half * HALF, (half + 1) * HALF)
            if (i, half) in HALVES_ON_GPSIMD:
                nc.gpsimd.tensor_scalar(
                    out=o0[i][:, cols], in0=ys[i][:, cols], scalar1=rstd[:, col], scalar2=nbias[:, col],
                    op0=ALU.mult, op1=ALU.add,
                )
            else:
                nc.scalar.activation(
                    out=o0[i][:, cols], in_=ys[i][:, cols], func=ACT.Identity, bias=nbias[:, col], scale=rstd[:, col]
                )

        def store_0(i):
            nc.sync.dma_start(out=rows_of(out_0, i), in_=o0[i][:, 0:T])

        def row_amax(i, first, last, slot):
            nc.vector.tensor_reduce(
                out=o0[NU - 1][:, T + slot : T + slot + 1], in_=o0[i][:, first:last], axis=AX.X, op=ALU.max,
                apply_absolute_value=True,
            )

        def first_half_amax():
            nc.vector.tensor_reduce(
                out=row_max[:, 0:1], in_=o0[NU - 1][:, 0:HALF], axis=AX.X, op=ALU.max, apply_absolute_value=True
            )

        def last_amax():
            nc.vector.tensor_reduce(
                out=row_max[:, 1:2], in_=o0[NU - 1][:, HALF : T + NU - 1], axis=AX.X, op=ALU.max, apply_absolute_value=True
            )


        def one_scale():
            across = ps_t.tile([P, 2 * P], F32, tag="tp", name="across")
            for c in range(2):
                nc.tensor.transpose(across[:, c * P : (c + 1) * P], row_max[:, c : c + 1].to_broadcast([P, P]), ident[:])
            scale = keep.tile([P, 1], F32, name="scale")
            unused = keep.tile([P, 2 * P], F32, name="across_scaled")
            nc.vector.tensor_scalar(
                out=unused[:], in0=across[:], scalar1=1.0 / 448.0, scalar2=None, op0=ALU.mult, op1=ALU.max, accum_out=scale[:]
            )
            nc.vector.reciprocal(out=inv_scale[:], in_=scale[:])

        f8 = [keep.tile([P, NJ, T], FP8, name="f8_%d" % n) for n in range(NSEQ)]

        def cast(i):
            n, j = divmod(i, NJ)
            if i % 3 == 2:
                nc.scalar.activation(
                    out=f8[n][:, j, :], in_=o0[i][:, 0:T], func=ACT.Identity, scale=inv_scale[:, 0:1], bias=zero_t[:, 0:1],
                    saturate=False,
                )
            else:
                nc.vector.tensor_scalar(
                    out=f8[n][:, j, :], in0=o0[i][:, 0:T], scalar1=inv_scale[:, 0:1], scalar2=None, op0=ALU.mult, saturate=False
                )

        def store_1(n, first, units):
            nc.sync.dma_start(
                out=out_1[n].rearrange("(p j) t -> p j t", j=NJ)[:, first : first + units, :],
                in_=f8[n][:, first : first + units, :].bitcast(U8),
            )


        nc.vector.memset(zeros[:], 0.0)
        nc.vector.memset(eps_t[:], EPS)
        nc.vector.memset(mrow[:], 0.0)
        nc.vector.memset(zero_t[:], 0.0)
        nc.scalar.activation(out=warm[:], in_=eps_t[:], func=ACT.Abs_reciprocal_sqrt)
        make_identity(nc, ident[:])
        make_identity(nc, ident_bf[:])
        nc.gpsimd.memset(ones[:], 1.0)
        load_w(0)
        load_h(0, 0)
        nc.sync.dma_start(out=mrow[0:1, :], in_=masks[0])
        nc.sync.dma_start(out=bo_bf[:], in_=bo.rearrange("(p j) -> p j", j=NJ))
        load_w(1)
        for c in range(1, T // CHUNK):
            load_h(0, c)
        for n in range(NSEQ):
            if n > 0:
                for c in range(T // CHUNK):
                    load_h(n, c)
            for i in {0: (0, 1, 2, 3, 5, 7), 1: (4, 6), 2: (8, 9, 10, 11)}[n]:
                load_x(i)
            if n > 0:
                nc.sync.dma_start(out=mask_n[n][:], in_=masks[n, 0].partition_broadcast(P))


        ops = {}

        def op(name, fn, args, needs):
            ops[name] = (fn, args, list(needs))

        op(("BO",), widen_bo, (), ())
        for w in range(2):
            op(("DUMMY", w), dummy_matmul, (), ())
        for i in (NU - 2, NU - 1):
            op(("WARM", i), late_load, (i,), [("D", i, 0)])
        for b in range(2):
            op(("T", "w%d" % b), transposes, ("w%d" % b,), ())
            op(("C", "w%d" % b), copy_out_w, (b,), [("T", "w%d" % b)])
            op(("QW", b), quantise_w, (b,), [("C", "w%d" % b)])
        for half in range(2):
            op(("MM", half), spread_mask, (half,), ())
            op(("CM", half), copy_mask, (half,), [("MM", half)])
        for n in range(NSEQ):
            for c in range(T // CHUNK):
                key = "h%d_%d" % (n, c)
                op(("T", key), transposes, (key,), ())
                op(("C", key), copy_out_h, (n, c), [("T", key)] + ([("C", "h%d_%d" % (n, c - 1))] if c % 2 else []))
            for pc in range(len(PIECES[n])):
                first, frames = PIECES[n][pc]
                op(("Q", n, pc), quantise, (n, pc), [("C", "h%d_%d" % (n, c)) for c in range(first // CHUNK, (first + frames) // CHUNK)])
        for i in range(NU):
            n, j = divmod(i, NJ)
            pieces = range(len(PIECES[n]))
            for pc in pieces:
                op(("P", i, pc), project, (i, pc), [("Q", n, pc), ("QW", j // 2)])
                op(("U", i, pc), bias_mask, (i, pc), [("P", i, pc), ("BO",)] + ([("CM", PIECES[n][pc][0] // HALF)] if n == 0 else []))
            if i in GPSIMD_ADDS:
                for half in range(2):
                    op(("Y", i, half), add_on_gpsimd, (i, half), [("U", i, pc) for pc in pieces if PIECES[n][pc][0] // HALF == half])
                op(("NM", i), neg_mean, (i,), [("U", i, pc) for pc in pieces] + [("SX", i)])
                op(("SQ", i), squares, (i,), [("Y", i, 0), ("Y", i, 1), ("NM", i)])
            else:
                op(("Y", i), add_on_vector, (i,), [("U", i, pc) for pc in pieces])
                op(("NM", i), neg_mean, (i,), [("Y", i)])
                op(("SQ", i), squares, (i,), [("Y", i)])
            op(("IS", i), inv_std, (i,), [("SQ", i)])
            op(("NB", i), neg_bias, (i,), [("IS", i), ("NM", i)])
            for half in range(2):
                op(("D", i, half), normalise, (i, half), [("NB", i)])
            op(("ST", i), store_0, (i,), [("D", i, 0), ("D", i, 1)])
            if i < NU - 1:
                op(("AM", i), row_amax, (i, 0, T, i), [("D", i, 0), ("D", i, 1)])
        for i in FOLDED:
            op(("FX", i), fold_x, (i,), ())
            op(("SX", i), sum_fold, (i,), [("FX", i)])
        for i in SX_SCALAR:
            op(("SX", i), sum_x_scalar, (i,), ())
        op(("AM", NU - 1), first_half_amax, (), [("D", NU - 1, 0)])
        op(("AM", NU), last_amax, (), [("D", NU - 1, 1)] + [("AM", i) for i in range(NU - 1)])

        PE_TAIL = [("P", 4, 0), ("P", 4, 1), ("T", "h2_0"), ("T", "h2_1"), ("P", 5, 0), ("P", 5, 1), ("T", "h2_2")]
        PE_TAIL += [("P", 6, 0), ("P", 6, 1), ("T", "h2_3"), ("P", 7, 0), ("P", 7, 1), ("P", 8, 0), ("P", 8, 1), ("P", 9, 0), ("P", 9, 1), ("FX", 9)]
        PE_TAIL += [("P", 10, 0), ("P", 10, 1), ("P", 11, 0), ("P", 11, 1), ("FX", 11)]
        V_BLOCKS = [
            ([("Y", 0), ("Q", 1, 0), ("Y", 1), ("Q", 1, 1), ("Y", 2)], (4,), 0),
            ([("Y", 4)], (5,), 1), ([], (6,), 1),
            ([("Y", 6), ("Q", 2, 0), ("Q", 2, 1)], (7,), 1), ([], (8,), 1),
            ([("Y", 8)], (9,), 1), ([], (10,), 1),
            ([("Y", 10)], (11,), 7),
        ]
        S_HEAD = [("SX", 3), ("SX", 5), ("SX", 7)] + [("C", "h1_%d" % c) for c in range(4)]
        S_EXTRA = {2: [("C", "h2_0"), ("C", "h2_1")], 3: [("C", "h2_2"), ("C", "h2_3")], 7: [("SX", 9)], 9: [("SX", 11)]}

        def adds_of(i):
            return [] if i in GPSIMD_ADDS else [("Y", i)]

        unit3_first = (3, 0, 1, 2)

        q_pe = [("DUMMY", 0), ("DUMMY", 1), ("T", "w0"), ("T", "h0_0"), ("MM", 0), ("T", "w1"), ("T", "h0_1"),
                ("P", 0, 0), ("P", 1, 0), ("T", "h0_2"), ("T", "h0_3"), ("P", 2, 0), ("P", 3, 0), ("MM", 1)]
        q_pe += [("P", j, pc) for pc in (1, 2) for j in unit3_first] + [("T", "h1_%d" % c) for c in range(4)]
        q_pe += PE_TAIL + [("WARM", NU - 2), ("WARM", NU - 1)]

        q_g = []
        for i in GPSIMD_ADDS:
            q_g += [("Y", i, 0), ("Y", i, 1)] + [("D", d, half) for d, half in GPSIMD_HALVES.get(i, ())]

        q_v = [("C", "w0"), ("QW", 0), ("BO",), ("Q", 0, 0), ("C", "w1"), ("U", 0, 0), ("QW", 1), ("U", 1, 0), ("Q", 0, 1), ("U", 2, 0), ("U", 3, 0)]
        q_v += [("Q", 0, 2)] + [("U", j, pc) for pc in (1, 2) for j in unit3_first]
        am = 0
        for two_port, reads, reduces in V_BLOCKS:
            q_v += list(two_port)
            for i in reads:
                q_v += [("U", i, 0), ("U", i, 1)]
            q_v += [("AM", am + r) for r in range(reduces)]
            am += reduces
        assert am == NU + 1

        q_s = [("C", "h0_0"), ("CM", 0), ("C", "h0_1"), ("C", "h0_2"), ("C", "h0_3"), ("CM", 1)] + S_HEAD
        for k in range(NU + 1):
            between = [("D", k - 1, half) for half in range(2) if k > 0 and (k - 1, half) not in HALVES_ON_GPSIMD]
            between[1:1] = S_EXTRA.get(k, [])
            if k + 1 in GPSIMD_ADDS:
                between += [("NM", k + 1)]
            if k < NU:
                q_s += ([] if k in GPSIMD_ADDS else [("NM", k)]) + [("SQ", k)] + between[0:1] + [("IS", k)] + between[1:] + [("NB", k)]
            else:
                q_s += between

        q_sp = [("ST", i) for i in range(NU)]


        def rotate(makers, readers_of, bufs):
            for m in range(bufs, len(makers)):
                ops[makers[m]][2].extend(readers_of(makers[m - bufs]))

        def psum_readers(name):
            return {"T": [("C", name[1])], "MM": [("CM", name[1])], "FX": [("SX", name[1])], "DUMMY": [], "WARM": []}.get(
                name[0], [("U",) + name[1:]]
            )

        def y_makers(i):
            return [("Y", i, 0), ("Y", i, 1)] if i in GPSIMD_ADDS else [("Y", i)]

        rotate([name for name in q_pe if name[0] in ("DUMMY", "MM", "P", "WARM")], psum_readers, BANKS)
        rotate([name for name in q_pe if name[0] in ("T", "FX")], psum_readers, BANKS)
        rotate([("U", i, 0) for i in range(NU)], lambda name: y_makers(name[1]), U_BUFS)
        rotate([y_makers(i)[0] for i in range(NU)], lambda name: [("SQ", name[1]), ("D", name[1], 0), ("D", name[1], 1)], Y_BUFS)
        rotate([("C", "h%d_%d" % (n, c)) for n in range(NSEQ) for c in (0, 2)],
               lambda name: [("Q", int(name[1][1]), pc) for pc in range(len(PIECES[int(name[1][1])]))], HG_BUFS)


        queues = [q_pe, q_v, q_g, q_s, q_sp]
        heads = [0, 0, 0, 0, 0]
        written = set()
        left = sum(len(q) for q in queues)
        while left > 0:
            before = left
            for k in range(len(queues)):
                q = queues[k]
                while heads[k] < len(q) and all(name in written for name in ops[q[heads[k]]][2]):
                    fn, args, needs = ops[q[heads[k]]]
                    fn(*args)
                    written.add(q[heads[k]])
                    heads[k] += 1
                    left -= 1
            assert left < before

        one_scale()
        for i in range(NU):
            cast(i)
            if i % 2 == 1:
                store_1(i // NJ, i % NJ - 1, 2)
